import numpy as np
import ml_dtypes


def mxq(x, axis, fmt="e4m3"):
    dtype, down = {"e4m3": (ml_dtypes.float8_e4m3fn, 7), "e5m2": (ml_dtypes.float8_e5m2, 14)}[fmt]
    v = np.moveaxis(np.asarray(x, np.float32).astype(ml_dtypes.bfloat16).astype(np.float64), axis, -1)
    blocks = v.reshape(v.shape[:-1] + (-1, 32))
    amax = np.abs(blocks).max(-1, keepdims=True)
    byte = np.maximum(np.where(amax > 0, np.frexp(amax)[1] - 1 + 127, 0) - down, 1)
    scale = np.exp2(byte - 127.0)
    codes = (blocks / scale).astype(np.float32).astype(dtype).astype(np.float64)
    return np.moveaxis((codes * scale).reshape(v.shape), -1, axis)


WIDE = False


def mx_kscale(k):
    if not WIDE:
        return np.ones(k)
    levels = np.array([10, -10, 5, -5, 0])
    a = np.random.permutation(np.resize(levels, k // 512 * 4)).reshape(k // 512, 4)
    idx = np.arange(k)
    return np.exp2(a[idx // 512, idx % 128 // 32])


BF16 = ml_dtypes.bfloat16


def bf(x):
    return np.asarray(x, np.float32).astype(BF16)


def f64(x):
    return np.asarray(x).astype(np.float64)


B, S, D, DI = 4, 2048, 512, 512
EPS = 1e-12


def l2norm(v):
    n = np.sqrt(np.sum(v * v, axis=-1, keepdims=True))
    return v / np.maximum(n, EPS)


def setup_inputs():
    s = mx_kscale(D)
    return {"x": bf(np.random.standard_normal((B, S, D)) * s),
            "wk": bf(np.random.standard_normal((D, DI)) / np.sqrt(D) / s[:, None]),
            "wv": bf(np.random.standard_normal((D, DI)) / np.sqrt(D) / s[:, None])}


def reference(x, wk, wv):
    xq = mxq(f64(x), 2, "e4m3")
    k = l2norm(xq @ mxq(f64(wk), 0, "e4m3"))
    v = xq @ mxq(f64(wv), 0, "e4m3")
    return np.sum(k * v, axis=-2, keepdims=True)

@@ -1,0 +1,319 @@
+from contextlib import ExitStack
+
+import concourse.mybir as mybir
+from concourse.masks import make_identity
+
+F32 = mybir.dt.float32
+BF16 = mybir.dt.bfloat16
+U32 = mybir.dt.uint32
+U8 = mybir.dt.uint8
+FP8X4 = mybir.dt.float8_e4m3fn_x4
+ACT = mybir.ActivationFunctionType
+ALU = mybir.AluOpType
+
+P = 128
+PACK = 4
+BATCH, TOKENS, D, DI = 4, 2048, 512, 512
+EPS = 1e-12
+WORDS = D // 2
+HALVES = WORDS // P
+PAIR = 2
+CHUNK_TILES = 4
+CHUNKS_PER_BATCH = TOKENS // (CHUNK_TILES * P)
+PAIRS_PER_CHUNK = CHUNK_TILES // PAIR
+PAIRS_PER_BATCH = CHUNKS_PER_BATCH * PAIRS_PER_CHUNK
+N_PAIRS = BATCH * PAIRS_PER_BATCH
+W_SPLIT = 320
+E_BLOCKS = DI // P
+
+FLOPS = 2 * 2 * BATCH * TOKENS * D * DI
+
+
+def tile_hydraencoderlayer_pa_t_kernel(tc, x, wk, wv, out):
+    nc = tc.nc
+    with ExitStack() as ctx:
+        ctx.enter_context(tc.manual_schedule())
+        consts = ctx.enter_context(tc.tile_pool(name="consts", bufs=1))
+        x_pool = ctx.enter_context(tc.tile_pool(name="x_pool", bufs=BATCH * CHUNKS_PER_BATCH))
+        stage = ctx.enter_context(tc.tile_pool(name="stage", bufs=2))
+        operands = ctx.enter_context(tc.tile_pool(name="operands", bufs=4))
+        work = ctx.enter_context(tc.tile_pool(name="work", bufs=6))
+        psum_t = ctx.enter_context(tc.psum_pool(name="psum_t", bufs=1))
+        psum_a = ctx.enter_context(tc.psum_pool(name="psum_a", bufs=3))
+        psum_v = ctx.enter_context(tc.psum_pool(name="psum_v", bufs=3))
+        psum_s = ctx.enter_context(tc.psum_pool(name="psum_s", bufs=1))
+
+        w_raw = {}
+
+        def load_weight(label, w):
+            w_raw[label] = consts.tile([P, PACK, DI], BF16, name="%s_raw" % label)
+            nc.sync.dma_start(
+                out=w_raw[label][:].rearrange("q (u e) c -> q u (e c)", u=HALVES),
+                in_=w.rearrange("(u q e) c -> q u (e c)", u=HALVES, e=2),
+            )
+        load_weight("wk", wk)
+        x_chunks = []
+        for b in range(BATCH):
+            chunks = x[b].rearrange("(p c t) k -> c p (t k)", c=CHUNKS_PER_BATCH, t=CHUNK_TILES)
+            for c in range(CHUNKS_PER_BATCH):
+                x_sb = x_pool.tile([P, CHUNK_TILES * D], BF16)
+                x_chunks.append(x_sb)
+                if b == 0 and c == 0:
+                    pair_cols = PAIR * D
+                    nc.sync.dma_start(out=x_sb[:, :pair_cols], in_=chunks[c][:, :pair_cols])
+                    load_weight("wv", wv)
+                    nc.sync.dma_start(out=x_sb[:, pair_cols:], in_=chunks[c][:, pair_cols:])
+                else:
+                    nc.sync.dma_start(out=x_sb[:], in_=chunks[c])
+
+        ident = consts.tile([P, P], F32)
+        make_identity(nc, ident[:])
+        out_cols = consts.tile([P, P], F32)
+        nc.vector.memset(out_cols[:], 0.0)
+        zeros = consts.tile([P, DI], BF16)
+        nc.vector.memset(zeros[:], 0.0)
+        table_load = consts.tile([P, 1], F32)
+        nc.scalar.activation(out=table_load[:], in_=zeros[:, :1], func=ACT.Abs_reciprocal_sqrt, bias=1.0)
+
+        w_grouped = {}
+        w_codes = {}
+        w_scales = {}
+        for label in ("wk", "wv"):
+            w_grouped[label] = consts.tile(
+                [P, DI, PACK], BF16, name="%s_grouped" % label, align_bytes=64
+            )
+            w_codes[label] = consts.tile([P, DI], U32, name="%s_codes" % label, align_bytes=256)
+            w_scales[label] = consts.tile([P, DI], U8, name="%s_scales" % label, align_bytes=256)
+
+        def quantise_weight(label):
+            nc.vector.quantize_mx(
+                out=w_codes[label][:].bitcast(FP8X4),
+                scales=w_scales[label][:],
+                in_=w_grouped[label][:].rearrange("q c t -> q (c t)"),
+            )
+
+        def interleave_weight(label):
+            by_column = w_raw[label][:].rearrange("q t c -> q c t")
+            grouped_w = w_grouped[label]
+            nc.vector.tensor_copy(out=grouped_w[:, :W_SPLIT, :], in_=by_column[:, :W_SPLIT, :])
+            nc.scalar.copy(out=grouped_w[:, W_SPLIT:, :], in_=by_column[:, W_SPLIT:, :])
+
+        def warm_up(count):
+            bank = psum_s.tile([P, DI], F32, name="token_sums")
+            for k in range(count):
+                nc.tensor.matmul(out=bank[:], lhsT=zeros[:, :P], rhs=zeros[:], start=True, stop=True)
+
+        xt, grouped, x_codes, x_scales = {}, {}, {}, {}
+        a_ps, v_ps, a_sb = {}, {}, {}
+        norm2, clamped, rnorm = {}, {}, {}
+        prod, pair_sum, token_sums = {}, {}, {}
+
+        def transpose_tile(bank, n, j):
+            x_words = x_chunks[n // PAIRS_PER_CHUNK][:].bitcast(F32)
+            first_word = ((n % PAIRS_PER_CHUNK) * PAIR + j) * WORDS
+            for u in range(HALVES):
+                w0 = first_word + u * P
+                nc.tensor.transpose(bank[:, j, u, :], x_words[:, w0 : w0 + P], ident[:])
+
+        def new_xt(pool=psum_t, name="xt"):
+            return pool.tile([P, PAIR, HALVES, P], F32, name=name)
+
+        def transpose_x(n, bank):
+            xt[n] = bank
+            for j in range(PAIR):
+                transpose_tile(bank, n, j)
+
+        def regroup_tiles(n, tiles, bank, copy):
+            if n not in grouped:
+                grouped[n] = stage.tile([P, PAIR * P * PACK], BF16, name="grouped", align_bytes=64)
+            words = grouped[n][:].bitcast(F32).rearrange("p (j r u) -> p j r u", j=PAIR, u=HALVES)
+            copy(
+                out=words[:, tiles, :, :],
+                in_=bank[:].rearrange("p j u r -> p j r u")[:, tiles, :, :],
+            )
+
+        def regroup_x(n):
+            regroup_tiles(n, slice(0, PAIR), xt[n], nc.vector.tensor_copy)
+
+        def quantise_tiles(n, tiles):
+            if n not in x_codes:
+                x_codes[n] = operands.tile([P, PAIR * P], U32, name="x_codes", align_bytes=256)
+                x_scales[n] = operands.tile([P, PAIR * P], U8, name="x_scales", align_bytes=256)
+            cols = slice(tiles.start * P, tiles.stop * P)
+            nc.vector.quantize_mx(
+                out=x_codes[n][:, cols].bitcast(FP8X4),
+                scales=x_scales[n][:, cols],
+                in_=grouped[n][:, tiles.start * P * PACK : tiles.stop * P * PACK],
+            )
+
+        def quantise_x(n):
+            quantise_tiles(n, slice(0, PAIR))
+
+        def mx_pass(bank, n, j, label):
+            cols = slice(j * P, (j + 1) * P)
+            nc.tensor.matmul_mx(
+                out=bank[:],
+                lhsT=x_codes[n][:, cols].bitcast(FP8X4),
+                lhsT_scale=x_scales[n][:, cols],
+                rhs=w_codes[label][:].bitcast(FP8X4),
+                rhs_scale=w_scales[label][:],
+                start=True,
+                stop=True,
+            )
+
+        def pass_a(n, j):
+            a_ps[n, j] = psum_a.tile([P, DI], F32, name="a_ps")
+            mx_pass(a_ps[n, j], n, j, "wk")
+
+        def pass_v(n, j):
+            v_ps[n, j] = psum_v.tile([P, DI], F32, name="v_ps")
+            mx_pass(v_ps[n, j], n, j, "wv")
+
+        def square_sum(n, j):
+            if j == 0:
+                norm2[n] = work.tile([P, PAIR], F32, name="norm2")
+            squares = work.tile([P, DI], BF16, name="squares")
+            nc.scalar.activation(
+                out=squares[:], in_=a_ps[n, j][:], func=ACT.Square,
+                accum_out=norm2[n][:, j : j + 1],
+            )
+
+        def copy_a(n, j, copy=nc.scalar.copy):
+            a_sb[n, j] = work.tile([P, DI], F32, name="a_sb")
+            copy(out=a_sb[n, j][:], in_=a_ps[n, j][:])
+
+        def clamp_norm(n):
+            clamped[n] = work.tile([P, PAIR], F32, name="clamped")
+            nc.gpsimd.tensor_scalar_max(out=clamped[n][:], in0=norm2[n][:], scalar1=EPS * EPS)
+
+        def invert_norm(n):
+            rnorm[n] = work.tile([P, PAIR], F32, name="rnorm")
+            nc.scalar.activation(out=rnorm[n][:], in_=clamped[n][:], func=ACT.Abs_reciprocal_sqrt)
+
+        def product(n, j):
+            if j == 0:
+                prod[n] = work.tile([P, PAIR, DI], F32, name="prod")
+            nc.vector.scalar_tensor_tensor(
+                out=prod[n][:, j, :],
+                in0=a_sb[n, j][:],
+                scalar=rnorm[n][:, j : j + 1],
+                in1=v_ps[n, j][:],
+                op0=ALU.mult,
+                op1=ALU.mult,
+            )
+
+        def add_pair(n):
+            if n % 4 != 1:
+                return
+            pair_sum[n] = work.tile([P, DI], F32, name="pair_sum")
+            nc.vector.tensor_tensor(
+                out=pair_sum[n][:], in0=prod[n][:, 0, :], in1=prod[n][:, 1, :], op=ALU.add
+            )
+
+        def add_tokens(n):
+            b, q = divmod(n, PAIRS_PER_BATCH)
+            if q == 0:
+                token_sums[b] = psum_s.tile([P, E_BLOCKS, P], F32, name="token_sums")
+            if n in pair_sum:
+                tiles = [pair_sum[n][:]]
+            else:
+                tiles = [prod[n][:, j, :] for j in range(PAIR)]
+            for k, tile in enumerate(tiles):
+                for i in range(E_BLOCKS):
+                    nc.tensor.matmul(
+                        out=token_sums[b][:, i, :],
+                        lhsT=tile[:, i * P : (i + 1) * P],
+                        rhs=ident[:],
+                        is_transpose=True,
+                        start=(q == 0 and k == 0 and i == 0),
+                        stop=(q == PAIRS_PER_BATCH - 1 and k == len(tiles) - 1 and i == E_BLOCKS - 1),
+                    )
+
+        def add_partitions(b):
+            nc.vector.tensor_reduce(
+                out=out_cols[:, b * E_BLOCKS : (b + 1) * E_BLOCKS],
+                in_=token_sums[b][:],
+                axis=mybir.AxisListType.X,
+                op=ALU.add,
+            )
+
+        def live(n):
+            return 0 <= n < N_PAIRS
+
+        def step(n):
+            if live(n + 1):
+                pass_a(n + 1, 0)
+            if live(n):
+                pass_v(n, 0)
+            if live(n + 3):
+                transpose_x(n + 3, new_xt())
+            if live(n - 2):
+                add_tokens(n - 2)
+            if live(n) and n < N_PAIRS - 1:
+                square_sum(n, 0)
+                if live(n - 1):
+                    invert_norm(n - 1)
+                copy_a(n, 0)
+                square_sum(n, 1)
+                clamp_norm(n)
+                if 0 < n < N_PAIRS - 2:
+                    copy_a(n, 1)
+            elif n == N_PAIRS - 1:
+                square_sum(n, 0)
+                invert_norm(n - 1)
+                square_sum(n, 1)
+                clamp_norm(n)
+                copy_a(n - 1, 1)
+                invert_norm(n)
+                copy_a(n, 0)
+            if live(n + 1):
+                pass_a(n + 1, 1)
+            if n == 0:
+                copy_a(n, 1, copy=nc.vector.tensor_copy)
+            if live(n - 1):
+                product(n - 1, 0)
+            if live(n + 2):
+                quantise_x(n + 2)
+            if n == N_PAIRS - 1:
+                copy_a(n, 1, copy=nc.vector.tensor_copy)
+            if live(n - 1):
+                product(n - 1, 1)
+            if live(n):
+                pass_v(n, 1)
+            if live(n - 2) and (n - 2) % PAIRS_PER_BATCH == PAIRS_PER_BATCH - 1:
+                add_partitions((n - 2) // PAIRS_PER_BATCH)
+            if live(n + 3):
+                regroup_x(n + 3)
+            if live(n - 1):
+                add_pair(n - 1)
+
+        warm_up(6)
+        interleave_weight("wk")
+        quantise_weight("wk")
+        banks = [new_xt(), new_xt(psum_v, "v_ps")]
+        for j in range(PAIR):
+            transpose_tile(banks[j], 0, j)
+        warm_up(2)
+        for j in range(PAIR):
+            regroup_tiles(0, slice(j, j + 1), banks[j], nc.scalar.copy)
+            quantise_tiles(0, slice(j, j + 1))
+        pass_a(0, 0)
+        interleave_weight("wv")
+        transpose_x(1, new_xt(psum_v, "v_ps"))
+        pass_a(0, 1)
+        regroup_x(1)
+        quantise_x(1)
+        quantise_weight("wv")
+        transpose_x(2, new_xt())
+        regroup_x(2)
+        for n in range(N_PAIRS + 2):
+            step(n)
+
+        out_rows_ps = psum_t.tile([P, P], F32, name="xt")
+        nc.tensor.transpose(out_rows_ps[:], out_cols[:], ident[:])
+        out_rows = consts.tile([P, P], F32)
+        nc.vector.tensor_copy(out=out_rows[:], in_=out_rows_ps[:])
+        nc.sync.dma_start(
+            out=out.rearrange("b o (i e) -> (b o i) e", i=E_BLOCKS),
+            in_=out_rows[0 : BATCH * E_BLOCKS, :],
+        )

@@ -26,6 +26,22 @@ N_PAIRS = BATCH * PAIRS_PER_BATCH
 W_SPLIT = 320
 E_BLOCKS = DI // P
 
+LAG = 3
+SUM_LAG = 2
+WV_AFTER = 1
+WV_STEP = 1
+WV_SPLIT = 512
+COPY_HEAD = 3
+GROUP = 2
+SINGLES = 4
+A_BUFS = 10
+POOL_BLOCKS = 4
+POOL_EVERY = 1
+POOL_TAIL = 2
+COPY_EVERY = 3
+COPY_TAIL = 3
+X_BUFS = 8
+
 FLOPS = 2 * 2 * BATCH * TOKENS * D * DI
 
 
@@ -35,8 +51,8 @@ def tile_hydraencoderlayer_pa_t_kernel(tc, x, wk, wv, out):
         ctx.enter_context(tc.manual_schedule())
         consts = ctx.enter_context(tc.tile_pool(name="consts", bufs=1))
         x_pool = ctx.enter_context(tc.tile_pool(name="x_pool", bufs=BATCH * CHUNKS_PER_BATCH))
-        stage = ctx.enter_context(tc.tile_pool(name="stage", bufs=2))
-        operands = ctx.enter_context(tc.tile_pool(name="operands", bufs=4))
+        stage = ctx.enter_context(tc.tile_pool(name="stage", bufs=3))
+        operands = ctx.enter_context(tc.tile_pool(name="operands", bufs=X_BUFS))
         work = ctx.enter_context(tc.tile_pool(name="work", bufs=6))
         psum_t = ctx.enter_context(tc.psum_pool(name="psum_t", bufs=1))
         psum_a = ctx.enter_context(tc.psum_pool(name="psum_a", bufs=3))
@@ -61,10 +77,11 @@ def tile_hydraencoderlayer_pa_t_kernel(tc, x, wk, wv, out):
                 if b == 0 and c == 0:
                     pair_cols = PAIR * D
                     nc.sync.dma_start(out=x_sb[:, :pair_cols], in_=chunks[c][:, :pair_cols])
-                    load_weight("wv", wv)
                     nc.sync.dma_start(out=x_sb[:, pair_cols:], in_=chunks[c][:, pair_cols:])
                 else:
                     nc.sync.dma_start(out=x_sb[:], in_=chunks[c])
+                if b == 0 and c == WV_AFTER:
+                    load_weight("wv", wv)
 
         ident = consts.tile([P, P], F32)
         make_identity(nc, ident[:])
@@ -92,11 +109,12 @@ def tile_hydraencoderlayer_pa_t_kernel(tc, x, wk, wv, out):
                 in_=w_grouped[label][:].rearrange("q c t -> q (c t)"),
             )
 
-        def interleave_weight(label):
+        def interleave_weight(label, split):
             by_column = w_raw[label][:].rearrange("q t c -> q c t")
             grouped_w = w_grouped[label]
-            nc.vector.tensor_copy(out=grouped_w[:, :W_SPLIT, :], in_=by_column[:, :W_SPLIT, :])
-            nc.scalar.copy(out=grouped_w[:, W_SPLIT:, :], in_=by_column[:, W_SPLIT:, :])
+            nc.vector.tensor_copy(out=grouped_w[:, :split, :], in_=by_column[:, :split, :])
+            if split < DI:
+                nc.scalar.copy(out=grouped_w[:, split:, :], in_=by_column[:, split:, :])
 
         def warm_up(count):
             bank = psum_s.tile([P, DI], F32, name="token_sums")
@@ -169,26 +187,44 @@ def tile_hydraencoderlayer_pa_t_kernel(tc, x, wk, wv, out):
             v_ps[n, j] = psum_v.tile([P, DI], F32, name="v_ps")
             mx_pass(v_ps[n, j], n, j, "wv")
 
-        def square_sum(n, j):
-            if j == 0:
-                norm2[n] = work.tile([P, PAIR], F32, name="norm2")
-            squares = work.tile([P, DI], BF16, name="squares")
-            nc.scalar.activation(
-                out=squares[:], in_=a_ps[n, j][:], func=ACT.Square,
-                accum_out=norm2[n][:, j : j + 1],
-            )
-
         def copy_a(n, j, copy=nc.scalar.copy):
-            a_sb[n, j] = work.tile([P, DI], F32, name="a_sb")
+            a_sb[n, j] = work.tile([P, DI], F32, name="a_sb", bufs=A_BUFS)
             copy(out=a_sb[n, j][:], in_=a_ps[n, j][:])
 
+        def group_of(n):
+            if n >= N_PAIRS - SINGLES:
+                return n, 1
+            return n - n % GROUP, GROUP
+
+        def square_sum(n, j, source=a_sb):
+            first, count = group_of(n)
+            if first not in norm2:
+                norm2[first] = work.tile([P, count * PAIR], F32, name="norm2")
+            col = (n - first) * PAIR + j
+            squares = work.tile([P, DI], BF16, name="squares")
+            nc.scalar.activation(
+                out=squares[:], in_=source[n, j][:], func=ACT.Square,
+                accum_out=norm2[first][:, col : col + 1],
+            )
+
+        def closes_group(n):
+            return live(n) and sum(group_of(n)) == n + 1
+
         def clamp_norm(n):
-            clamped[n] = work.tile([P, PAIR], F32, name="clamped")
-            nc.gpsimd.tensor_scalar_max(out=clamped[n][:], in0=norm2[n][:], scalar1=EPS * EPS)
+            first, count = group_of(n)
+            clamped[first] = work.tile([P, count * PAIR], F32, name="clamped")
+            nc.scalar.activation(out=clamped[first][:], in_=norm2[first][:], func=ACT.Relu, bias=-EPS * EPS)
 
         def invert_norm(n):
-            rnorm[n] = work.tile([P, PAIR], F32, name="rnorm")
-            nc.scalar.activation(out=rnorm[n][:], in_=clamped[n][:], func=ACT.Abs_reciprocal_sqrt)
+            first, count = group_of(n)
+            rnorm[first] = work.tile([P, count * PAIR], F32, name="rnorm")
+            nc.scalar.activation(out=rnorm[first][:], in_=clamped[first][:], func=ACT.Abs_reciprocal_sqrt,
+                                 bias=EPS * EPS)
+
+        def rnorm_of(n, j):
+            first, count = group_of(n)
+            col = (n - first) * PAIR + j
+            return rnorm[first][:, col : col + 1]
 
         def product(n, j):
             if j == 0:
@@ -196,38 +232,41 @@ def tile_hydraencoderlayer_pa_t_kernel(tc, x, wk, wv, out):
             nc.vector.scalar_tensor_tensor(
                 out=prod[n][:, j, :],
                 in0=a_sb[n, j][:],
-                scalar=rnorm[n][:, j : j + 1],
+                scalar=rnorm_of(n, j),
                 in1=v_ps[n, j][:],
                 op0=ALU.mult,
                 op1=ALU.mult,
             )
 
         def add_pair(n):
-            if n % 4 != 1:
+            if POOL_BLOCKS == 0 or n >= N_PAIRS - POOL_TAIL or n % POOL_EVERY:
                 return
+            cols = POOL_BLOCKS * P
             pair_sum[n] = work.tile([P, DI], F32, name="pair_sum")
-            nc.vector.tensor_tensor(
-                out=pair_sum[n][:], in0=prod[n][:, 0, :], in1=prod[n][:, 1, :], op=ALU.add
+            nc.gpsimd.tensor_tensor(
+                out=pair_sum[n][:, :cols], in0=prod[n][:, 0, :cols], in1=prod[n][:, 1, :cols], op=ALU.add
             )
 
         def add_tokens(n):
             b, q = divmod(n, PAIRS_PER_BATCH)
             if q == 0:
                 token_sums[b] = psum_s.tile([P, E_BLOCKS, P], F32, name="token_sums")
-            if n in pair_sum:
-                tiles = [pair_sum[n][:]]
-            else:
-                tiles = [prod[n][:, j, :] for j in range(PAIR)]
-            for k, tile in enumerate(tiles):
-                for i in range(E_BLOCKS):
-                    nc.tensor.matmul(
-                        out=token_sums[b][:, i, :],
-                        lhsT=tile[:, i * P : (i + 1) * P],
-                        rhs=ident[:],
-                        is_transpose=True,
-                        start=(q == 0 and k == 0 and i == 0),
-                        stop=(q == PAIRS_PER_BATCH - 1 and k == len(tiles) - 1 and i == E_BLOCKS - 1),
-                    )
+            blocks = []
+            for i in range(E_BLOCKS):
+                cols = slice(i * P, (i + 1) * P)
+                if n in pair_sum and i < POOL_BLOCKS:
+                    blocks.append((i, pair_sum[n][:, cols]))
+                else:
+                    blocks.extend([(i, prod[n][:, j, cols]) for j in range(PAIR)])
+            for k, (i, block) in enumerate(blocks):
+                nc.tensor.matmul(
+                    out=token_sums[b][:, i, :],
+                    lhsT=block,
+                    rhs=ident[:],
+                    is_transpose=True,
+                    start=(q == 0 and k == 0),
+                    stop=(q == PAIRS_PER_BATCH - 1 and k == len(blocks) - 1),
+                )
 
         def add_partitions(b):
             nc.vector.tensor_reduce(
@@ -240,73 +279,84 @@ def tile_hydraencoderlayer_pa_t_kernel(tc, x, wk, wv, out):
         def live(n):
             return 0 <= n < N_PAIRS
 
+        def on_vector(n, j):
+            if n < COPY_HEAD:
+                return j == 1
+            return j == 1 and n % COPY_EVERY == COPY_EVERY - 1 and n < N_PAIRS - COPY_TAIL
+
         def step(n):
-            if live(n + 1):
-                pass_a(n + 1, 0)
-            if live(n):
-                pass_v(n, 0)
-            if live(n + 3):
-                transpose_x(n + 3, new_xt())
-            if live(n - 2):
-                add_tokens(n - 2)
-            if live(n) and n < N_PAIRS - 1:
-                square_sum(n, 0)
-                if live(n - 1):
-                    invert_norm(n - 1)
-                copy_a(n, 0)
-                square_sum(n, 1)
-                clamp_norm(n)
-                if 0 < n < N_PAIRS - 2:
-                    copy_a(n, 1)
-            elif n == N_PAIRS - 1:
-                square_sum(n, 0)
-                invert_norm(n - 1)
-                square_sum(n, 1)
-                clamp_norm(n)
-                copy_a(n - 1, 1)
-                invert_norm(n)
-                copy_a(n, 0)
-            if live(n + 1):
-                pass_a(n + 1, 1)
-            if n == 0:
-                copy_a(n, 1, copy=nc.vector.tensor_copy)
-            if live(n - 1):
-                product(n - 1, 0)
-            if live(n + 2):
-                quantise_x(n + 2)
-            if n == N_PAIRS - 1:
-                copy_a(n, 1, copy=nc.vector.tensor_copy)
-            if live(n - 1):
-                product(n - 1, 1)
-            if live(n):
-                pass_v(n, 1)
-            if live(n - 2) and (n - 2) % PAIRS_PER_BATCH == PAIRS_PER_BATCH - 1:
-                add_partitions((n - 2) // PAIRS_PER_BATCH)
+            m = n - LAG
+            s = m - SUM_LAG
+            if live(n) and on_vector(n, 0):
+                copy_a(n, 0, copy=nc.vector.tensor_copy)
             if live(n + 3):
                 regroup_x(n + 3)
+            if live(s - 1) and (s - 1) % PAIRS_PER_BATCH == PAIRS_PER_BATCH - 1:
+                add_partitions((s - 1) // PAIRS_PER_BATCH)
+            if live(n) and n > 0:
+                pass_a(n, 1)
+            if live(m):
+                pass_v(m, 1)
+            if live(n + 1):
+                pass_a(n + 1, 0)
+            if live(n) and not on_vector(n, 0):
+                copy_a(n, 0)
+            if closes_group(n - 2):
+                invert_norm(n - 2)
             if live(n - 1):
-                add_pair(n - 1)
+                square_sum(n - 1, 1)
+            if live(n) and not on_vector(n, 1):
+                copy_a(n, 1)
+            if live(n):
+                square_sum(n, 0)
+            if closes_group(n - 1):
+                clamp_norm(n - 1)
+            if live(m):
+                product(m, 0)
+            if live(n) and on_vector(n, 1):
+                copy_a(n, 1, copy=nc.vector.tensor_copy)
+            if n == WV_STEP:
+                quantise_weight("wv")
+            if live(m + 1):
+                pass_v(m + 1, 0)
+            if live(n + 4):
+                transpose_x(n + 4, new_xt())
+            if live(s):
+                add_tokens(s)
+            if live(m):
+                product(m, 1)
+                add_pair(m)
+            if live(n + 3):
+                quantise_x(n + 3)
 
         warm_up(6)
-        interleave_weight("wk")
+        interleave_weight("wk", W_SPLIT)
         quantise_weight("wk")
         banks = [new_xt(), new_xt(psum_v, "v_ps")]
         for j in range(PAIR):
             transpose_tile(banks[j], 0, j)
-        warm_up(2)
+        transpose_x(1, new_xt(psum_v, "v_ps"))
+        warm_up(1)
         for j in range(PAIR):
             regroup_tiles(0, slice(j, j + 1), banks[j], nc.scalar.copy)
             quantise_tiles(0, slice(j, j + 1))
+        regroup_tiles(1, slice(0, PAIR), xt[1], nc.scalar.copy)
         pass_a(0, 0)
-        interleave_weight("wv")
-        transpose_x(1, new_xt(psum_v, "v_ps"))
         pass_a(0, 1)
-        regroup_x(1)
         quantise_x(1)
-        quantise_weight("wv")
-        transpose_x(2, new_xt())
-        regroup_x(2)
-        for n in range(N_PAIRS + 2):
+        transpose_x(2, new_xt(psum_v, "v_ps"))
+        transpose_x(3, new_xt())
+        pass_a(1, 0)
+        copy_a(0, 0)
+        copy_a(0, 1, copy=nc.vector.tensor_copy)
+        regroup_tiles(2, slice(0, PAIR), xt[2], nc.scalar.copy)
+        regroup_x(3)
+        transpose_x(4, new_xt())
+        square_sum(0, 0)
+        quantise_x(2)
+        interleave_weight("wv", WV_SPLIT)
+        quantise_x(3)
+        for n in range(1, N_PAIRS + LAG + SUM_LAG + 1):
             step(n)
 
         out_rows_ps = psum_t.tile([P, P], F32, name="xt")

@@ -38,7 +38,7 @@ A_BUFS = 10
 POOL_BLOCKS = 4
 POOL_EVERY = 1
 POOL_TAIL = 2
-COPY_EVERY = 3
+COPY_EVERY = 6
 COPY_TAIL = 3
 X_BUFS = 8
 

@@ -23,6 +23,7 @@ CHUNKS_PER_BATCH = TOKENS // (CHUNK_TILES * P)
 PAIRS_PER_CHUNK = CHUNK_TILES // PAIR
 PAIRS_PER_BATCH = CHUNKS_PER_BATCH * PAIRS_PER_CHUNK
 N_PAIRS = BATCH * PAIRS_PER_BATCH
+N_CHUNKS = BATCH * CHUNKS_PER_BATCH
 W_SPLIT = 320
 E_BLOCKS = DI // P
 
@@ -38,7 +39,7 @@ A_BUFS = 10
 POOL_BLOCKS = 4
 POOL_EVERY = 1
 POOL_TAIL = 2
-COPY_EVERY = 6
+COPY_EVERY = 4
 COPY_TAIL = 3
 X_BUFS = 8
 
@@ -69,19 +70,18 @@ def tile_hydraencoderlayer_pa_t_kernel(tc, x, wk, wv, out):
             )
         load_weight("wk", wk)
         x_chunks = []
-        for b in range(BATCH):
-            chunks = x[b].rearrange("(p c t) k -> c p (t k)", c=CHUNKS_PER_BATCH, t=CHUNK_TILES)
-            for c in range(CHUNKS_PER_BATCH):
-                x_sb = x_pool.tile([P, CHUNK_TILES * D], BF16)
-                x_chunks.append(x_sb)
-                if b == 0 and c == 0:
-                    pair_cols = PAIR * D
-                    nc.sync.dma_start(out=x_sb[:, :pair_cols], in_=chunks[c][:, :pair_cols])
-                    nc.sync.dma_start(out=x_sb[:, pair_cols:], in_=chunks[c][:, pair_cols:])
-                else:
-                    nc.sync.dma_start(out=x_sb[:], in_=chunks[c])
-                if b == 0 and c == WV_AFTER:
-                    load_weight("wv", wv)
+        chunks = x.rearrange("b (q c t) k -> c (b q) (t k)", c=N_CHUNKS, t=CHUNK_TILES)
+        for c in range(N_CHUNKS):
+            x_sb = x_pool.tile([P, CHUNK_TILES * D], BF16)
+            x_chunks.append(x_sb)
+            if c == 0:
+                pair_cols = PAIR * D
+                nc.sync.dma_start(out=x_sb[:, :pair_cols], in_=chunks[c][:, :pair_cols])
+                nc.sync.dma_start(out=x_sb[:, pair_cols:], in_=chunks[c][:, pair_cols:])
+            else:
+                nc.sync.dma_start(out=x_sb[:], in_=chunks[c])
+            if c == WV_AFTER:
+                load_weight("wv", wv)
 
         ident = consts.tile([P, P], F32)
         make_identity(nc, ident[:])
@@ -248,7 +248,7 @@ def tile_hydraencoderlayer_pa_t_kernel(tc, x, wk, wv, out):
             )
 
         def add_tokens(n):
-            b, q = divmod(n, PAIRS_PER_BATCH)
+            b, q = 0, n
             if q == 0:
                 token_sums[b] = psum_s.tile([P, E_BLOCKS, P], F32, name="token_sums")
             blocks = []
@@ -265,13 +265,13 @@ def tile_hydraencoderlayer_pa_t_kernel(tc, x, wk, wv, out):
                     rhs=ident[:],
                     is_transpose=True,
                     start=(q == 0 and k == 0),
-                    stop=(q == PAIRS_PER_BATCH - 1 and k == len(blocks) - 1),
+                    stop=(q == N_PAIRS - 1 and k == len(blocks) - 1),
                 )
 
-        def add_partitions(b):
+        def add_partitions():
             nc.vector.tensor_reduce(
-                out=out_cols[:, b * E_BLOCKS : (b + 1) * E_BLOCKS],
-                in_=token_sums[b][:],
+                out=out_cols[:, : BATCH * E_BLOCKS].rearrange("e (b i) -> e i b", b=BATCH),
+                in_=token_sums[0][:].rearrange("e i (b q) -> e i b q", b=BATCH),
                 axis=mybir.AxisListType.X,
                 op=ALU.add,
             )
@@ -291,8 +291,6 @@ def tile_hydraencoderlayer_pa_t_kernel(tc, x, wk, wv, out):
                 copy_a(n, 0, copy=nc.vector.tensor_copy)
             if live(n + 3):
                 regroup_x(n + 3)
-            if live(s - 1) and (s - 1) % PAIRS_PER_BATCH == PAIRS_PER_BATCH - 1:
-                add_partitions((s - 1) // PAIRS_PER_BATCH)
             if live(n) and n > 0:
                 pass_a(n, 1)
             if live(m):
@@ -356,8 +354,9 @@ def tile_hydraencoderlayer_pa_t_kernel(tc, x, wk, wv, out):
         quantise_x(2)
         interleave_weight("wv", WV_SPLIT)
         quantise_x(3)
-        for n in range(1, N_PAIRS + LAG + SUM_LAG + 1):
+        for n in range(1, N_PAIRS + LAG + SUM_LAG):
             step(n)
+        add_partitions()
 
         out_rows_ps = psum_t.tile([P, P], F32, name="xt")
         nc.tensor.transpose(out_rows_ps[:], out_cols[:], ident[:])

@@ -33,12 +33,15 @@ WV_AFTER = 1
 WV_STEP = 1
 WV_SPLIT = 512
 COPY_HEAD = 3
-GROUP = 2
-SINGLES = 4
+GROUP = 4
+PAIRED = 8
+SINGLES = 2
+N_TILES = N_PAIRS * PAIR
+TAIL_VEC = 0
 A_BUFS = 10
 POOL_BLOCKS = 4
 POOL_EVERY = 1
-POOL_TAIL = 2
+POOL_TAIL = 3
 COPY_EVERY = 4
 COPY_TAIL = 3
 X_BUFS = 8
@@ -183,48 +186,47 @@ def tile_hydraencoderlayer_pa_t_kernel(tc, x, wk, wv, out):
             a_ps[n, j] = psum_a.tile([P, DI], F32, name="a_ps")
             mx_pass(a_ps[n, j], n, j, "wk")
 
-        def pass_v(n, j):
-            v_ps[n, j] = psum_v.tile([P, DI], F32, name="v_ps")
+        def pass_v(n, j, pool=psum_v, name="v_ps"):
+            v_ps[n, j] = pool.tile([P, DI], F32, name=name)
             mx_pass(v_ps[n, j], n, j, "wv")
 
         def copy_a(n, j, copy=nc.scalar.copy):
             a_sb[n, j] = work.tile([P, DI], F32, name="a_sb", bufs=A_BUFS)
             copy(out=a_sb[n, j][:], in_=a_ps[n, j][:])
 
-        def group_of(n):
-            if n >= N_PAIRS - SINGLES:
-                return n, 1
-            return n - n % GROUP, GROUP
+        def group_of(t):
+            size = GROUP if t < N_TILES - PAIRED else (PAIR if t < N_TILES - SINGLES else 1)
+            return t - t % size, size
 
         def square_sum(n, j, source=a_sb):
-            first, count = group_of(n)
+            t = n * PAIR + j
+            first, count = group_of(t)
             if first not in norm2:
-                norm2[first] = work.tile([P, count * PAIR], F32, name="norm2")
-            col = (n - first) * PAIR + j
+                norm2[first] = work.tile([P, count], F32, name="norm2")
             squares = work.tile([P, DI], BF16, name="squares")
             nc.scalar.activation(
                 out=squares[:], in_=source[n, j][:], func=ACT.Square,
-                accum_out=norm2[first][:, col : col + 1],
+                accum_out=norm2[first][:, t - first : t - first + 1],
             )
 
         def closes_group(n):
-            return live(n) and sum(group_of(n)) == n + 1
+            return live(n) and sum(group_of(n * PAIR + 1)) == (n + 1) * PAIR
 
-        def clamp_norm(n):
-            first, count = group_of(n)
-            clamped[first] = work.tile([P, count * PAIR], F32, name="clamped")
+        def clamp_norm(n, j=1):
+            first, count = group_of(n * PAIR + j)
+            clamped[first] = work.tile([P, count], F32, name="clamped")
             nc.scalar.activation(out=clamped[first][:], in_=norm2[first][:], func=ACT.Relu, bias=-EPS * EPS)
 
-        def invert_norm(n):
-            first, count = group_of(n)
-            rnorm[first] = work.tile([P, count * PAIR], F32, name="rnorm")
+        def invert_norm(n, j=1):
+            first, count = group_of(n * PAIR + j)
+            rnorm[first] = work.tile([P, count], F32, name="rnorm")
             nc.scalar.activation(out=rnorm[first][:], in_=clamped[first][:], func=ACT.Abs_reciprocal_sqrt,
                                  bias=EPS * EPS)
 
         def rnorm_of(n, j):
-            first, count = group_of(n)
-            col = (n - first) * PAIR + j
-            return rnorm[first][:, col : col + 1]
+            t = n * PAIR + j
+            first, count = group_of(t)
+            return rnorm[first][:, t - first : t - first + 1]
 
         def product(n, j):
             if j == 0:
@@ -247,17 +249,18 @@ def tile_hydraencoderlayer_pa_t_kernel(tc, x, wk, wv, out):
                 out=pair_sum[n][:, :cols], in0=prod[n][:, 0, :cols], in1=prod[n][:, 1, :cols], op=ALU.add
             )
 
-        def add_tokens(n):
+        def add_tokens(n, tiles=range(PAIR)):
             b, q = 0, n
             if q == 0:
                 token_sums[b] = psum_s.tile([P, E_BLOCKS, P], F32, name="token_sums")
             blocks = []
-            for i in range(E_BLOCKS):
-                cols = slice(i * P, (i + 1) * P)
-                if n in pair_sum and i < POOL_BLOCKS:
-                    blocks.append((i, pair_sum[n][:, cols]))
-                else:
-                    blocks.extend([(i, prod[n][:, j, cols]) for j in range(PAIR)])
+            for j in tiles:
+                for i in range(E_BLOCKS):
+                    cols = slice(i * P, (i + 1) * P)
+                    if n not in pair_sum or i >= POOL_BLOCKS:
+                        blocks.append((i, prod[n][:, j, cols]))
+                    elif j == 0:
+                        blocks.append((i, pair_sum[n][:, cols]))
             for k, (i, block) in enumerate(blocks):
                 nc.tensor.matmul(
                     out=token_sums[b][:, i, :],
@@ -265,7 +268,7 @@ def tile_hydraencoderlayer_pa_t_kernel(tc, x, wk, wv, out):
                     rhs=ident[:],
                     is_transpose=True,
                     start=(q == 0 and k == 0),
-                    stop=(q == N_PAIRS - 1 and k == len(blocks) - 1),
+                    stop=(q == N_PAIRS - 1 and PAIR - 1 in tiles and k == len(blocks) - 1),
                 )
 
         def add_partitions():
@@ -354,8 +357,78 @@ def tile_hydraencoderlayer_pa_t_kernel(tc, x, wk, wv, out):
         quantise_x(2)
         interleave_weight("wv", WV_SPLIT)
         quantise_x(3)
-        for n in range(1, N_PAIRS + LAG + SUM_LAG):
+        tail = N_PAIRS - 3
+        for n in range(1, tail):
             step(n)
+
+        vec = nc.vector.tensor_copy
+        n = tail
+        last = N_PAIRS - 1
+        pass_a(n, 1)
+        pass_v(n - 3, 1)
+        pass_a(n + 1, 0)
+        copy_a(n, 0)
+        invert_norm(n - 2)
+        copy_a(n, 1, copy=vec)
+        square_sum(n - 1, 1)
+        square_sum(n, 0)
+        clamp_norm(n - 1)
+        product(n - 3, 0)
+        pass_v(n - 2, 0)
+        pass_a(n + 1, 1)
+        add_tokens(n - 5)
+        product(n - 3, 1)
+        add_pair(n - 3)
+        pass_v(n - 2, 1)
+        copy_a(n + 1, 0)
+        invert_norm(n - 1)
+        square_sum(n, 1)
+        product(n - 2, 0)
+        pass_a(last, 0)
+        pass_v(n - 1, 0)
+        if TAIL_VEC:
+            copy_a(n + 1, 1, copy=vec)
+        else:
+            copy_a(n + 1, 1)
+        square_sum(n + 1, 0)
+        clamp_norm(n)
+        add_tokens(n - 4)
+        product(n - 2, 1)
+        add_pair(n - 2)
+        pass_a(last, 1)
+        pass_v(n - 1, 1)
+        copy_a(last, 0)
+        invert_norm(n)
+        square_sum(n + 1, 1)
+        product(n - 1, 0)
+        pass_v(n, 0)
+        add_tokens(n - 3)
+        product(n - 1, 1)
+        add_pair(n - 1)
+        pass_v(n, 1)
+        pass_v(last, 0, psum_t, "xt")
+        copy_a(last, 1)
+        clamp_norm(n + 1)
+        square_sum(last, 0)
+        invert_norm(n + 1)
+        product(n, 0)
+        pass_v(n + 1, 0)
+        pass_v(n + 1, 1, psum_a, "a_ps")
+        add_tokens(n - 2)
+        product(n, 1)
+        add_pair(n)
+        pass_v(last, 1)
+        clamp_norm(last, 0)
+        square_sum(last, 1)
+        invert_norm(last, 0)
+        clamp_norm(last, 1)
+        invert_norm(last, 1)
+        add_tokens(n - 1)
+        add_tokens(n)
+        for m in (n + 1, last):
+            for j in range(PAIR):
+                product(m, j)
+                add_tokens(m, [j])
         add_partitions()
 
         out_rows_ps = psum_t.tile([P, P], F32, name="xt")

@@ -31,13 +31,16 @@ LAG = 3
 SUM_LAG = 2
 WV_AFTER = 1
 WV_STEP = 1
-WV_SPLIT = 512
+WV_SPLIT = 320
 COPY_HEAD = 3
 GROUP = 4
 PAIRED = 8
 SINGLES = 2
 N_TILES = N_PAIRS * PAIR
 TAIL_VEC = 0
+LATE_SQ = 0
+RUN = 4
+WV_EARLY = 0
 A_BUFS = 10
 POOL_BLOCKS = 4
 POOL_EVERY = 1
@@ -113,11 +116,11 @@ def tile_hydraencoderlayer_pa_t_kernel(tc, x, wk, wv, out):
             )
 
         def interleave_weight(label, split):
-            by_column = w_raw[label][:].rearrange("q t c -> q c t")
-            grouped_w = w_grouped[label]
-            nc.vector.tensor_copy(out=grouped_w[:, :split, :], in_=by_column[:, :split, :])
+            by_column = w_raw[label][:].rearrange("q t (c i) -> q c t i", i=RUN)
+            grouped_w = w_grouped[label][:].rearrange("q (c i) t -> q c t i", i=RUN)
+            nc.vector.tensor_copy(out=grouped_w[:, : split // RUN], in_=by_column[:, : split // RUN])
             if split < DI:
-                nc.scalar.copy(out=grouped_w[:, split:, :], in_=by_column[:, split:, :])
+                nc.scalar.copy(out=grouped_w[:, split // RUN :], in_=by_column[:, split // RUN :])
 
         def warm_up(count):
             bank = psum_s.tile([P, DI], F32, name="token_sums")
@@ -304,10 +307,13 @@ def tile_hydraencoderlayer_pa_t_kernel(tc, x, wk, wv, out):
                 copy_a(n, 0)
             if closes_group(n - 2):
                 invert_norm(n - 2)
-            if live(n - 1):
+            late = LATE_SQ == 2 or (LATE_SQ == 1 and on_vector(n - 1, 1))
+            if live(n - 1) and not late:
                 square_sum(n - 1, 1)
             if live(n) and not on_vector(n, 1):
                 copy_a(n, 1)
+            if live(n - 1) and late:
+                square_sum(n - 1, 1)
             if live(n):
                 square_sum(n, 0)
             if closes_group(n - 1):
@@ -345,6 +351,8 @@ def tile_hydraencoderlayer_pa_t_kernel(tc, x, wk, wv, out):
         pass_a(0, 0)
         pass_a(0, 1)
         quantise_x(1)
+        if WV_EARLY:
+            interleave_weight("wv", WV_SPLIT)
         transpose_x(2, new_xt(psum_v, "v_ps"))
         transpose_x(3, new_xt())
         pass_a(1, 0)
@@ -355,7 +363,8 @@ def tile_hydraencoderlayer_pa_t_kernel(tc, x, wk, wv, out):
         transpose_x(4, new_xt())
         square_sum(0, 0)
         quantise_x(2)
-        interleave_weight("wv", WV_SPLIT)
+        if not WV_EARLY:
+            interleave_weight("wv", WV_SPLIT)
         quantise_x(3)
         tail = N_PAIRS - 3
         for n in range(1, tail):

@@ -24,7 +24,7 @@ PAIRS_PER_CHUNK = CHUNK_TILES // PAIR
 PAIRS_PER_BATCH = CHUNKS_PER_BATCH * PAIRS_PER_CHUNK
 N_PAIRS = BATCH * PAIRS_PER_BATCH
 N_CHUNKS = BATCH * CHUNKS_PER_BATCH
-W_SPLIT = 320
+W_SPLIT = 336
 E_BLOCKS = DI // P
 
 LAG = 3
@@ -37,7 +37,7 @@ GROUP = 4
 PAIRED = 8
 SINGLES = 2
 N_TILES = N_PAIRS * PAIR
-TAIL_VEC = 0
+TAIL_VEC = 1
 LATE_SQ = 0
 RUN = 4
 WV_EARLY = 0
@@ -81,9 +81,8 @@ def tile_hydraencoderlayer_pa_t_kernel(tc, x, wk, wv, out):
             x_sb = x_pool.tile([P, CHUNK_TILES * D], BF16)
             x_chunks.append(x_sb)
             if c == 0:
-                pair_cols = PAIR * D
-                nc.sync.dma_start(out=x_sb[:, :pair_cols], in_=chunks[c][:, :pair_cols])
-                nc.sync.dma_start(out=x_sb[:, pair_cols:], in_=chunks[c][:, pair_cols:])
+                for first, stop in ((0, D), (D, PAIR * D), (PAIR * D, CHUNK_TILES * D)):
+                    nc.sync.dma_start(out=x_sb[:, first:stop], in_=chunks[c][:, first:stop])
             else:
                 nc.sync.dma_start(out=x_sb[:], in_=chunks[c])
             if c == WV_AFTER:
@@ -108,17 +107,19 @@ def tile_hydraencoderlayer_pa_t_kernel(tc, x, wk, wv, out):
             w_codes[label] = consts.tile([P, DI], U32, name="%s_codes" % label, align_bytes=256)
             w_scales[label] = consts.tile([P, DI], U8, name="%s_scales" % label, align_bytes=256)
 
-        def quantise_weight(label):
+        def quantise_weight(label, cols=slice(0, DI)):
             nc.vector.quantize_mx(
-                out=w_codes[label][:].bitcast(FP8X4),
-                scales=w_scales[label][:],
-                in_=w_grouped[label][:].rearrange("q c t -> q (c t)"),
+                out=w_codes[label][:, cols].bitcast(FP8X4),
+                scales=w_scales[label][:, cols],
+                in_=w_grouped[label][:, cols, :].rearrange("q c t -> q (c t)"),
             )
 
-        def interleave_weight(label, split):
+        def interleave_weight(label, split, first=0):
             by_column = w_raw[label][:].rearrange("q t (c i) -> q c t i", i=RUN)
             grouped_w = w_grouped[label][:].rearrange("q (c i) t -> q c t i", i=RUN)
-            nc.vector.tensor_copy(out=grouped_w[:, : split // RUN], in_=by_column[:, : split // RUN])
+            if first:
+                nc.vector.tensor_copy(out=grouped_w[:, : first // RUN], in_=by_column[:, : first // RUN])
+            nc.vector.tensor_copy(out=grouped_w[:, first // RUN : split // RUN], in_=by_column[:, first // RUN : split // RUN])
             if split < DI:
                 nc.scalar.copy(out=grouped_w[:, split // RUN :], in_=by_column[:, split // RUN :])
 
@@ -337,8 +338,9 @@ def tile_hydraencoderlayer_pa_t_kernel(tc, x, wk, wv, out):
                 quantise_x(n + 3)
 
         warm_up(6)
-        interleave_weight("wk", W_SPLIT)
-        quantise_weight("wk")
+        interleave_weight("wk", W_SPLIT, DI // 2)
+        quantise_weight("wk", slice(0, DI // 2))
+        quantise_weight("wk", slice(DI // 2, DI))
         banks = [new_xt(), new_xt(psum_v, "v_ps")]
         for j in range(PAIR):
             transpose_tile(banks[j], 0, j)

@@ -294,48 +294,42 @@ def tile_hydraencoderlayer_pa_t_kernel(tc, x, wk, wv, out):
         def step(n):
             m = n - LAG
             s = m - SUM_LAG
-            if live(n) and on_vector(n, 0):
-                copy_a(n, 0, copy=nc.vector.tensor_copy)
-            if live(n + 3):
-                regroup_x(n + 3)
-            if live(n) and n > 0:
-                pass_a(n, 1)
+            regroup_x(n + 3)
+            pass_a(n, 1)
+            if on_vector(n, 1):
+                copy_a(n, 1, copy=nc.vector.tensor_copy)
             if live(m):
                 pass_v(m, 1)
-            if live(n + 1):
-                pass_a(n + 1, 0)
-            if live(n) and not on_vector(n, 0):
-                copy_a(n, 0)
-            if closes_group(n - 2):
+            pass_a(n + 1, 0)
+            copy_a(n, 0)
+            if closes_group(n - 2) and on_vector(n - 1, 1):
                 invert_norm(n - 2)
-            late = LATE_SQ == 2 or (LATE_SQ == 1 and on_vector(n - 1, 1))
-            if live(n - 1) and not late:
-                square_sum(n - 1, 1)
-            if live(n) and not on_vector(n, 1):
-                copy_a(n, 1)
-            if live(n - 1) and late:
-                square_sum(n - 1, 1)
-            if live(n):
+            square_sum(n - 1, 1)
+            if on_vector(n, 1):
                 square_sum(n, 0)
-            if closes_group(n - 1):
-                clamp_norm(n - 1)
+                if closes_group(n - 1):
+                    clamp_norm(n - 1)
+            else:
+                copy_a(n, 1)
+                if closes_group(n - 1):
+                    clamp_norm(n - 1)
+                square_sum(n, 0)
+                if closes_group(n - 1):
+                    invert_norm(n - 1)
             if live(m):
                 product(m, 0)
-            if live(n) and on_vector(n, 1):
-                copy_a(n, 1, copy=nc.vector.tensor_copy)
             if n == WV_STEP:
                 quantise_weight("wv")
             if live(m + 1):
                 pass_v(m + 1, 0)
-            if live(n + 4):
-                transpose_x(n + 4, new_xt())
             if live(s):
                 add_tokens(s)
+            if live(n + 4):
+                transpose_x(n + 4, new_xt())
             if live(m):
                 product(m, 1)
                 add_pair(m)
-            if live(n + 3):
-                quantise_x(n + 3)
+            quantise_x(n + 3)
 
         warm_up(6)
         interleave_weight("wk", W_SPLIT, DI // 2)
@@ -379,7 +373,6 @@ def tile_hydraencoderlayer_pa_t_kernel(tc, x, wk, wv, out):
         pass_v(n - 3, 1)
         pass_a(n + 1, 0)
         copy_a(n, 0)
-        invert_norm(n - 2)
         copy_a(n, 1, copy=vec)
         square_sum(n - 1, 1)
         square_sum(n, 0)

@@ -35,16 +35,21 @@ WV_SPLIT = 320
 COPY_HEAD = 3
 GROUP = 4
 PAIRED = 8
-SINGLES = 2
+SINGLES = 0
 N_TILES = N_PAIRS * PAIR
-TAIL_VEC = 1
-LATE_SQ = 0
+TAIL_VEC = 0
+ORDER = 0
+VEC_CLAMP = 2
+TAIL_SPLIT = 512
+LAST_PARTS = 2
+COPY_PHASE = 3
+COPY_FROM = 0
 RUN = 4
 WV_EARLY = 0
 A_BUFS = 10
 POOL_BLOCKS = 4
 POOL_EVERY = 1
-POOL_TAIL = 3
+POOL_TAIL = 2
 COPY_EVERY = 4
 COPY_TAIL = 3
 X_BUFS = 8
@@ -68,12 +73,18 @@ def tile_hydraencoderlayer_pa_t_kernel(tc, x, wk, wv, out):
 
         w_raw = {}
 
-        def load_weight(label, w):
-            w_raw[label] = consts.tile([P, PACK, DI], BF16, name="%s_raw" % label)
-            nc.sync.dma_start(
-                out=w_raw[label][:].rearrange("q (u e) c -> q u (e c)", u=HALVES),
-                in_=w.rearrange("(u q e) c -> q u (e c)", u=HALVES, e=2),
-            )
+        def load_weight(label, w, cols=slice(0, DI)):
+            if label not in w_raw:
+                w_raw[label] = consts.tile([P, PACK, DI], BF16, name="%s_raw" % label)
+            if cols.stop - cols.start == DI:
+                nc.sync.dma_start(
+                    out=w_raw[label][:].rearrange("q (u e) c -> q u (e c)", u=HALVES),
+                    in_=w.rearrange("(u q e) c -> q u (e c)", u=HALVES, e=2),
+                )
+                return
+            rows = w.rearrange("(u q e) c -> u q e c", u=HALVES, e=2)
+            for u in range(HALVES):
+                nc.sync.dma_start(out=w_raw[label][:, 2 * u : 2 * u + 2, cols], in_=rows[u][:, :, cols])
         load_weight("wk", wk)
         x_chunks = []
         chunks = x.rearrange("b (q c t) k -> c (b q) (t k)", c=N_CHUNKS, t=CHUNK_TILES)
@@ -85,8 +96,10 @@ def tile_hydraencoderlayer_pa_t_kernel(tc, x, wk, wv, out):
                     nc.sync.dma_start(out=x_sb[:, first:stop], in_=chunks[c][:, first:stop])
             else:
                 nc.sync.dma_start(out=x_sb[:], in_=chunks[c])
+            if c == 0:
+                load_weight("wv", wv, slice(WV_SPLIT, DI))
             if c == WV_AFTER:
-                load_weight("wv", wv)
+                load_weight("wv", wv, slice(0, WV_SPLIT))
 
         ident = consts.tile([P, P], F32)
         make_identity(nc, ident[:])
@@ -96,6 +109,12 @@ def tile_hydraencoderlayer_pa_t_kernel(tc, x, wk, wv, out):
         nc.vector.memset(zeros[:], 0.0)
         table_load = consts.tile([P, 1], F32)
         nc.scalar.activation(out=table_load[:], in_=zeros[:, :1], func=ACT.Abs_reciprocal_sqrt, bias=1.0)
+
+        floored = {}
+        for n in range(N_PAIRS - VEC_CLAMP, N_PAIRS):
+            floored[n * PAIR] = consts.tile([P, PAIR, 2], F32, name="floored_%d" % n)
+            nc.vector.tensor_scalar(out=floored[n * PAIR][:].rearrange("p a b -> p (a b)"), in0=out_cols[:, : 2 * PAIR],
+                                    scalar1=EPS * EPS, scalar2=None, op0=ALU.add)
 
         w_grouped = {}
         w_codes = {}
@@ -114,14 +133,11 @@ def tile_hydraencoderlayer_pa_t_kernel(tc, x, wk, wv, out):
                 in_=w_grouped[label][:, cols, :].rearrange("q c t -> q (c t)"),
             )
 
-        def interleave_weight(label, split, first=0):
+        def interleave_weight(label, cols, copy):
             by_column = w_raw[label][:].rearrange("q t (c i) -> q c t i", i=RUN)
             grouped_w = w_grouped[label][:].rearrange("q (c i) t -> q c t i", i=RUN)
-            if first:
-                nc.vector.tensor_copy(out=grouped_w[:, : first // RUN], in_=by_column[:, : first // RUN])
-            nc.vector.tensor_copy(out=grouped_w[:, first // RUN : split // RUN], in_=by_column[:, first // RUN : split // RUN])
-            if split < DI:
-                nc.scalar.copy(out=grouped_w[:, split // RUN :], in_=by_column[:, split // RUN :])
+            runs = slice(cols.start // RUN, cols.stop // RUN)
+            copy(out=grouped_w[:, runs], in_=by_column[:, runs])
 
         def warm_up(count):
             bank = psum_s.tile([P, DI], F32, name="token_sums")
@@ -194,9 +210,10 @@ def tile_hydraencoderlayer_pa_t_kernel(tc, x, wk, wv, out):
             v_ps[n, j] = pool.tile([P, DI], F32, name=name)
             mx_pass(v_ps[n, j], n, j, "wv")
 
-        def copy_a(n, j, copy=nc.scalar.copy):
-            a_sb[n, j] = work.tile([P, DI], F32, name="a_sb", bufs=A_BUFS)
-            copy(out=a_sb[n, j][:], in_=a_ps[n, j][:])
+        def copy_a(n, j, copy=nc.scalar.copy, cols=slice(0, DI)):
+            if (n, j) not in a_sb:
+                a_sb[n, j] = work.tile([P, DI], F32, name="a_sb", bufs=A_BUFS)
+            copy(out=a_sb[n, j][:, cols], in_=a_ps[n, j][:, cols])
 
         def group_of(t):
             size = GROUP if t < N_TILES - PAIRED else (PAIR if t < N_TILES - SINGLES else 1)
@@ -205,13 +222,14 @@ def tile_hydraencoderlayer_pa_t_kernel(tc, x, wk, wv, out):
         def square_sum(n, j, source=a_sb):
             t = n * PAIR + j
             first, count = group_of(t)
-            if first not in norm2:
-                norm2[first] = work.tile([P, count], F32, name="norm2")
+            if first in floored:
+                column = floored[first][:, t - first, 0:1]
+            else:
+                if first not in norm2:
+                    norm2[first] = work.tile([P, count], F32, name="norm2")
+                column = norm2[first][:, t - first : t - first + 1]
             squares = work.tile([P, DI], BF16, name="squares")
-            nc.scalar.activation(
-                out=squares[:], in_=source[n, j][:], func=ACT.Square,
-                accum_out=norm2[first][:, t - first : t - first + 1],
-            )
+            nc.scalar.activation(out=squares[:], in_=source[n, j][:], func=ACT.Square, accum_out=column)
 
         def closes_group(n):
             return live(n) and sum(group_of(n * PAIR + 1)) == (n + 1) * PAIR
@@ -219,27 +237,30 @@ def tile_hydraencoderlayer_pa_t_kernel(tc, x, wk, wv, out):
         def clamp_norm(n, j=1):
             first, count = group_of(n * PAIR + j)
             clamped[first] = work.tile([P, count], F32, name="clamped")
-            nc.scalar.activation(out=clamped[first][:], in_=norm2[first][:], func=ACT.Relu, bias=-EPS * EPS)
+            if first in floored:
+                nc.vector.tensor_reduce(out=clamped[first][:], in_=floored[first][:], axis=mybir.AxisListType.X, op=ALU.max)
+            else:
+                nc.scalar.activation(out=clamped[first][:], in_=norm2[first][:], func=ACT.Relu, bias=-EPS * EPS)
 
         def invert_norm(n, j=1):
             first, count = group_of(n * PAIR + j)
             rnorm[first] = work.tile([P, count], F32, name="rnorm")
             nc.scalar.activation(out=rnorm[first][:], in_=clamped[first][:], func=ACT.Abs_reciprocal_sqrt,
-                                 bias=EPS * EPS)
+                                 bias=(0.0 if first in floored else EPS * EPS))
 
         def rnorm_of(n, j):
             t = n * PAIR + j
             first, count = group_of(t)
             return rnorm[first][:, t - first : t - first + 1]
 
-        def product(n, j):
-            if j == 0:
+        def product(n, j, cols=slice(0, DI)):
+            if n not in prod:
                 prod[n] = work.tile([P, PAIR, DI], F32, name="prod")
             nc.vector.scalar_tensor_tensor(
-                out=prod[n][:, j, :],
-                in0=a_sb[n, j][:],
+                out=prod[n][:, j, cols],
+                in0=a_sb[n, j][:, cols],
                 scalar=rnorm_of(n, j),
-                in1=v_ps[n, j][:],
+                in1=v_ps[n, j][:, cols],
                 op0=ALU.mult,
                 op1=ALU.mult,
             )
@@ -253,13 +274,13 @@ def tile_hydraencoderlayer_pa_t_kernel(tc, x, wk, wv, out):
                 out=pair_sum[n][:, :cols], in0=prod[n][:, 0, :cols], in1=prod[n][:, 1, :cols], op=ALU.add
             )
 
-        def add_tokens(n, tiles=range(PAIR)):
+        def add_tokens(n, tiles=range(PAIR), col_blocks=range(E_BLOCKS)):
             b, q = 0, n
             if q == 0:
                 token_sums[b] = psum_s.tile([P, E_BLOCKS, P], F32, name="token_sums")
             blocks = []
             for j in tiles:
-                for i in range(E_BLOCKS):
+                for i in col_blocks:
                     cols = slice(i * P, (i + 1) * P)
                     if n not in pair_sum or i >= POOL_BLOCKS:
                         blocks.append((i, prod[n][:, j, cols]))
@@ -272,7 +293,7 @@ def tile_hydraencoderlayer_pa_t_kernel(tc, x, wk, wv, out):
                     rhs=ident[:],
                     is_transpose=True,
                     start=(q == 0 and k == 0),
-                    stop=(q == N_PAIRS - 1 and PAIR - 1 in tiles and k == len(blocks) - 1),
+                    stop=(q == N_PAIRS - 1 and PAIR - 1 in tiles and i == E_BLOCKS - 1),
                 )
 
         def add_partitions():
@@ -289,7 +310,7 @@ def tile_hydraencoderlayer_pa_t_kernel(tc, x, wk, wv, out):
         def on_vector(n, j):
             if n < COPY_HEAD:
                 return j == 1
-            return j == 1 and n % COPY_EVERY == COPY_EVERY - 1 and n < N_PAIRS - COPY_TAIL
+            return j == 1 and n % COPY_EVERY == COPY_PHASE and COPY_FROM <= n < N_PAIRS - COPY_TAIL
 
         def step(n):
             m = n - LAG
@@ -318,7 +339,7 @@ def tile_hydraencoderlayer_pa_t_kernel(tc, x, wk, wv, out):
                     invert_norm(n - 1)
             if live(m):
                 product(m, 0)
-            if n == WV_STEP:
+            if n == WV_STEP and ORDER == 0:
                 quantise_weight("wv")
             if live(m + 1):
                 pass_v(m + 1, 0)
@@ -332,7 +353,9 @@ def tile_hydraencoderlayer_pa_t_kernel(tc, x, wk, wv, out):
             quantise_x(n + 3)
 
         warm_up(6)
-        interleave_weight("wk", W_SPLIT, DI // 2)
+        interleave_weight("wk", slice(0, DI // 2), nc.vector.tensor_copy)
+        interleave_weight("wk", slice(DI // 2, W_SPLIT), nc.vector.tensor_copy)
+        interleave_weight("wk", slice(W_SPLIT, DI), nc.scalar.copy)
         quantise_weight("wk", slice(0, DI // 2))
         quantise_weight("wk", slice(DI // 2, DI))
         banks = [new_xt(), new_xt(psum_v, "v_ps")]
@@ -343,24 +366,29 @@ def tile_hydraencoderlayer_pa_t_kernel(tc, x, wk, wv, out):
         for j in range(PAIR):
             regroup_tiles(0, slice(j, j + 1), banks[j], nc.scalar.copy)
             quantise_tiles(0, slice(j, j + 1))
-        regroup_tiles(1, slice(0, PAIR), xt[1], nc.scalar.copy)
+        regroup_x(1)
+        interleave_weight("wv", slice(WV_SPLIT, DI), nc.scalar.copy)
         pass_a(0, 0)
         pass_a(0, 1)
         quantise_x(1)
-        if WV_EARLY:
-            interleave_weight("wv", WV_SPLIT)
         transpose_x(2, new_xt(psum_v, "v_ps"))
         transpose_x(3, new_xt())
-        pass_a(1, 0)
         copy_a(0, 0)
         copy_a(0, 1, copy=nc.vector.tensor_copy)
+        pass_a(1, 0)
         regroup_tiles(2, slice(0, PAIR), xt[2], nc.scalar.copy)
-        regroup_x(3)
-        transpose_x(4, new_xt())
         square_sum(0, 0)
-        quantise_x(2)
-        if not WV_EARLY:
-            interleave_weight("wv", WV_SPLIT)
+        if ORDER == 0:
+            regroup_x(3)
+            quantise_x(2)
+            interleave_weight("wv", slice(0, WV_SPLIT), nc.vector.tensor_copy)
+        else:
+            interleave_weight("wv", slice(0, WV_SPLIT), nc.vector.tensor_copy)
+            regroup_x(3)
+            quantise_x(2)
+        transpose_x(4, new_xt())
+        if ORDER == 1:
+            quantise_weight("wv")
         quantise_x(3)
         tail = N_PAIRS - 3
         for n in range(1, tail):
@@ -373,10 +401,15 @@ def tile_hydraencoderlayer_pa_t_kernel(tc, x, wk, wv, out):
         pass_v(n - 3, 1)
         pass_a(n + 1, 0)
         copy_a(n, 0)
-        copy_a(n, 1, copy=vec)
+        copy_a(n, 1, vec, slice(0, TAIL_SPLIT))
         square_sum(n - 1, 1)
-        square_sum(n, 0)
-        clamp_norm(n - 1)
+        if TAIL_SPLIT < DI:
+            copy_a(n, 1, cols=slice(TAIL_SPLIT, DI))
+            clamp_norm(n - 1)
+            square_sum(n, 0)
+        else:
+            square_sum(n, 0)
+            clamp_norm(n - 1)
         product(n - 3, 0)
         pass_v(n - 2, 0)
         pass_a(n + 1, 1)
@@ -394,15 +427,14 @@ def tile_hydraencoderlayer_pa_t_kernel(tc, x, wk, wv, out):
             copy_a(n + 1, 1, copy=vec)
         else:
             copy_a(n + 1, 1)
-        square_sum(n + 1, 0)
         clamp_norm(n)
+        square_sum(n + 1, 0)
+        invert_norm(n)
         add_tokens(n - 4)
         product(n - 2, 1)
         add_pair(n - 2)
-        pass_a(last, 1)
         pass_v(n - 1, 1)
-        copy_a(last, 0)
-        invert_norm(n)
+        pass_a(last, 1)
         square_sum(n + 1, 1)
         product(n - 1, 0)
         pass_v(n, 0)
@@ -411,28 +443,32 @@ def tile_hydraencoderlayer_pa_t_kernel(tc, x, wk, wv, out):
         add_pair(n - 1)
         pass_v(n, 1)
         pass_v(last, 0, psum_t, "xt")
-        copy_a(last, 1)
-        clamp_norm(n + 1)
-        square_sum(last, 0)
-        invert_norm(n + 1)
+        square_sum(last, 0, a_ps)
         product(n, 0)
+        clamp_norm(n + 1)
+        invert_norm(n + 1)
+        square_sum(last, 1, a_ps)
+        copy_a(last, 0)
         pass_v(n + 1, 0)
         pass_v(n + 1, 1, psum_a, "a_ps")
         add_tokens(n - 2)
         product(n, 1)
         add_pair(n)
         pass_v(last, 1)
-        clamp_norm(last, 0)
-        square_sum(last, 1)
-        invert_norm(last, 0)
-        clamp_norm(last, 1)
-        invert_norm(last, 1)
         add_tokens(n - 1)
-        add_tokens(n)
-        for m in (n + 1, last):
-            for j in range(PAIR):
-                product(m, j)
-                add_tokens(m, [j])
+        for m, j in ((n + 1, 0), (n + 1, 1), (last, 0)):
+            product(m, j)
+            if (m, j) == (n + 1, 0):
+                clamp_norm(last)
+                invert_norm(last)
+                copy_a(last, 1)
+            if (m, j) == (last, 0):
+                add_tokens(n)
+            add_tokens(m, [j])
+        step_blocks = E_BLOCKS // LAST_PARTS
+        for first in range(0, E_BLOCKS, step_blocks):
+            product(last, 1, slice(first * P, (first + step_blocks) * P))
+            add_tokens(last, [1], range(first, first + step_blocks))
         add_partitions()
 
         out_rows_ps = psum_t.tile([P, P], F32, name="xt")

@@ -96,10 +96,8 @@ def tile_hydraencoderlayer_pa_t_kernel(tc, x, wk, wv, out):
                     nc.sync.dma_start(out=x_sb[:, first:stop], in_=chunks[c][:, first:stop])
             else:
                 nc.sync.dma_start(out=x_sb[:], in_=chunks[c])
-            if c == 0:
-                load_weight("wv", wv, slice(WV_SPLIT, DI))
             if c == WV_AFTER:
-                load_weight("wv", wv, slice(0, WV_SPLIT))
+                load_weight("wv", wv)
 
         ident = consts.tile([P, P], F32)
         make_identity(nc, ident[:])
@@ -366,29 +364,22 @@ def tile_hydraencoderlayer_pa_t_kernel(tc, x, wk, wv, out):
         for j in range(PAIR):
             regroup_tiles(0, slice(j, j + 1), banks[j], nc.scalar.copy)
             quantise_tiles(0, slice(j, j + 1))
-        regroup_x(1)
-        interleave_weight("wv", slice(WV_SPLIT, DI), nc.scalar.copy)
+        regroup_tiles(1, slice(0, PAIR), xt[1], nc.scalar.copy)
         pass_a(0, 0)
         pass_a(0, 1)
         quantise_x(1)
         transpose_x(2, new_xt(psum_v, "v_ps"))
         transpose_x(3, new_xt())
+        pass_a(1, 0)
         copy_a(0, 0)
         copy_a(0, 1, copy=nc.vector.tensor_copy)
-        pass_a(1, 0)
         regroup_tiles(2, slice(0, PAIR), xt[2], nc.scalar.copy)
-        square_sum(0, 0)
-        if ORDER == 0:
-            regroup_x(3)
-            quantise_x(2)
-            interleave_weight("wv", slice(0, WV_SPLIT), nc.vector.tensor_copy)
-        else:
-            interleave_weight("wv", slice(0, WV_SPLIT), nc.vector.tensor_copy)
-            regroup_x(3)
-            quantise_x(2)
+        regroup_x(3)
         transpose_x(4, new_xt())
-        if ORDER == 1:
-            quantise_weight("wv")
+        square_sum(0, 0)
+        quantise_x(2)
+        interleave_weight("wv", slice(0, WV_SPLIT), nc.vector.tensor_copy)
+        interleave_weight("wv", slice(WV_SPLIT, DI), nc.scalar.copy)
         quantise_x(3)
         tail = N_PAIRS - 3
         for n in range(1, tail):

@@ -101,7 +101,7 @@ def tile_hydraencoderlayer_pa_t_kernel(tc, x, wk, wv, out):
 
         ident = consts.tile([P, P], F32)
         make_identity(nc, ident[:])
-        out_cols = consts.tile([P, P], F32)
+        out_cols = consts.tile([P, 32], F32, align_bytes=64)
         nc.vector.memset(out_cols[:], 0.0)
         zeros = consts.tile([P, DI], BF16)
         nc.vector.memset(zeros[:], 0.0)
@@ -462,11 +462,9 @@ def tile_hydraencoderlayer_pa_t_kernel(tc, x, wk, wv, out):
             add_tokens(last, [1], range(first, first + step_blocks))
         add_partitions()
 
-        out_rows_ps = psum_t.tile([P, P], F32, name="xt")
-        nc.tensor.transpose(out_rows_ps[:], out_cols[:], ident[:])
-        out_rows = consts.tile([P, P], F32)
-        nc.vector.tensor_copy(out=out_rows[:], in_=out_rows_ps[:])
-        nc.sync.dma_start(
-            out=out.rearrange("b o (i e) -> (b o i) e", i=E_BLOCKS),
-            in_=out_rows[0 : BATCH * E_BLOCKS, :],
-        )
+        out_rows = consts.tile([P, 32], F32, align_bytes=64)
+        nc.vector.transpose(out=out_rows[:], in_=out_cols[:])
+        pieces = out.rearrange("b o (i g q) -> g (b o i) q", i=E_BLOCKS, q=32)
+        for g in range(4):
+            queue = nc.sync if g % 2 == 0 else nc.scalar
+            queue.dma_start(out=pieces[g], in_=out_rows[32 * g : 32 * g + BATCH * E_BLOCKS, :])

@@ -256,9 +256,9 @@ def tile_hydraencoderlayer_pa_t_kernel(tc, x, wk, wv, out):
                 prod[n] = work.tile([P, PAIR, DI], F32, name="prod")
             nc.vector.scalar_tensor_tensor(
                 out=prod[n][:, j, cols],
-                in0=a_sb[n, j][:, cols],
+                in0=v_ps[n, j][:, cols],
                 scalar=rnorm_of(n, j),
-                in1=v_ps[n, j][:, cols],
+                in1=a_sb[n, j][:, cols],
                 op0=ALU.mult,
                 op1=ALU.mult,
             )

@@ -10,49 +10,34 @@ U8 = mybir.dt.uint8
 FP8X4 = mybir.dt.float8_e4m3fn_x4
 ACT = mybir.ActivationFunctionType
 ALU = mybir.AluOpType
+AXIS = mybir.AxisListType
 
 P = 128
+QUADRANT = 32
 PACK = 4
 BATCH, TOKENS, D, DI = 4, 2048, 512, 512
 EPS = 1e-12
 WORDS = D // 2
 HALVES = WORDS // P
+E_BLOCKS = DI // P
 PAIR = 2
 CHUNK_TILES = 4
-CHUNKS_PER_BATCH = TOKENS // (CHUNK_TILES * P)
 PAIRS_PER_CHUNK = CHUNK_TILES // PAIR
-PAIRS_PER_BATCH = CHUNKS_PER_BATCH * PAIRS_PER_CHUNK
-N_PAIRS = BATCH * PAIRS_PER_BATCH
-N_CHUNKS = BATCH * CHUNKS_PER_BATCH
-W_SPLIT = 336
-E_BLOCKS = DI // P
+N_CHUNKS = BATCH * TOKENS // (CHUNK_TILES * P)
+N_PAIRS = N_CHUNKS * PAIRS_PER_CHUNK
+LAST = N_PAIRS - 1
 
+AHEAD = 3
 LAG = 3
 SUM_LAG = 2
-WV_AFTER = 1
-WV_STEP = 1
-WV_SPLIT = 320
-COPY_HEAD = 3
-GROUP = 4
-PAIRED = 8
-SINGLES = 0
-N_TILES = N_PAIRS * PAIR
-TAIL_VEC = 0
-ORDER = 0
-VEC_CLAMP = 2
-TAIL_SPLIT = 512
-LAST_PARTS = 2
-COPY_PHASE = 3
-COPY_FROM = 0
-RUN = 4
-WV_EARLY = 0
-A_BUFS = 10
-POOL_BLOCKS = 4
-POOL_EVERY = 1
-POOL_TAIL = 2
+GROUP_PAIRS = 2
+SINGLE_PAIRS = 4
+VECTOR_CLAMPS = 2
+
 COPY_EVERY = 4
-COPY_TAIL = 3
-X_BUFS = 8
+WK_SPLIT = 336
+WV_SPLIT = 320
+RUN = 4
 
 FLOPS = 2 * 2 * BATCH * TOKENS * D * DI
 
@@ -62,32 +47,29 @@ def tile_hydraencoderlayer_pa_t_kernel(tc, x, wk, wv, out):
     with ExitStack() as ctx:
         ctx.enter_context(tc.manual_schedule())
         consts = ctx.enter_context(tc.tile_pool(name="consts", bufs=1))
-        x_pool = ctx.enter_context(tc.tile_pool(name="x_pool", bufs=BATCH * CHUNKS_PER_BATCH))
-        stage = ctx.enter_context(tc.tile_pool(name="stage", bufs=3))
-        operands = ctx.enter_context(tc.tile_pool(name="operands", bufs=X_BUFS))
-        work = ctx.enter_context(tc.tile_pool(name="work", bufs=6))
+        x_pool = ctx.enter_context(tc.tile_pool(name="x_pool", bufs=N_CHUNKS))
+        stage = ctx.enter_context(tc.tile_pool(name="stage", bufs=AHEAD))
+        operands = ctx.enter_context(tc.tile_pool(name="operands", bufs=AHEAD + LAG + 2))
+        work = ctx.enter_context(tc.tile_pool(name="work", bufs=2 * (SUM_LAG + 1)))
         psum_t = ctx.enter_context(tc.psum_pool(name="psum_t", bufs=1))
         psum_a = ctx.enter_context(tc.psum_pool(name="psum_a", bufs=3))
         psum_v = ctx.enter_context(tc.psum_pool(name="psum_v", bufs=3))
         psum_s = ctx.enter_context(tc.psum_pool(name="psum_s", bufs=1))
+        on_vector = nc.vector.tensor_copy
+        on_scalar = nc.scalar.copy
 
         w_raw = {}
 
-        def load_weight(label, w, cols=slice(0, DI)):
-            if label not in w_raw:
-                w_raw[label] = consts.tile([P, PACK, DI], BF16, name="%s_raw" % label)
-            if cols.stop - cols.start == DI:
-                nc.sync.dma_start(
-                    out=w_raw[label][:].rearrange("q (u e) c -> q u (e c)", u=HALVES),
-                    in_=w.rearrange("(u q e) c -> q u (e c)", u=HALVES, e=2),
-                )
-                return
-            rows = w.rearrange("(u q e) c -> u q e c", u=HALVES, e=2)
-            for u in range(HALVES):
-                nc.sync.dma_start(out=w_raw[label][:, 2 * u : 2 * u + 2, cols], in_=rows[u][:, :, cols])
+        def load_weight(label, w):
+            w_raw[label] = consts.tile([P, PACK, DI], BF16, name="%s_raw" % label)
+            nc.sync.dma_start(
+                out=w_raw[label][:].rearrange("q (u e) c -> q u (e c)", u=HALVES),
+                in_=w.rearrange("(u q e) c -> q u (e c)", u=HALVES, e=2),
+            )
+
         load_weight("wk", wk)
-        x_chunks = []
         chunks = x.rearrange("b (q c t) k -> c (b q) (t k)", c=N_CHUNKS, t=CHUNK_TILES)
+        x_chunks = []
         for c in range(N_CHUNKS):
             x_sb = x_pool.tile([P, CHUNK_TILES * D], BF16)
             x_chunks.append(x_sb)
@@ -96,46 +78,46 @@ def tile_hydraencoderlayer_pa_t_kernel(tc, x, wk, wv, out):
                     nc.sync.dma_start(out=x_sb[:, first:stop], in_=chunks[c][:, first:stop])
             else:
                 nc.sync.dma_start(out=x_sb[:], in_=chunks[c])
-            if c == WV_AFTER:
+            if c == 1:
                 load_weight("wv", wv)
 
         ident = consts.tile([P, P], F32)
         make_identity(nc, ident[:])
-        out_cols = consts.tile([P, 32], F32, align_bytes=64)
+        out_cols = consts.tile([P, QUADRANT], F32, align_bytes=64)
         nc.vector.memset(out_cols[:], 0.0)
         zeros = consts.tile([P, DI], BF16)
         nc.vector.memset(zeros[:], 0.0)
         table_load = consts.tile([P, 1], F32)
         nc.scalar.activation(out=table_load[:], in_=zeros[:, :1], func=ACT.Abs_reciprocal_sqrt, bias=1.0)
-
         floored = {}
-        for n in range(N_PAIRS - VEC_CLAMP, N_PAIRS):
-            floored[n * PAIR] = consts.tile([P, PAIR, 2], F32, name="floored_%d" % n)
-            nc.vector.tensor_scalar(out=floored[n * PAIR][:].rearrange("p a b -> p (a b)"), in0=out_cols[:, : 2 * PAIR],
-                                    scalar1=EPS * EPS, scalar2=None, op0=ALU.add)
-
-        w_grouped = {}
-        w_codes = {}
-        w_scales = {}
-        for label in ("wk", "wv"):
-            w_grouped[label] = consts.tile(
-                [P, DI, PACK], BF16, name="%s_grouped" % label, align_bytes=64
+        for n in range(N_PAIRS - VECTOR_CLAMPS, N_PAIRS):
+            floored[n] = consts.tile([P, PAIR, 2], F32, name="floored_%d" % n)
+            nc.vector.tensor_scalar(
+                out=floored[n][:].rearrange("p j s -> p (j s)"),
+                in0=out_cols[:, : PAIR * 2],
+                scalar1=EPS * EPS,
+                scalar2=None,
+                op0=ALU.add,
             )
+
+        w_grouped, w_codes, w_scales = {}, {}, {}
+        for label in ("wk", "wv"):
+            w_grouped[label] = consts.tile([P, DI, PACK], BF16, name="%s_grouped" % label, align_bytes=64)
             w_codes[label] = consts.tile([P, DI], U32, name="%s_codes" % label, align_bytes=256)
             w_scales[label] = consts.tile([P, DI], U8, name="%s_scales" % label, align_bytes=256)
 
-        def quantise_weight(label, cols=slice(0, DI)):
-            nc.vector.quantize_mx(
-                out=w_codes[label][:, cols].bitcast(FP8X4),
-                scales=w_scales[label][:, cols],
-                in_=w_grouped[label][:, cols, :].rearrange("q c t -> q (c t)"),
-            )
-
-        def interleave_weight(label, cols, copy):
+        def interleave_weight(label, first, stop, copy):
             by_column = w_raw[label][:].rearrange("q t (c i) -> q c t i", i=RUN)
-            grouped_w = w_grouped[label][:].rearrange("q (c i) t -> q c t i", i=RUN)
-            runs = slice(cols.start // RUN, cols.stop // RUN)
-            copy(out=grouped_w[:, runs], in_=by_column[:, runs])
+            side_by_side = w_grouped[label][:].rearrange("q (c i) t -> q c t i", i=RUN)
+            runs = slice(first // RUN, stop // RUN)
+            copy(out=side_by_side[:, runs], in_=by_column[:, runs])
+
+        def quantise_weight(label, first, stop):
+            nc.vector.quantize_mx(
+                out=w_codes[label][:, first:stop].bitcast(FP8X4),
+                scales=w_scales[label][:, first:stop],
+                in_=w_grouped[label][:, first:stop, :].rearrange("q c t -> q (c t)"),
+            )
 
         def warm_up(count):
             bank = psum_s.tile([P, DI], F32, name="token_sums")
@@ -145,7 +127,10 @@ def tile_hydraencoderlayer_pa_t_kernel(tc, x, wk, wv, out):
         xt, grouped, x_codes, x_scales = {}, {}, {}, {}
         a_ps, v_ps, a_sb = {}, {}, {}
         norm2, clamped, rnorm = {}, {}, {}
-        prod, pair_sum, token_sums = {}, {}, {}
+        prod, pair_sum, token_sums = {}, {}, []
+
+        def new_xt(pool=psum_t, name="xt"):
+            return pool.tile([P, PAIR, HALVES, P], F32, name=name)
 
         def transpose_tile(bank, n, j):
             x_words = x_chunks[n // PAIRS_PER_CHUNK][:].bitcast(F32)
@@ -153,9 +138,6 @@ def tile_hydraencoderlayer_pa_t_kernel(tc, x, wk, wv, out):
             for u in range(HALVES):
                 w0 = first_word + u * P
                 nc.tensor.transpose(bank[:, j, u, :], x_words[:, w0 : w0 + P], ident[:])
-
-        def new_xt(pool=psum_t, name="xt"):
-            return pool.tile([P, PAIR, HALVES, P], F32, name=name)
 
         def transpose_x(n, bank):
             xt[n] = bank
@@ -171,8 +153,8 @@ def tile_hydraencoderlayer_pa_t_kernel(tc, x, wk, wv, out):
                 in_=bank[:].rearrange("p j u r -> p j r u")[:, tiles, :, :],
             )
 
-        def regroup_x(n):
-            regroup_tiles(n, slice(0, PAIR), xt[n], nc.vector.tensor_copy)
+        def regroup_x(n, copy=on_vector):
+            regroup_tiles(n, slice(0, PAIR), xt[n], copy)
 
         def quantise_tiles(n, tiles):
             if n not in x_codes:
@@ -208,163 +190,134 @@ def tile_hydraencoderlayer_pa_t_kernel(tc, x, wk, wv, out):
             v_ps[n, j] = pool.tile([P, DI], F32, name=name)
             mx_pass(v_ps[n, j], n, j, "wv")
 
-        def copy_a(n, j, copy=nc.scalar.copy, cols=slice(0, DI)):
-            if (n, j) not in a_sb:
-                a_sb[n, j] = work.tile([P, DI], F32, name="a_sb", bufs=A_BUFS)
-            copy(out=a_sb[n, j][:, cols], in_=a_ps[n, j][:, cols])
+        def copy_a(n, j, copy=on_scalar):
+            a_sb[n, j] = work.tile([P, DI], F32, name="a_sb", bufs=PAIR * (LAG + 2))
+            copy(out=a_sb[n, j][:], in_=a_ps[n, j][:])
 
-        def group_of(t):
-            size = GROUP if t < N_TILES - PAIRED else (PAIR if t < N_TILES - SINGLES else 1)
-            return t - t % size, size
-
-        def square_sum(n, j, source=a_sb):
-            t = n * PAIR + j
-            first, count = group_of(t)
-            if first in floored:
-                column = floored[first][:, t - first, 0:1]
-            else:
-                if first not in norm2:
-                    norm2[first] = work.tile([P, count], F32, name="norm2")
-                column = norm2[first][:, t - first : t - first + 1]
-            squares = work.tile([P, DI], BF16, name="squares")
-            nc.scalar.activation(out=squares[:], in_=source[n, j][:], func=ACT.Square, accum_out=column)
+        def group_of(n):
+            count = GROUP_PAIRS if n < N_PAIRS - SINGLE_PAIRS else 1
+            return n - n % count, count
 
         def closes_group(n):
-            return live(n) and sum(group_of(n * PAIR + 1)) == (n + 1) * PAIR
+            return n >= 0 and sum(group_of(n)) == n + 1
 
-        def clamp_norm(n, j=1):
-            first, count = group_of(n * PAIR + j)
-            clamped[first] = work.tile([P, count], F32, name="clamped")
+        def square_sum(n, j, source=a_sb):
+            first, count = group_of(n)
+            col = (n - first) * PAIR + j
             if first in floored:
-                nc.vector.tensor_reduce(out=clamped[first][:], in_=floored[first][:], axis=mybir.AxisListType.X, op=ALU.max)
+                total = floored[first][:, col, 0:1]
+            else:
+                if first not in norm2:
+                    norm2[first] = work.tile([P, count * PAIR], F32, name="norm2")
+                total = norm2[first][:, col : col + 1]
+            squares = work.tile([P, DI], BF16, name="squares")
+            nc.scalar.activation(out=squares[:], in_=source[n, j][:], func=ACT.Square, accum_out=total)
+
+        def clamp_norms(n):
+            first, count = group_of(n)
+            clamped[first] = work.tile([P, count * PAIR], F32, name="clamped")
+            if first in floored:
+                nc.vector.tensor_reduce(out=clamped[first][:], in_=floored[first][:], axis=AXIS.X, op=ALU.max)
             else:
                 nc.scalar.activation(out=clamped[first][:], in_=norm2[first][:], func=ACT.Relu, bias=-EPS * EPS)
 
-        def invert_norm(n, j=1):
-            first, count = group_of(n * PAIR + j)
-            rnorm[first] = work.tile([P, count], F32, name="rnorm")
-            nc.scalar.activation(out=rnorm[first][:], in_=clamped[first][:], func=ACT.Abs_reciprocal_sqrt,
-                                 bias=(0.0 if first in floored else EPS * EPS))
-
-        def rnorm_of(n, j):
-            t = n * PAIR + j
-            first, count = group_of(t)
-            return rnorm[first][:, t - first : t - first + 1]
+        def invert_norms(n):
+            first, count = group_of(n)
+            rnorm[first] = work.tile([P, count * PAIR], F32, name="rnorm")
+            nc.scalar.activation(
+                out=rnorm[first][:],
+                in_=clamped[first][:],
+                func=ACT.Abs_reciprocal_sqrt,
+                bias=(0.0 if first in floored else EPS * EPS),
+            )
 
         def product(n, j, cols=slice(0, DI)):
             if n not in prod:
                 prod[n] = work.tile([P, PAIR, DI], F32, name="prod")
+            first, count = group_of(n)
+            col = (n - first) * PAIR + j
             nc.vector.scalar_tensor_tensor(
                 out=prod[n][:, j, cols],
                 in0=v_ps[n, j][:, cols],
-                scalar=rnorm_of(n, j),
+                scalar=rnorm[first][:, col : col + 1],
                 in1=a_sb[n, j][:, cols],
                 op0=ALU.mult,
                 op1=ALU.mult,
             )
 
         def add_pair(n):
-            if POOL_BLOCKS == 0 or n >= N_PAIRS - POOL_TAIL or n % POOL_EVERY:
-                return
-            cols = POOL_BLOCKS * P
             pair_sum[n] = work.tile([P, DI], F32, name="pair_sum")
-            nc.gpsimd.tensor_tensor(
-                out=pair_sum[n][:, :cols], in0=prod[n][:, 0, :cols], in1=prod[n][:, 1, :cols], op=ALU.add
-            )
+            nc.gpsimd.tensor_tensor(out=pair_sum[n][:], in0=prod[n][:, 0, :], in1=prod[n][:, 1, :], op=ALU.add)
 
-        def add_tokens(n, tiles=range(PAIR), col_blocks=range(E_BLOCKS)):
-            b, q = 0, n
-            if q == 0:
-                token_sums[b] = psum_s.tile([P, E_BLOCKS, P], F32, name="token_sums")
-            blocks = []
-            for j in tiles:
-                for i in col_blocks:
-                    cols = slice(i * P, (i + 1) * P)
-                    if n not in pair_sum or i >= POOL_BLOCKS:
-                        blocks.append((i, prod[n][:, j, cols]))
-                    elif j == 0:
-                        blocks.append((i, pair_sum[n][:, cols]))
-            for k, (i, block) in enumerate(blocks):
+        def add_tokens(source, blocks=range(E_BLOCKS), closes=False):
+            opens = not token_sums
+            if opens:
+                token_sums.append(psum_s.tile([P, E_BLOCKS, P], F32, name="token_sums"))
+            for i in blocks:
                 nc.tensor.matmul(
-                    out=token_sums[b][:, i, :],
-                    lhsT=block,
+                    out=token_sums[0][:, i, :],
+                    lhsT=source[:, i * P : (i + 1) * P],
                     rhs=ident[:],
                     is_transpose=True,
-                    start=(q == 0 and k == 0),
-                    stop=(q == N_PAIRS - 1 and PAIR - 1 in tiles and i == E_BLOCKS - 1),
+                    start=(opens and i == 0),
+                    stop=(closes and i == E_BLOCKS - 1),
                 )
-
-        def add_partitions():
-            nc.vector.tensor_reduce(
-                out=out_cols[:, : BATCH * E_BLOCKS].rearrange("e (b i) -> e i b", b=BATCH),
-                in_=token_sums[0][:].rearrange("e i (b q) -> e i b q", b=BATCH),
-                axis=mybir.AxisListType.X,
-                op=ALU.add,
-            )
-
-        def live(n):
-            return 0 <= n < N_PAIRS
-
-        def on_vector(n, j):
-            if n < COPY_HEAD:
-                return j == 1
-            return j == 1 and n % COPY_EVERY == COPY_PHASE and COPY_FROM <= n < N_PAIRS - COPY_TAIL
 
         def step(n):
             m = n - LAG
-            s = m - SUM_LAG
-            regroup_x(n + 3)
+            vector_copies = m < 0 or n % COPY_EVERY == COPY_EVERY - 1
+            regroup_x(n + AHEAD)
             pass_a(n, 1)
-            if on_vector(n, 1):
-                copy_a(n, 1, copy=nc.vector.tensor_copy)
-            if live(m):
+            if vector_copies:
+                copy_a(n, 1, on_vector)
+            if m >= 0:
                 pass_v(m, 1)
             pass_a(n + 1, 0)
             copy_a(n, 0)
-            if closes_group(n - 2) and on_vector(n - 1, 1):
-                invert_norm(n - 2)
+            if closes_group(n - 2) and group_of(n - 2)[0] not in rnorm:
+                invert_norms(n - 2)
             square_sum(n - 1, 1)
-            if on_vector(n, 1):
+            if vector_copies:
                 square_sum(n, 0)
                 if closes_group(n - 1):
-                    clamp_norm(n - 1)
+                    clamp_norms(n - 1)
             else:
                 copy_a(n, 1)
                 if closes_group(n - 1):
-                    clamp_norm(n - 1)
+                    clamp_norms(n - 1)
                 square_sum(n, 0)
                 if closes_group(n - 1):
-                    invert_norm(n - 1)
-            if live(m):
+                    invert_norms(n - 1)
+            if m >= 0:
                 product(m, 0)
-            if n == WV_STEP and ORDER == 0:
-                quantise_weight("wv")
-            if live(m + 1):
+            if m + 1 == -1:
+                quantise_weight("wv", 0, DI)
+            if m + 1 >= 0:
                 pass_v(m + 1, 0)
-            if live(s):
-                add_tokens(s)
-            if live(n + 4):
-                transpose_x(n + 4, new_xt())
-            if live(m):
+            if m >= SUM_LAG:
+                add_tokens(pair_sum[m - SUM_LAG])
+            if n + AHEAD < LAST:
+                transpose_x(n + AHEAD + 1, new_xt())
+            if m >= 0:
                 product(m, 1)
                 add_pair(m)
-            quantise_x(n + 3)
+            quantise_x(n + AHEAD)
 
         warm_up(6)
-        interleave_weight("wk", slice(0, DI // 2), nc.vector.tensor_copy)
-        interleave_weight("wk", slice(DI // 2, W_SPLIT), nc.vector.tensor_copy)
-        interleave_weight("wk", slice(W_SPLIT, DI), nc.scalar.copy)
-        quantise_weight("wk", slice(0, DI // 2))
-        quantise_weight("wk", slice(DI // 2, DI))
+        interleave_weight("wk", 0, DI // 2, on_vector)
+        interleave_weight("wk", DI // 2, WK_SPLIT, on_vector)
+        interleave_weight("wk", WK_SPLIT, DI, on_scalar)
+        quantise_weight("wk", 0, DI // 2)
+        quantise_weight("wk", DI // 2, DI)
         banks = [new_xt(), new_xt(psum_v, "v_ps")]
         for j in range(PAIR):
             transpose_tile(banks[j], 0, j)
         transpose_x(1, new_xt(psum_v, "v_ps"))
         warm_up(1)
         for j in range(PAIR):
-            regroup_tiles(0, slice(j, j + 1), banks[j], nc.scalar.copy)
+            regroup_tiles(0, slice(j, j + 1), banks[j], on_scalar)
             quantise_tiles(0, slice(j, j + 1))
-        regroup_tiles(1, slice(0, PAIR), xt[1], nc.scalar.copy)
+        regroup_x(1, on_scalar)
         pass_a(0, 0)
         pass_a(0, 1)
         quantise_x(1)
@@ -372,99 +325,100 @@ def tile_hydraencoderlayer_pa_t_kernel(tc, x, wk, wv, out):
         transpose_x(3, new_xt())
         pass_a(1, 0)
         copy_a(0, 0)
-        copy_a(0, 1, copy=nc.vector.tensor_copy)
-        regroup_tiles(2, slice(0, PAIR), xt[2], nc.scalar.copy)
+        copy_a(0, 1, on_vector)
+        regroup_x(2, on_scalar)
         regroup_x(3)
         transpose_x(4, new_xt())
         square_sum(0, 0)
         quantise_x(2)
-        interleave_weight("wv", slice(0, WV_SPLIT), nc.vector.tensor_copy)
-        interleave_weight("wv", slice(WV_SPLIT, DI), nc.scalar.copy)
+        interleave_weight("wv", 0, WV_SPLIT, on_vector)
+        interleave_weight("wv", WV_SPLIT, DI, on_scalar)
         quantise_x(3)
-        tail = N_PAIRS - 3
-        for n in range(1, tail):
+
+        for n in range(1, N_PAIRS - AHEAD):
             step(n)
 
-        vec = nc.vector.tensor_copy
-        n = tail
-        last = N_PAIRS - 1
+        n = LAST - 2
         pass_a(n, 1)
         pass_v(n - 3, 1)
         pass_a(n + 1, 0)
         copy_a(n, 0)
-        copy_a(n, 1, vec, slice(0, TAIL_SPLIT))
+        copy_a(n, 1, on_vector)
         square_sum(n - 1, 1)
-        if TAIL_SPLIT < DI:
-            copy_a(n, 1, cols=slice(TAIL_SPLIT, DI))
-            clamp_norm(n - 1)
-            square_sum(n, 0)
-        else:
-            square_sum(n, 0)
-            clamp_norm(n - 1)
+        square_sum(n, 0)
+        clamp_norms(n - 1)
         product(n - 3, 0)
         pass_v(n - 2, 0)
         pass_a(n + 1, 1)
-        add_tokens(n - 5)
+        add_tokens(pair_sum[n - 5])
         product(n - 3, 1)
         add_pair(n - 3)
         pass_v(n - 2, 1)
-        copy_a(n + 1, 0)
-        invert_norm(n - 1)
+
+        n = LAST - 1
+        copy_a(n, 0)
+        invert_norms(n - 2)
+        square_sum(n - 1, 1)
+        product(n - 3, 0)
+        pass_a(LAST, 0)
+        pass_v(n - 2, 0)
+        copy_a(n, 1)
+        clamp_norms(n - 1)
+        square_sum(n, 0)
+        invert_norms(n - 1)
+        add_tokens(pair_sum[n - 5])
+        product(n - 3, 1)
+        add_pair(n - 3)
+        pass_v(n - 2, 1)
+        pass_a(LAST, 1)
         square_sum(n, 1)
         product(n - 2, 0)
-        pass_a(last, 0)
         pass_v(n - 1, 0)
-        if TAIL_VEC:
-            copy_a(n + 1, 1, copy=vec)
-        else:
-            copy_a(n + 1, 1)
-        clamp_norm(n)
-        square_sum(n + 1, 0)
-        invert_norm(n)
-        add_tokens(n - 4)
+        add_tokens(pair_sum[n - 4])
         product(n - 2, 1)
         add_pair(n - 2)
         pass_v(n - 1, 1)
-        pass_a(last, 1)
-        square_sum(n + 1, 1)
-        product(n - 1, 0)
-        pass_v(n, 0)
-        add_tokens(n - 3)
-        product(n - 1, 1)
-        add_pair(n - 1)
-        pass_v(n, 1)
-        pass_v(last, 0, psum_t, "xt")
-        square_sum(last, 0, a_ps)
-        product(n, 0)
-        clamp_norm(n + 1)
-        invert_norm(n + 1)
-        square_sum(last, 1, a_ps)
-        copy_a(last, 0)
-        pass_v(n + 1, 0)
-        pass_v(n + 1, 1, psum_a, "a_ps")
-        add_tokens(n - 2)
-        product(n, 1)
-        add_pair(n)
-        pass_v(last, 1)
-        add_tokens(n - 1)
-        for m, j in ((n + 1, 0), (n + 1, 1), (last, 0)):
-            product(m, j)
-            if (m, j) == (n + 1, 0):
-                clamp_norm(last)
-                invert_norm(last)
-                copy_a(last, 1)
-            if (m, j) == (last, 0):
-                add_tokens(n)
-            add_tokens(m, [j])
-        step_blocks = E_BLOCKS // LAST_PARTS
-        for first in range(0, E_BLOCKS, step_blocks):
-            product(last, 1, slice(first * P, (first + step_blocks) * P))
-            add_tokens(last, [1], range(first, first + step_blocks))
-        add_partitions()
 
-        out_rows = consts.tile([P, 32], F32, align_bytes=64)
+        n = LAST
+        pass_v(n, 0, psum_t, "xt")
+        square_sum(n, 0, a_ps)
+        product(n - 2, 0)
+        clamp_norms(n - 1)
+        invert_norms(n - 1)
+        square_sum(n, 1, a_ps)
+        copy_a(n, 0)
+        pass_v(n - 1, 0)
+        pass_v(n - 1, 1, psum_a, "a_ps")
+        add_tokens(pair_sum[n - 4])
+        product(n - 2, 1)
+        add_pair(n - 2)
+        pass_v(n, 1)
+        add_tokens(pair_sum[n - 3])
+        product(n - 1, 0)
+        clamp_norms(n)
+        invert_norms(n)
+        copy_a(n, 1)
+        add_tokens(prod[n - 1][:, 0, :])
+        product(n - 1, 1)
+        add_tokens(prod[n - 1][:, 1, :])
+        product(n, 0)
+        add_tokens(pair_sum[n - 2])
+        add_tokens(prod[n][:, 0, :])
+        for first in range(0, E_BLOCKS, E_BLOCKS // 2):
+            blocks = range(first, first + E_BLOCKS // 2)
+            product(n, 1, slice(blocks.start * P, blocks.stop * P))
+            add_tokens(prod[n][:, 1, :], blocks, closes=True)
+
+        nc.vector.tensor_reduce(
+            out=out_cols[:, : BATCH * E_BLOCKS].rearrange("e (b i) -> e i b", b=BATCH),
+            in_=token_sums[0][:].rearrange("e i (b q) -> e i b q", b=BATCH),
+            axis=AXIS.X,
+            op=ALU.add,
+        )
+        out_rows = consts.tile([P, QUADRANT], F32, align_bytes=64)
         nc.vector.transpose(out=out_rows[:], in_=out_cols[:])
-        pieces = out.rearrange("b o (i g q) -> g (b o i) q", i=E_BLOCKS, q=32)
-        for g in range(4):
+        pieces = out.rearrange("b o (i g q) -> g (b o i) q", i=E_BLOCKS, q=QUADRANT)
+        for g in range(P // QUADRANT):
             queue = nc.sync if g % 2 == 0 else nc.scalar
-            queue.dma_start(out=pieces[g], in_=out_rows[32 * g : 32 * g + BATCH * E_BLOCKS, :])
+            first = g * QUADRANT
+            queue.dma_start(out=pieces[g], in_=out_rows[first : first + BATCH * E_BLOCKS, :])

@@ -32,7 +32,7 @@ LAG = 3
 SUM_LAG = 2
 GROUP_PAIRS = 2
 SINGLE_PAIRS = 4
-VECTOR_CLAMPS = 2
+VECTOR_CLAMPS = 0
 
 COPY_EVERY = 4
 WK_SPLIT = 336
@@ -384,9 +384,12 @@ def tile_hydraencoderlayer_pa_t_kernel(tc, x, wk, wv, out):
         square_sum(n, 0, a_ps)
         product(n - 2, 0)
         clamp_norms(n - 1)
-        invert_norms(n - 1)
         square_sum(n, 1, a_ps)
+        invert_norms(n - 1)
+        clamp_norms(n)
         copy_a(n, 0)
+        invert_norms(n)
+        copy_a(n, 1)
         pass_v(n - 1, 0)
         pass_v(n - 1, 1, psum_a, "a_ps")
         add_tokens(pair_sum[n - 4])
@@ -395,9 +398,6 @@ def tile_hydraencoderlayer_pa_t_kernel(tc, x, wk, wv, out):
         pass_v(n, 1)
         add_tokens(pair_sum[n - 3])
         product(n - 1, 0)
-        clamp_norms(n)
-        invert_norms(n)
-        copy_a(n, 1)
         add_tokens(prod[n - 1][:, 0, :])
         product(n - 1, 1)
         add_tokens(prod[n - 1][:, 1, :])

@@ -404,10 +404,8 @@ def tile_hydraencoderlayer_pa_t_kernel(tc, x, wk, wv, out):
         product(n, 0)
         add_tokens(pair_sum[n - 2])
         add_tokens(prod[n][:, 0, :])
-        for first in range(0, E_BLOCKS, E_BLOCKS // 2):
-            blocks = range(first, first + E_BLOCKS // 2)
-            product(n, 1, slice(blocks.start * P, blocks.stop * P))
-            add_tokens(prod[n][:, 1, :], blocks, closes=True)
+        product(n, 1)
+        add_tokens(prod[n][:, 1, :], closes=True)
 
         nc.vector.tensor_reduce(
             out=out_cols[:, : BATCH * E_BLOCKS].rearrange("e (b i) -> e i b", b=BATCH),

@@ -32,7 +32,6 @@ LAG = 3
 SUM_LAG = 2
 GROUP_PAIRS = 2
 SINGLE_PAIRS = 4
-VECTOR_CLAMPS = 0
 
 COPY_EVERY = 4
 WK_SPLIT = 336
@@ -89,16 +88,6 @@ def tile_hydraencoderlayer_pa_t_kernel(tc, x, wk, wv, out):
         nc.vector.memset(zeros[:], 0.0)
         table_load = consts.tile([P, 1], F32)
         nc.scalar.activation(out=table_load[:], in_=zeros[:, :1], func=ACT.Abs_reciprocal_sqrt, bias=1.0)
-        floored = {}
-        for n in range(N_PAIRS - VECTOR_CLAMPS, N_PAIRS):
-            floored[n] = consts.tile([P, PAIR, 2], F32, name="floored_%d" % n)
-            nc.vector.tensor_scalar(
-                out=floored[n][:].rearrange("p j s -> p (j s)"),
-                in0=out_cols[:, : PAIR * 2],
-                scalar1=EPS * EPS,
-                scalar2=None,
-                op0=ALU.add,
-            )
 
         w_grouped, w_codes, w_scales = {}, {}, {}
         for label in ("wk", "wv"):
@@ -191,7 +180,7 @@ def tile_hydraencoderlayer_pa_t_kernel(tc, x, wk, wv, out):
             mx_pass(v_ps[n, j], n, j, "wv")
 
         def copy_a(n, j, copy=on_scalar):
-            a_sb[n, j] = work.tile([P, DI], F32, name="a_sb", bufs=PAIR * (LAG + 2))
+            a_sb[n, j] = work.tile([P, DI], F32, name="a_sb", bufs=PAIR * (LAG + 4))
             copy(out=a_sb[n, j][:], in_=a_ps[n, j][:])
 
         def group_of(n):
@@ -204,22 +193,16 @@ def tile_hydraencoderlayer_pa_t_kernel(tc, x, wk, wv, out):
         def square_sum(n, j, source=a_sb):
             first, count = group_of(n)
             col = (n - first) * PAIR + j
-            if first in floored:
-                total = floored[first][:, col, 0:1]
-            else:
-                if first not in norm2:
-                    norm2[first] = work.tile([P, count * PAIR], F32, name="norm2")
-                total = norm2[first][:, col : col + 1]
+            if first not in norm2:
+                norm2[first] = work.tile([P, count * PAIR], F32, name="norm2")
+            total = norm2[first][:, col : col + 1]
             squares = work.tile([P, DI], BF16, name="squares")
             nc.scalar.activation(out=squares[:], in_=source[n, j][:], func=ACT.Square, accum_out=total)
 
         def clamp_norms(n):
             first, count = group_of(n)
             clamped[first] = work.tile([P, count * PAIR], F32, name="clamped")
-            if first in floored:
-                nc.vector.tensor_reduce(out=clamped[first][:], in_=floored[first][:], axis=AXIS.X, op=ALU.max)
-            else:
-                nc.scalar.activation(out=clamped[first][:], in_=norm2[first][:], func=ACT.Relu, bias=-EPS * EPS)
+            nc.scalar.activation(out=clamped[first][:], in_=norm2[first][:], func=ACT.Relu, bias=-EPS * EPS)
 
         def invert_norms(n):
             first, count = group_of(n)
@@ -228,19 +211,19 @@ def tile_hydraencoderlayer_pa_t_kernel(tc, x, wk, wv, out):
                 out=rnorm[first][:],
                 in_=clamped[first][:],
                 func=ACT.Abs_reciprocal_sqrt,
-                bias=(0.0 if first in floored else EPS * EPS),
+                bias=EPS * EPS,
             )
 
-        def product(n, j, cols=slice(0, DI)):
+        def product(n, j):
             if n not in prod:
                 prod[n] = work.tile([P, PAIR, DI], F32, name="prod")
             first, count = group_of(n)
             col = (n - first) * PAIR + j
             nc.vector.scalar_tensor_tensor(
-                out=prod[n][:, j, cols],
-                in0=v_ps[n, j][:, cols],
+                out=prod[n][:, j, :],
+                in0=v_ps[n, j][:],
                 scalar=rnorm[first][:, col : col + 1],
-                in1=a_sb[n, j][:, cols],
+                in1=a_sb[n, j][:],
                 op0=ALU.mult,
                 op1=ALU.mult,
             )
@@ -249,11 +232,11 @@ def tile_hydraencoderlayer_pa_t_kernel(tc, x, wk, wv, out):
             pair_sum[n] = work.tile([P, DI], F32, name="pair_sum")
             nc.gpsimd.tensor_tensor(out=pair_sum[n][:], in0=prod[n][:, 0, :], in1=prod[n][:, 1, :], op=ALU.add)
 
-        def add_tokens(source, blocks=range(E_BLOCKS), closes=False):
+        def add_tokens(source, closes=False):
             opens = not token_sums
             if opens:
                 token_sums.append(psum_s.tile([P, E_BLOCKS, P], F32, name="token_sums"))
-            for i in blocks:
+            for i in range(E_BLOCKS):
                 nc.tensor.matmul(
                     out=token_sums[0][:, i, :],
                     lhsT=source[:, i * P : (i + 1) * P],

@@ -30,6 +30,7 @@ LAST = N_PAIRS - 1
 AHEAD = 3
 LAG = 3
 SUM_LAG = 2
+SPARE_PAIRS = 4
 GROUP_PAIRS = 2
 SINGLE_PAIRS = 4
 
@@ -37,6 +38,9 @@ COPY_EVERY = 4
 WK_SPLIT = 336
 WV_SPLIT = 320
 RUN = 4
+
+RESULT_BANKS = 3
+WARM_UP = 6
 
 FLOPS = 2 * 2 * BATCH * TOKENS * D * DI
 
@@ -51,8 +55,8 @@ def tile_hydraencoderlayer_pa_t_kernel(tc, x, wk, wv, out):
         operands = ctx.enter_context(tc.tile_pool(name="operands", bufs=AHEAD + LAG + 2))
         work = ctx.enter_context(tc.tile_pool(name="work", bufs=2 * (SUM_LAG + 1)))
         psum_t = ctx.enter_context(tc.psum_pool(name="psum_t", bufs=1))
-        psum_a = ctx.enter_context(tc.psum_pool(name="psum_a", bufs=3))
-        psum_v = ctx.enter_context(tc.psum_pool(name="psum_v", bufs=3))
+        psum_a = ctx.enter_context(tc.psum_pool(name="psum_a", bufs=RESULT_BANKS))
+        psum_v = ctx.enter_context(tc.psum_pool(name="psum_v", bufs=RESULT_BANKS))
         psum_s = ctx.enter_context(tc.psum_pool(name="psum_s", bufs=1))
         on_vector = nc.vector.tensor_copy
         on_scalar = nc.scalar.copy
@@ -73,8 +77,8 @@ def tile_hydraencoderlayer_pa_t_kernel(tc, x, wk, wv, out):
             x_sb = x_pool.tile([P, CHUNK_TILES * D], BF16)
             x_chunks.append(x_sb)
             if c == 0:
-                for first, stop in ((0, D), (D, PAIR * D), (PAIR * D, CHUNK_TILES * D)):
-                    nc.sync.dma_start(out=x_sb[:, first:stop], in_=chunks[c][:, first:stop])
+                for part in (slice(0, D), slice(D, PAIR * D), slice(PAIR * D, CHUNK_TILES * D)):
+                    nc.sync.dma_start(out=x_sb[:, part], in_=chunks[c][:, part])
             else:
                 nc.sync.dma_start(out=x_sb[:], in_=chunks[c])
             if c == 1:
@@ -95,22 +99,22 @@ def tile_hydraencoderlayer_pa_t_kernel(tc, x, wk, wv, out):
             w_codes[label] = consts.tile([P, DI], U32, name="%s_codes" % label, align_bytes=256)
             w_scales[label] = consts.tile([P, DI], U8, name="%s_scales" % label, align_bytes=256)
 
-        def interleave_weight(label, first, stop, copy):
+        def interleave_weight(label, cols, copy):
             by_column = w_raw[label][:].rearrange("q t (c i) -> q c t i", i=RUN)
             side_by_side = w_grouped[label][:].rearrange("q (c i) t -> q c t i", i=RUN)
-            runs = slice(first // RUN, stop // RUN)
+            runs = slice(cols.start // RUN, cols.stop // RUN)
             copy(out=side_by_side[:, runs], in_=by_column[:, runs])
 
-        def quantise_weight(label, first, stop):
+        def quantise_weight(label, cols):
             nc.vector.quantize_mx(
-                out=w_codes[label][:, first:stop].bitcast(FP8X4),
-                scales=w_scales[label][:, first:stop],
-                in_=w_grouped[label][:, first:stop, :].rearrange("q c t -> q (c t)"),
+                out=w_codes[label][:, cols].bitcast(FP8X4),
+                scales=w_scales[label][:, cols],
+                in_=w_grouped[label][:, cols, :].rearrange("q c t -> q (c t)"),
             )
 
-        def warm_up(count):
+        def warm_up():
             bank = psum_s.tile([P, DI], F32, name="token_sums")
-            for k in range(count):
+            for _ in range(WARM_UP):
                 nc.tensor.matmul(out=bank[:], lhsT=zeros[:, :P], rhs=zeros[:], start=True, stop=True)
 
         xt, grouped, x_codes, x_scales = {}, {}, {}, {}
@@ -180,7 +184,7 @@ def tile_hydraencoderlayer_pa_t_kernel(tc, x, wk, wv, out):
             mx_pass(v_ps[n, j], n, j, "wv")
 
         def copy_a(n, j, copy=on_scalar):
-            a_sb[n, j] = work.tile([P, DI], F32, name="a_sb", bufs=PAIR * (LAG + 4))
+            a_sb[n, j] = work.tile([P, DI], F32, name="a_sb", bufs=PAIR * (LAG + SPARE_PAIRS))
             copy(out=a_sb[n, j][:], in_=a_ps[n, j][:])
 
         def group_of(n):
@@ -230,7 +234,9 @@ def tile_hydraencoderlayer_pa_t_kernel(tc, x, wk, wv, out):
 
         def add_pair(n):
             pair_sum[n] = work.tile([P, DI], F32, name="pair_sum")
-            nc.gpsimd.tensor_tensor(out=pair_sum[n][:], in0=prod[n][:, 0, :], in1=prod[n][:, 1, :], op=ALU.add)
+            nc.gpsimd.tensor_tensor(
+                out=pair_sum[n][:], in0=prod[n][:, 0, :], in1=prod[n][:, 1, :], op=ALU.add
+            )
 
         def add_tokens(source, closes=False):
             opens = not token_sums
@@ -274,7 +280,7 @@ def tile_hydraencoderlayer_pa_t_kernel(tc, x, wk, wv, out):
             if m >= 0:
                 product(m, 0)
             if m + 1 == -1:
-                quantise_weight("wv", 0, DI)
+                quantise_weight("wv", slice(0, DI))
             if m + 1 >= 0:
                 pass_v(m + 1, 0)
             if m >= SUM_LAG:
@@ -286,17 +292,16 @@ def tile_hydraencoderlayer_pa_t_kernel(tc, x, wk, wv, out):
                 add_pair(m)
             quantise_x(n + AHEAD)
 
-        warm_up(6)
-        interleave_weight("wk", 0, DI // 2, on_vector)
-        interleave_weight("wk", DI // 2, WK_SPLIT, on_vector)
-        interleave_weight("wk", WK_SPLIT, DI, on_scalar)
-        quantise_weight("wk", 0, DI // 2)
-        quantise_weight("wk", DI // 2, DI)
+        warm_up()
+        interleave_weight("wk", slice(0, DI // 2), on_vector)
+        interleave_weight("wk", slice(DI // 2, WK_SPLIT), on_vector)
+        interleave_weight("wk", slice(WK_SPLIT, DI), on_scalar)
+        quantise_weight("wk", slice(0, DI // 2))
+        quantise_weight("wk", slice(DI // 2, DI))
         banks = [new_xt(), new_xt(psum_v, "v_ps")]
         for j in range(PAIR):
             transpose_tile(banks[j], 0, j)
         transpose_x(1, new_xt(psum_v, "v_ps"))
-        warm_up(1)
         for j in range(PAIR):
             regroup_tiles(0, slice(j, j + 1), banks[j], on_scalar)
             quantise_tiles(0, slice(j, j + 1))
@@ -314,8 +319,8 @@ def tile_hydraencoderlayer_pa_t_kernel(tc, x, wk, wv, out):
         transpose_x(4, new_xt())
         square_sum(0, 0)
         quantise_x(2)
-        interleave_weight("wv", 0, WV_SPLIT, on_vector)
-        interleave_weight("wv", WV_SPLIT, DI, on_scalar)
+        interleave_weight("wv", slice(0, WV_SPLIT), on_vector)
+        interleave_weight("wv", slice(WV_SPLIT, DI), on_scalar)
         quantise_x(3)
 
         for n in range(1, N_PAIRS - AHEAD):
@@ -401,5 +406,5 @@ def tile_hydraencoderlayer_pa_t_kernel(tc, x, wk, wv, out):
         pieces = out.rearrange("b o (i g q) -> g (b o i) q", i=E_BLOCKS, q=QUADRANT)
         for g in range(P // QUADRANT):
             queue = nc.sync if g % 2 == 0 else nc.scalar
-            first = g * QUADRANT
-            queue.dma_start(out=pieces[g], in_=out_rows[first : first + BATCH * E_BLOCKS, :])
+            rows = slice(g * QUADRANT, g * QUADRANT + BATCH * E_BLOCKS)
+            queue.dma_start(out=pieces[g], in_=out_rows[rows, :])

@@ -21,25 +21,21 @@ WORDS = D // 2
 HALVES = WORDS // P
 E_BLOCKS = DI // P
 PAIR = 2
-CHUNK_TILES = 4
-PAIRS_PER_CHUNK = CHUNK_TILES // PAIR
-N_CHUNKS = BATCH * TOKENS // (CHUNK_TILES * P)
-N_PAIRS = N_CHUNKS * PAIRS_PER_CHUNK
-LAST = N_PAIRS - 1
-
+QUAD = 4
+N_QUADS = BATCH * TOKENS // (QUAD * P)
+N_TILES = N_QUADS * QUAD
+RING = 7
 AHEAD = 3
-LAG = 3
-SUM_LAG = 2
-SPARE_PAIRS = 4
-GROUP_PAIRS = 2
-SINGLE_PAIRS = 4
-
-COPY_EVERY = 4
+LAG = 2
+ADD_COLS = 256
+FOLDED = 128
+G_FIRST = 2
+G_LAST = 12
+COPY_EVERY = 50
+COPY_AT = 10
+TAIL = 54
 WK_SPLIT = 336
-WV_SPLIT = 320
 RUN = 4
-
-RESULT_BANKS = 3
 WARM_UP = 6
 
 FLOPS = 2 * 2 * BATCH * TOKENS * D * DI
@@ -50,14 +46,11 @@ def tile_hydraencoderlayer_pa_t_kernel(tc, x, wk, wv, out):
     with ExitStack() as ctx:
         ctx.enter_context(tc.manual_schedule())
         consts = ctx.enter_context(tc.tile_pool(name="consts", bufs=1))
-        x_pool = ctx.enter_context(tc.tile_pool(name="x_pool", bufs=N_CHUNKS))
-        stage = ctx.enter_context(tc.tile_pool(name="stage", bufs=AHEAD))
-        operands = ctx.enter_context(tc.tile_pool(name="operands", bufs=AHEAD + LAG + 2))
-        work = ctx.enter_context(tc.tile_pool(name="work", bufs=2 * (SUM_LAG + 1)))
-        psum_t = ctx.enter_context(tc.psum_pool(name="psum_t", bufs=1))
-        psum_a = ctx.enter_context(tc.psum_pool(name="psum_a", bufs=RESULT_BANKS))
-        psum_v = ctx.enter_context(tc.psum_pool(name="psum_v", bufs=RESULT_BANKS))
-        psum_s = ctx.enter_context(tc.psum_pool(name="psum_s", bufs=1))
+        x_pool = ctx.enter_context(tc.tile_pool(name="x_pool", bufs=N_QUADS))
+        stage = ctx.enter_context(tc.tile_pool(name="stage", bufs=1))
+        operands = ctx.enter_context(tc.tile_pool(name="operands", bufs=AHEAD + LAG + 3))
+        work = ctx.enter_context(tc.tile_pool(name="work", bufs=3))
+        psum = ctx.enter_context(tc.psum_pool(name="psum", bufs=1))
         on_vector = nc.vector.tensor_copy
         on_scalar = nc.scalar.copy
 
@@ -71,13 +64,13 @@ def tile_hydraencoderlayer_pa_t_kernel(tc, x, wk, wv, out):
             )
 
         load_weight("wk", wk)
-        chunks = x.rearrange("b (q c t) k -> c (b q) (t k)", c=N_CHUNKS, t=CHUNK_TILES)
+        chunks = x.rearrange("b (q c t) k -> c (b q) (t k)", c=N_QUADS, t=QUAD)
         x_chunks = []
-        for c in range(N_CHUNKS):
-            x_sb = x_pool.tile([P, CHUNK_TILES * D], BF16)
+        for c in range(N_QUADS):
+            x_sb = x_pool.tile([P, QUAD * D], BF16)
             x_chunks.append(x_sb)
             if c == 0:
-                for part in (slice(0, D), slice(D, PAIR * D), slice(PAIR * D, CHUNK_TILES * D)):
+                for part in (slice(0, D), slice(D, PAIR * D), slice(PAIR * D, QUAD * D)):
                     nc.sync.dma_start(out=x_sb[:, part], in_=chunks[c][:, part])
             else:
                 nc.sync.dma_start(out=x_sb[:], in_=chunks[c])
@@ -95,9 +88,10 @@ def tile_hydraencoderlayer_pa_t_kernel(tc, x, wk, wv, out):
 
         w_grouped, w_codes, w_scales = {}, {}, {}
         for label in ("wk", "wv"):
-            w_grouped[label] = consts.tile([P, DI, PACK], BF16, name="%s_grouped" % label, align_bytes=64)
             w_codes[label] = consts.tile([P, DI], U32, name="%s_codes" % label, align_bytes=256)
             w_scales[label] = consts.tile([P, DI], U8, name="%s_scales" % label, align_bytes=256)
+
+        w_grouped["wk"] = consts.tile([P, DI, PACK], BF16, name="wk_grouped", align_bytes=64)
 
         def interleave_weight(label, cols, copy):
             by_column = w_raw[label][:].rearrange("q t (c i) -> q c t i", i=RUN)
@@ -113,184 +107,270 @@ def tile_hydraencoderlayer_pa_t_kernel(tc, x, wk, wv, out):
             )
 
         def warm_up():
-            bank = psum_s.tile([P, DI], F32, name="token_sums")
+            bank = psum.tile([P, DI], F32, name="token_sums")
             for _ in range(WARM_UP):
                 nc.tensor.matmul(out=bank[:], lhsT=zeros[:, :P], rhs=zeros[:], start=True, stop=True)
 
+        taken = []
+
+        def next_bank(shape):
+            taken.append(len(taken) % RING)
+            return psum.tile(shape, F32, name="bank%d" % taken[-1])
+
         xt, grouped, x_codes, x_scales = {}, {}, {}, {}
         a_ps, v_ps, a_sb = {}, {}, {}
+        folds = {}
         norm2, clamped, rnorm = {}, {}, {}
-        prod, pair_sum, token_sums = {}, {}, []
+        prod, pair_sum, summed, token_sums = {}, {}, set(), []
 
-        def new_xt(pool=psum_t, name="xt"):
-            return pool.tile([P, PAIR, HALVES, P], F32, name=name)
+        on_gpsimd = [q * QUAD + QUAD - 1 for q in range(G_FIRST, G_LAST + 1)]
+        groups = [list(range(QUAD)), [QUAD, QUAD + 1]]
+        for first in range(QUAD + PAIR, TAIL, QUAD):
+            own = [t for t in range(first, first + QUAD) if t not in on_gpsimd]
+            groups.append(own + [t for t in on_gpsimd if t == first - 2 * QUAD + 1])
+        late = [t for t in on_gpsimd if t > TAIL - 2 * QUAD]
+        for first in range(TAIL, N_TILES, PAIR):
+            groups.append([first, first + 1] + [t for t in late if 2 * first == 2 * TAIL + t - late[0] + QUAD])
+        place = {t: (g, col) for g in range(len(groups)) for col, t in enumerate(groups[g])}
 
-        def transpose_tile(bank, n, j):
-            x_words = x_chunks[n // PAIRS_PER_CHUNK][:].bitcast(F32)
-            first_word = ((n % PAIRS_PER_CHUNK) * PAIR + j) * WORDS
-            for u in range(HALVES):
-                w0 = first_word + u * P
-                nc.tensor.transpose(bank[:, j, u, :], x_words[:, w0 : w0 + P], ident[:])
+        def batch_of(t):
+            return divmod(t if t < 2 * QUAD else t + PAIR, QUAD)
 
-        def transpose_x(n, bank):
-            xt[n] = bank
-            for j in range(PAIR):
-                transpose_tile(bank, n, j)
+        def stage_tile(s, shape):
+            return stage.tile(shape, BF16, name="stage_wv" if s == 1 else "stage%d" % (s % 3), align_bytes=64)
 
-        def regroup_tiles(n, tiles, bank, copy):
-            if n not in grouped:
-                grouped[n] = stage.tile([P, PAIR * P * PACK], BF16, name="grouped", align_bytes=64)
-            words = grouped[n][:].bitcast(F32).rearrange("p (j r u) -> p j r u", j=PAIR, u=HALVES)
+        def transpose_tiles(tiles):
+            bank = next_bank([P, PAIR, HALVES, P])
+            for j, t in enumerate(tiles):
+                xt[t] = (bank, j)
+                x_words = x_chunks[t // QUAD][:].bitcast(F32)
+                for u in range(HALVES):
+                    w0 = (t % QUAD) * WORDS + u * P
+                    nc.tensor.transpose(bank[:, j, u, :], x_words[:, w0 : w0 + P], ident[:])
+
+        def transpose_pair(n):
+            transpose_tiles([PAIR * n, PAIR * n + 1])
+
+        def regroup(first, count, copy):
+            q, col = batch_of(first)
+            if q not in grouped:
+                grouped[q] = stage_tile(q, [P, QUAD * P * PACK])
+            words = grouped[q][:].bitcast(F32).rearrange("p (j r u) -> p j r u", j=QUAD, u=HALVES)
+            bank, j = xt[first]
             copy(
-                out=words[:, tiles, :, :],
-                in_=bank[:].rearrange("p j u r -> p j r u")[:, tiles, :, :],
+                out=words[:, col : col + count, :, :],
+                in_=bank[:].rearrange("p j u r -> p j r u")[:, j : j + count, :, :],
             )
 
-        def regroup_x(n, copy=on_vector):
-            regroup_tiles(n, slice(0, PAIR), xt[n], copy)
+        def regroup_pair(n, copy=on_vector):
+            regroup(PAIR * n, PAIR, copy)
 
-        def quantise_tiles(n, tiles):
-            if n not in x_codes:
-                x_codes[n] = operands.tile([P, PAIR * P], U32, name="x_codes", align_bytes=256)
-                x_scales[n] = operands.tile([P, PAIR * P], U8, name="x_scales", align_bytes=256)
-            cols = slice(tiles.start * P, tiles.stop * P)
+        def quantise(first, count):
+            q, j = batch_of(first)
+            if q not in x_codes:
+                x_codes[q] = operands.tile([P, QUAD * P], U32, name="x_codes", align_bytes=256)
+                x_scales[q] = operands.tile([P, QUAD * P], U8, name="x_scales", align_bytes=256)
+            cols = slice(j * P, (j + count) * P)
             nc.vector.quantize_mx(
-                out=x_codes[n][:, cols].bitcast(FP8X4),
-                scales=x_scales[n][:, cols],
-                in_=grouped[n][:, tiles.start * P * PACK : tiles.stop * P * PACK],
+                out=x_codes[q][:, cols].bitcast(FP8X4),
+                scales=x_scales[q][:, cols],
+                in_=grouped[q][:, j * P * PACK : (j + count) * P * PACK],
             )
 
-        def quantise_x(n):
-            quantise_tiles(n, slice(0, PAIR))
-
-        def mx_pass(bank, n, j, label):
+        def mx_pass(t, label):
+            bank = next_bank([P, DI])
+            q, j = batch_of(t)
             cols = slice(j * P, (j + 1) * P)
             nc.tensor.matmul_mx(
                 out=bank[:],
-                lhsT=x_codes[n][:, cols].bitcast(FP8X4),
-                lhsT_scale=x_scales[n][:, cols],
+                lhsT=x_codes[q][:, cols].bitcast(FP8X4),
+                lhsT_scale=x_scales[q][:, cols],
                 rhs=w_codes[label][:].bitcast(FP8X4),
                 rhs_scale=w_scales[label][:],
                 start=True,
                 stop=True,
             )
+            return bank
 
-        def pass_a(n, j):
-            a_ps[n, j] = psum_a.tile([P, DI], F32, name="a_ps")
-            mx_pass(a_ps[n, j], n, j, "wk")
+        def pass_a(t):
+            a_ps[t] = mx_pass(t, "wk")
 
-        def pass_v(n, j, pool=psum_v, name="v_ps"):
-            v_ps[n, j] = pool.tile([P, DI], F32, name=name)
-            mx_pass(v_ps[n, j], n, j, "wv")
+        def pass_v(t):
+            v_ps[t] = mx_pass(t, "wv")
 
-        def copy_a(n, j, copy=on_scalar):
-            a_sb[n, j] = work.tile([P, DI], F32, name="a_sb", bufs=PAIR * (LAG + SPARE_PAIRS))
-            copy(out=a_sb[n, j][:], in_=a_ps[n, j][:])
+        def copy_a(t, copy=on_scalar):
+            a_sb[t] = work.tile([P, DI], F32, name="a_sb", bufs=QUAD * (LAG + 3))
+            copy(out=a_sb[t][:], in_=a_ps[t][:])
 
-        def group_of(n):
-            count = GROUP_PAIRS if n < N_PAIRS - SINGLE_PAIRS else 1
-            return n - n % count, count
+        def norm_column(t):
+            g, col = place[t]
+            if g not in norm2:
+                norm2[g] = work.tile([P, len(groups[g])], F32, name="norm2", bufs=4)
+            return norm2[g][:, col : col + 1]
 
-        def closes_group(n):
-            return n >= 0 and sum(group_of(n)) == n + 1
+        def square_sum(t, source=a_sb):
+            unread = work.tile([P, DI], BF16, name="squares")
+            nc.scalar.activation(out=unread[:], in_=source[t][:], func=ACT.Square, accum_out=norm_column(t))
 
-        def square_sum(n, j, source=a_sb):
-            first, count = group_of(n)
-            col = (n - first) * PAIR + j
-            if first not in norm2:
-                norm2[first] = work.tile([P, count * PAIR], F32, name="norm2")
-            total = norm2[first][:, col : col + 1]
-            squares = work.tile([P, DI], BF16, name="squares")
-            nc.scalar.activation(out=squares[:], in_=source[n, j][:], func=ACT.Square, accum_out=total)
+        def fold_tile(q):
+            if q not in folds:
+                folds[q] = work.tile([P, 7, FOLDED], F32, name="folds")
+            return folds[q]
 
-        def clamp_norms(n):
-            first, count = group_of(n)
-            clamped[first] = work.tile([P, count * PAIR], F32, name="clamped")
-            nc.scalar.activation(out=clamped[first][:], in_=norm2[first][:], func=ACT.Relu, bias=-EPS * EPS)
+        def square_on_gpsimd(t):
+            blocks = a_sb[t][:].rearrange("p (i c) -> p i c", c=FOLDED)
+            nc.gpsimd.tensor_tensor(out=fold_tile(t // QUAD + 1)[:, 3:, :], in0=blocks, in1=blocks, op=ALU.mult)
 
-        def invert_norms(n):
-            first, count = group_of(n)
-            rnorm[first] = work.tile([P, count * PAIR], F32, name="rnorm")
+        def fold(q):
+            once, twice = QUAD * q - 1 in on_gpsimd, QUAD * (q - 1) - 1 in on_gpsimd
+            pieces = slice(0 if twice else 1, 3 if once else 1)
+            if once or twice:
+                source = fold_tile(q)[:, 1:, :].rearrange("p (i h) c -> p h i c", h=2)
+                nc.gpsimd.tensor_tensor(
+                    out=fold_tile(q + 1)[:, pieces, :],
+                    in0=source[:, 0, pieces, :],
+                    in1=source[:, 1, pieces, :],
+                    op=ALU.add,
+                )
+
+        def sum_folded(t):
+            unread = work.tile([P, FOLDED], BF16, name="folded_unread")
             nc.scalar.activation(
-                out=rnorm[first][:],
-                in_=clamped[first][:],
-                func=ACT.Abs_reciprocal_sqrt,
-                bias=EPS * EPS,
+                out=unread[:],
+                in_=folds[t // QUAD + 3][:, 0, :],
+                func=ACT.Identity,
+                accum_out=norm_column(t),
             )
 
-        def product(n, j):
-            if n not in prod:
-                prod[n] = work.tile([P, PAIR, DI], F32, name="prod")
-            first, count = group_of(n)
-            col = (n - first) * PAIR + j
+        def clamp_norms(g, cols=slice(None)):
+            if g not in clamped:
+                clamped[g] = work.tile([P, len(groups[g])], F32, name="clamped")
+            nc.scalar.activation(out=clamped[g][:, cols], in_=norm2[g][:, cols], func=ACT.Relu, bias=-EPS * EPS)
+
+        def invert_norms(g, cols=slice(None)):
+            if g not in rnorm:
+                rnorm[g] = work.tile([P, len(groups[g])], F32, name="rnorm")
+            nc.scalar.activation(
+                out=rnorm[g][:, cols], in_=clamped[g][:, cols], func=ACT.Abs_reciprocal_sqrt, bias=EPS * EPS
+            )
+
+        def product(t):
+            g, col = place[t]
+            if g not in prod:
+                prod[g] = work.tile([P, QUAD + 1, DI], F32, name="prod")
             nc.vector.scalar_tensor_tensor(
-                out=prod[n][:, j, :],
-                in0=v_ps[n, j][:],
-                scalar=rnorm[first][:, col : col + 1],
-                in1=a_sb[n, j][:],
+                out=prod[g][:, col, :],
+                in0=v_ps[t][:],
+                scalar=rnorm[g][:, col : col + 1],
+                in1=a_sb[t][:],
                 op0=ALU.mult,
                 op1=ALU.mult,
             )
 
-        def add_pair(n):
-            pair_sum[n] = work.tile([P, DI], F32, name="pair_sum")
+        def add_pairs(g, cols=DI, first=0):
+            pairs = min(PAIR, (len(groups[g]) - first) // 2)
+            pair_sum[g] = (work.tile([P, PAIR, DI], F32, name="pair_sum", bufs=3), cols, first, pairs)
             nc.gpsimd.tensor_tensor(
-                out=pair_sum[n][:], in0=prod[n][:, 0, :], in1=prod[n][:, 1, :], op=ALU.add
+                out=pair_sum[g][0][:, :pairs, :cols],
+                in0=prod[g][:, first : first + pairs, :cols],
+                in1=prod[g][:, first + pairs : first + 2 * pairs, :cols],
+                op=ALU.add,
             )
 
-        def add_tokens(source, closes=False):
+        def add_block(source, i, closes=False):
             opens = not token_sums
             if opens:
-                token_sums.append(psum_s.tile([P, E_BLOCKS, P], F32, name="token_sums"))
-            for i in range(E_BLOCKS):
-                nc.tensor.matmul(
-                    out=token_sums[0][:, i, :],
-                    lhsT=source[:, i * P : (i + 1) * P],
-                    rhs=ident[:],
-                    is_transpose=True,
-                    start=(opens and i == 0),
-                    stop=(closes and i == E_BLOCKS - 1),
-                )
+                token_sums.append(psum.tile([P, E_BLOCKS, P], F32, name="token_sums"))
+            nc.tensor.matmul(
+                out=token_sums[0][:, i, :],
+                lhsT=source[:, i * P : (i + 1) * P],
+                rhs=ident[:],
+                is_transpose=True,
+                start=opens,
+                stop=closes,
+            )
 
-        def step(n):
-            m = n - LAG
-            vector_copies = m < 0 or n % COPY_EVERY == COPY_EVERY - 1
-            regroup_x(n + AHEAD)
-            pass_a(n, 1)
-            if vector_copies:
-                copy_a(n, 1, on_vector)
-            if m >= 0:
-                pass_v(m, 1)
-            pass_a(n + 1, 0)
-            copy_a(n, 0)
-            if closes_group(n - 2) and group_of(n - 2)[0] not in rnorm:
-                invert_norms(n - 2)
-            square_sum(n - 1, 1)
-            if vector_copies:
-                square_sum(n, 0)
-                if closes_group(n - 1):
-                    clamp_norms(n - 1)
+        def add_tile(source, closes=False):
+            for i in range(E_BLOCKS):
+                add_block(source, i, closes and i == E_BLOCKS - 1)
+
+        def add_group(g, closes=False):
+            sums, cols, first, pairs = pair_sum.get(g, (None, 0, 0, 0))
+            blocks = []
+            for j in range(len(groups[g])):
+                start = cols // P if first <= j < first + 2 * pairs else 0
+                if (g, j) not in summed:
+                    blocks.extend((prod[g][:, j, :], i) for i in range(start, E_BLOCKS))
+            for h in range(pairs):
+                blocks.extend((sums[:, h, :], i) for i in range(cols // P))
+            for count, (source, i) in enumerate(blocks):
+                add_block(source, i, closes and count == len(blocks) - 1)
+
+        def add_product(t, closes=False):
+            g, col = place[t]
+            summed.add((g, col))
+            add_tile(prod[g][:, col, :], closes)
+
+        def interleave_wv():
+            w_grouped["wv"] = stage_tile(1, [P, DI, PACK])
+            nc.gpsimd.tensor_scalar(
+                out=w_grouped["wv"][:],
+                in0=w_raw["wv"][:].rearrange("q t c -> q c t"),
+                scalar1=1.0,
+                scalar2=0.0,
+                op0=ALU.mult,
+                op1=ALU.add,
+            )
+
+        def period(k):
+            t0 = QUAD * k
+            products = groups[k - 1]
+            late = [t for t in groups[k] if t in on_gpsimd]
+            squares_here = t0 + QUAD - 1 in on_gpsimd
+            by_vector = k % COPY_EVERY == COPY_AT or len(products) < QUAD
+            for j in range(QUAD):
+                pass_a(t0 + j)
+                if j < QUAD - 1:
+                    pass_v(products[j])
+            copy_a(t0)
+            for t in products[QUAD - 1 :]:
+                pass_v(t)
+            if t0 - 1 not in on_gpsimd:
+                square_sum(t0 - 1)
+            copy_a(t0 + 1)
+            product(products[0])
+            square_sum(t0)
+            product(products[1])
+            square_sum(t0 + 1)
+            if late:
+                sum_folded(late[0])
+            copy_a(t0 + 2)
+            clamp_norms(k)
+            for t in products[2:-1]:
+                product(t)
+            if by_vector:
+                square_sum(t0 + 2)
+                invert_norms(k)
             else:
-                copy_a(n, 1)
-                if closes_group(n - 1):
-                    clamp_norms(n - 1)
-                square_sum(n, 0)
-                if closes_group(n - 1):
-                    invert_norms(n - 1)
-            if m >= 0:
-                product(m, 0)
-            if m + 1 == -1:
-                quantise_weight("wv", slice(0, DI))
-            if m + 1 >= 0:
-                pass_v(m + 1, 0)
-            if m >= SUM_LAG:
-                add_tokens(pair_sum[m - SUM_LAG])
-            if n + AHEAD < LAST:
-                transpose_x(n + AHEAD + 1, new_xt())
-            if m >= 0:
-                product(m, 1)
-                add_pair(m)
-            quantise_x(n + AHEAD)
+                copy_a(t0 + 3)
+                invert_norms(k)
+                square_sum(t0 + 2)
+            if by_vector:
+                copy_a(t0 + QUAD - 1, on_vector)
+            product(products[-1])
+            add_pairs(k - 1, ADD_COLS if squares_here and len(products) == QUAD else DI, len(products) % PAIR)
+            quantise(QUAD * (k + 2) - PAIR, QUAD)
+            fold(k)
+            if squares_here:
+                square_on_gpsimd(t0 + QUAD - 1)
+            pairs = [n for n in (2 * k + 5, 2 * k + 6) if n < N_TILES // PAIR]
+            for n in pairs:
+                transpose_pair(n)
+            if k == 3:
+                add_group(0)
+            add_group(k - 2)
+            for n in pairs:
+                regroup_pair(n)
 
         warm_up()
         interleave_weight("wk", slice(0, DI // 2), on_vector)
@@ -298,102 +378,186 @@ def tile_hydraencoderlayer_pa_t_kernel(tc, x, wk, wv, out):
         interleave_weight("wk", slice(WK_SPLIT, DI), on_scalar)
         quantise_weight("wk", slice(0, DI // 2))
         quantise_weight("wk", slice(DI // 2, DI))
-        banks = [new_xt(), new_xt(psum_v, "v_ps")]
-        for j in range(PAIR):
-            transpose_tile(banks[j], 0, j)
-        transpose_x(1, new_xt(psum_v, "v_ps"))
-        for j in range(PAIR):
-            regroup_tiles(0, slice(j, j + 1), banks[j], on_scalar)
-            quantise_tiles(0, slice(j, j + 1))
-        regroup_x(1, on_scalar)
-        pass_a(0, 0)
-        pass_a(0, 1)
-        quantise_x(1)
-        transpose_x(2, new_xt(psum_v, "v_ps"))
-        transpose_x(3, new_xt())
-        pass_a(1, 0)
-        copy_a(0, 0)
-        copy_a(0, 1, on_vector)
-        regroup_x(2, on_scalar)
-        regroup_x(3)
-        transpose_x(4, new_xt())
-        square_sum(0, 0)
-        quantise_x(2)
-        interleave_weight("wv", slice(0, WV_SPLIT), on_vector)
-        interleave_weight("wv", slice(WV_SPLIT, DI), on_scalar)
-        quantise_x(3)
+        transpose_tiles([0])
+        transpose_tiles([1])
+        transpose_pair(1)
+        for t in range(PAIR):
+            regroup(t, 1, on_scalar)
+            quantise(t, 1)
+        regroup_pair(1, on_scalar)
+        pass_a(0)
+        pass_a(1)
+        quantise(2, 2)
+        transpose_pair(2)
+        transpose_pair(3)
+        copy_a(0)
+        copy_a(1, on_vector)
+        pass_a(2)
+        pass_a(3)
+        regroup_pair(2)
+        square_sum(0)
+        regroup_pair(3)
+        copy_a(2)
+        quantise(4, 2)
+        quantise(6, 2)
+        interleave_wv()
+        square_sum(1)
+        copy_a(3, on_vector)
+        transpose_pair(4)
+        pass_a(4)
+        pass_a(5)
+        transpose_pair(5)
+        square_sum(2)
+        regroup_pair(4)
+        copy_a(4)
+        square_sum(3)
+        transpose_pair(6)
+        pass_a(6)
+        pass_a(7)
+        regroup_pair(5)
+        copy_a(5)
+        transpose_pair(7)
+        clamp_norms(0)
+        square_sum(4)
+        invert_norms(0)
+        regroup_pair(6)
+        copy_a(6)
+        copy_a(7, on_vector)
+        transpose_pair(8)
+        quantise(8, 2)
+        quantise_weight("wv", slice(0, DI))
+        quantise(10, 4)
+        regroup_pair(7)
+        square_sum(5)
+        pass_a(8)
+        pass_a(9)
+        pass_v(0)
+        pass_v(1)
+        regroup_pair(8)
+        copy_a(8)
+        clamp_norms(1)
+        square_sum(6)
+        invert_norms(1)
+        product(0)
+        pass_a(10)
+        pass_v(2)
+        copy_a(9)
+        product(1)
+        pass_a(11)
+        pass_v(3)
+        square_sum(7)
+        square_sum(8)
+        product(2)
+        pass_v(4)
+        pass_v(5)
+        add_product(0)
+        product(3)
+        add_pairs(0, DI, PAIR)
+        quantise(14, 4)
+        square_sum(9)
+        copy_a(10)
+        clamp_norms(2)
+        copy_a(11)
+        invert_norms(2)
+        add_product(1)
+        transpose_pair(9)
+        transpose_pair(10)
+        product(4)
+        product(5)
+        square_on_gpsimd(11)
+        add_pairs(1)
+        regroup_pair(9)
+        regroup_pair(10)
+        square_sum(10)
+        for k in range(3, 14):
+            period(k)
 
-        for n in range(1, N_PAIRS - AHEAD):
-            step(n)
-
-        n = LAST - 2
-        pass_a(n, 1)
-        pass_v(n - 3, 1)
-        pass_a(n + 1, 0)
-        copy_a(n, 0)
-        copy_a(n, 1, on_vector)
-        square_sum(n - 1, 1)
-        square_sum(n, 0)
-        clamp_norms(n - 1)
-        product(n - 3, 0)
-        pass_v(n - 2, 0)
-        pass_a(n + 1, 1)
-        add_tokens(pair_sum[n - 5])
-        product(n - 3, 1)
-        add_pair(n - 3)
-        pass_v(n - 2, 1)
-
-        n = LAST - 1
-        copy_a(n, 0)
-        invert_norms(n - 2)
-        square_sum(n - 1, 1)
-        product(n - 3, 0)
-        pass_a(LAST, 0)
-        pass_v(n - 2, 0)
-        copy_a(n, 1)
-        clamp_norms(n - 1)
-        square_sum(n, 0)
-        invert_norms(n - 1)
-        add_tokens(pair_sum[n - 5])
-        product(n - 3, 1)
-        add_pair(n - 3)
-        pass_v(n - 2, 1)
-        pass_a(LAST, 1)
-        square_sum(n, 1)
-        product(n - 2, 0)
-        pass_v(n - 1, 0)
-        add_tokens(pair_sum[n - 4])
-        product(n - 2, 1)
-        add_pair(n - 2)
-        pass_v(n - 1, 1)
-
-        n = LAST
-        pass_v(n, 0, psum_t, "xt")
-        square_sum(n, 0, a_ps)
-        product(n - 2, 0)
-        clamp_norms(n - 1)
-        square_sum(n, 1, a_ps)
-        invert_norms(n - 1)
-        clamp_norms(n)
-        copy_a(n, 0)
-        invert_norms(n)
-        copy_a(n, 1)
-        pass_v(n - 1, 0)
-        pass_v(n - 1, 1, psum_a, "a_ps")
-        add_tokens(pair_sum[n - 4])
-        product(n - 2, 1)
-        add_pair(n - 2)
-        pass_v(n, 1)
-        add_tokens(pair_sum[n - 3])
-        product(n - 1, 0)
-        add_tokens(prod[n - 1][:, 0, :])
-        product(n - 1, 1)
-        add_tokens(prod[n - 1][:, 1, :])
-        product(n, 0)
-        add_tokens(pair_sum[n - 2])
-        add_tokens(prod[n][:, 0, :])
-        product(n, 1)
-        add_tokens(prod[n][:, 1, :], closes=True)
+        pass_a(56)
+        pass_v(50)
+        pass_a(57)
+        pass_v(52)
+        pass_a(58)
+        pass_v(53)
+        pass_a(59)
+        copy_a(56)
+        pass_v(43)
+        square_sum(55)
+        product(50)
+        copy_a(57)
+        product(52)
+        clamp_norms(14)
+        square_sum(56)
+        invert_norms(14)
+        product(53)
+        add_group(12)
+        product(43)
+        add_pairs(13)
+        quantise(62, 2)
+        fold(14)
+        square_sum(57)
+        sum_folded(47)
+        copy_a(58, on_vector)
+        pass_v(54)
+        pass_a(60)
+        pass_v(55)
+        pass_a(61)
+        copy_a(59, on_vector)
+        square_sum(58)
+        clamp_norms(15)
+        square_sum(59)
+        invert_norms(15)
+        product(54)
+        pass_v(56)
+        pass_v(57)
+        product(55)
+        add_pairs(14)
+        pass_v(47)
+        copy_a(60)
+        sum_folded(51)
+        add_group(13)
+        copy_a(61)
+        clamp_norms(16)
+        square_sum(60)
+        invert_norms(16)
+        product(56)
+        pass_a(62)
+        pass_a(63)
+        pass_v(58)
+        product(57)
+        add_pairs(15)
+        pass_v(59)
+        product(47)
+        pass_v(51)
+        add_group(14)
+        square_sum(61)
+        square_sum(62, a_ps)
+        clamp_norms(17)
+        square_sum(63, a_ps)
+        invert_norms(17)
+        product(58)
+        pass_v(60)
+        pass_v(61)
+        add_group(15)
+        product(59)
+        add_pairs(16)
+        copy_a(62)
+        clamp_norms(18)
+        copy_a(63)
+        invert_norms(18)
+        product(51)
+        taken.extend(range(PAIR))
+        pass_v(62)
+        pass_v(63)
+        add_product(51)
+        product(60)
+        add_product(60)
+        add_group(16)
+        product(61)
+        add_product(61)
+        product(62)
+        add_product(62)
+        product(63)
+        add_product(63, closes=True)
 
         nc.vector.tensor_reduce(
             out=out_cols[:, : BATCH * E_BLOCKS].rearrange("e (b i) -> e i b", b=BATCH),

@@ -32,7 +32,7 @@ FOLDED = 128
 G_FIRST = 2
 G_LAST = 12
 COPY_EVERY = 50
-COPY_AT = 10
+COPY_AT = 1
 TAIL = 54
 WK_SPLIT = 336
 RUN = 4
@@ -358,7 +358,10 @@ def tile_hydraencoderlayer_pa_t_kernel(tc, x, wk, wv, out):
             if by_vector:
                 copy_a(t0 + QUAD - 1, on_vector)
             product(products[-1])
-            add_pairs(k - 1, ADD_COLS if squares_here and len(products) == QUAD else DI, len(products) % PAIR)
+            if squares_here:
+                add_pairs(k - 1, ADD_COLS, len(products) - PAIR)
+            else:
+                add_pairs(k - 1)
             quantise(QUAD * (k + 2) - PAIR, QUAD)
             fold(k)
             if squares_here:

@@ -27,11 +27,15 @@ N_TILES = N_QUADS * QUAD
 RING = 7
 AHEAD = 3
 LAG = 2
-ADD_COLS = 256
+ADD_SQUARES = 6
+ADD_FOLDS = 6
+G_CYCLE = 2
+G_OFF = 1
+LATE = 2
 FOLDED = 128
-G_FIRST = 2
+G_FIRST = 0
 G_LAST = 12
-COPY_EVERY = 50
+COPY_EVERY = 3
 COPY_AT = 1
 TAIL = 54
 WK_SPLIT = 336
@@ -74,7 +78,7 @@ def tile_hydraencoderlayer_pa_t_kernel(tc, x, wk, wv, out):
                     nc.sync.dma_start(out=x_sb[:, part], in_=chunks[c][:, part])
             else:
                 nc.sync.dma_start(out=x_sb[:], in_=chunks[c])
-            if c == 1:
+            if c == 2:
                 load_weight("wv", wv)
 
         ident = consts.tile([P, P], F32)
@@ -123,21 +127,26 @@ def tile_hydraencoderlayer_pa_t_kernel(tc, x, wk, wv, out):
         norm2, clamped, rnorm = {}, {}, {}
         prod, pair_sum, summed, token_sums = {}, {}, set(), []
 
-        on_gpsimd = [q * QUAD + QUAD - 1 for q in range(G_FIRST, G_LAST + 1)]
-        groups = [list(range(QUAD)), [QUAD, QUAD + 1]]
+        on_gpsimd = [q * QUAD + QUAD - 1 for q in range(G_FIRST, G_LAST + 1) if q % G_CYCLE != G_OFF]
+        groups = [[t for t in range(QUAD + PAIR) if t not in on_gpsimd], []]
         for first in range(QUAD + PAIR, TAIL, QUAD):
             own = [t for t in range(first, first + QUAD) if t not in on_gpsimd]
-            groups.append(own + [t for t in on_gpsimd if t == first - 2 * QUAD + 1])
+            groups.append(own + [t for t in on_gpsimd if t == first - LATE * QUAD + 1])
         late = [t for t in on_gpsimd if t > TAIL - 2 * QUAD]
         for first in range(TAIL, N_TILES, PAIR):
-            groups.append([first, first + 1] + [t for t in late if 2 * first == 2 * TAIL + t - late[0] + QUAD])
+            groups.append([t for t in late if 2 * first == 2 * TAIL + t - (TAIL - 7) + QUAD] + [first, first + 1])
         place = {t: (g, col) for g in range(len(groups)) for col, t in enumerate(groups[g])}
 
         def batch_of(t):
+            if t >= N_TILES - QUAD - PAIR:
+                return (N_QUADS - 1, t - (N_TILES - QUAD - PAIR))
             return divmod(t if t < 2 * QUAD else t + PAIR, QUAD)
 
+        def batch_tiles(q):
+            return QUAD + PAIR if q == N_QUADS - 1 else QUAD
+
         def stage_tile(s, shape):
-            return stage.tile(shape, BF16, name="stage_wv" if s == 1 else "stage%d" % (s % 3), align_bytes=64)
+            return stage.tile(shape, BF16, name={1: "stage_wv", 3: "stage_g"}.get(s, "stage%d" % (s % 3)), align_bytes=64)
 
         def transpose_tiles(tiles):
             bank = next_bank([P, PAIR, HALVES, P])
@@ -154,8 +163,8 @@ def tile_hydraencoderlayer_pa_t_kernel(tc, x, wk, wv, out):
         def regroup(first, count, copy):
             q, col = batch_of(first)
             if q not in grouped:
-                grouped[q] = stage_tile(q, [P, QUAD * P * PACK])
-            words = grouped[q][:].bitcast(F32).rearrange("p (j r u) -> p j r u", j=QUAD, u=HALVES)
+                grouped[q] = stage_tile(q, [P, batch_tiles(q) * P * PACK])
+            words = grouped[q][:].bitcast(F32).rearrange("p (j r u) -> p j r u", r=P, u=HALVES)
             bank, j = xt[first]
             copy(
                 out=words[:, col : col + count, :, :],
@@ -168,8 +177,8 @@ def tile_hydraencoderlayer_pa_t_kernel(tc, x, wk, wv, out):
         def quantise(first, count):
             q, j = batch_of(first)
             if q not in x_codes:
-                x_codes[q] = operands.tile([P, QUAD * P], U32, name="x_codes", align_bytes=256)
-                x_scales[q] = operands.tile([P, QUAD * P], U8, name="x_scales", align_bytes=256)
+                x_codes[q] = operands.tile([P, batch_tiles(q) * P], U32, name="x_codes", align_bytes=256)
+                x_scales[q] = operands.tile([P, batch_tiles(q) * P], U8, name="x_scales", align_bytes=256)
             cols = slice(j * P, (j + count) * P)
             nc.vector.quantize_mx(
                 out=x_codes[q][:, cols].bitcast(FP8X4),
@@ -213,8 +222,10 @@ def tile_hydraencoderlayer_pa_t_kernel(tc, x, wk, wv, out):
             nc.scalar.activation(out=unread[:], in_=source[t][:], func=ACT.Square, accum_out=norm_column(t))
 
         def fold_tile(q):
+            if q == 1 and q not in folds:
+                folds[q] = stage.tile([P, 7, FOLDED], F32, name="stage_g", align_bytes=64)
             if q not in folds:
-                folds[q] = work.tile([P, 7, FOLDED], F32, name="folds")
+                folds[q] = work.tile([P, 7, FOLDED], F32, name="folds", bufs=LATE + 1)
             return folds[q]
 
         def square_on_gpsimd(t):
@@ -267,13 +278,17 @@ def tile_hydraencoderlayer_pa_t_kernel(tc, x, wk, wv, out):
                 op1=ALU.mult,
             )
 
-        def add_pairs(g, cols=DI, first=0):
-            pairs = min(PAIR, (len(groups[g]) - first) // 2)
-            pair_sum[g] = (work.tile([P, PAIR, DI], F32, name="pair_sum", bufs=3), cols, first, pairs)
+        def add_pairs(g, blocks=PAIR * E_BLOCKS):
+            count = len(groups[g])
+            pairs = min(PAIR, count // 2)
+            blocks = min(blocks, pairs * E_BLOCKS)
+            flat = prod[g][:].rearrange("p j e -> p (j e)")
+            ends = ((count - pairs) * DI, count * DI)
+            pair_sum[g] = (work.tile([P, PAIR * DI], F32, name="pair_sum", bufs=3), blocks)
             nc.gpsimd.tensor_tensor(
-                out=pair_sum[g][0][:, :pairs, :cols],
-                in0=prod[g][:, first : first + pairs, :cols],
-                in1=prod[g][:, first + pairs : first + 2 * pairs, :cols],
+                out=pair_sum[g][0][:, : blocks * P],
+                in0=flat[:, ends[0] - blocks * P : ends[0]],
+                in1=flat[:, ends[1] - blocks * P : ends[1]],
                 op=ALU.add,
             )
 
@@ -283,7 +298,7 @@ def tile_hydraencoderlayer_pa_t_kernel(tc, x, wk, wv, out):
                 token_sums.append(psum.tile([P, E_BLOCKS, P], F32, name="token_sums"))
             nc.tensor.matmul(
                 out=token_sums[0][:, i, :],
-                lhsT=source[:, i * P : (i + 1) * P],
+                lhsT=source,
                 rhs=ident[:],
                 is_transpose=True,
                 start=opens,
@@ -292,19 +307,19 @@ def tile_hydraencoderlayer_pa_t_kernel(tc, x, wk, wv, out):
 
         def add_tile(source, closes=False):
             for i in range(E_BLOCKS):
-                add_block(source, i, closes and i == E_BLOCKS - 1)
+                add_block(source[:, i * P : (i + 1) * P], i, closes and i == E_BLOCKS - 1)
 
-        def add_group(g, closes=False):
-            sums, cols, first, pairs = pair_sum.get(g, (None, 0, 0, 0))
-            blocks = []
-            for j in range(len(groups[g])):
-                start = cols // P if first <= j < first + 2 * pairs else 0
-                if (g, j) not in summed:
-                    blocks.extend((prod[g][:, j, :], i) for i in range(start, E_BLOCKS))
-            for h in range(pairs):
-                blocks.extend((sums[:, h, :], i) for i in range(cols // P))
-            for count, (source, i) in enumerate(blocks):
-                add_block(source, i, closes and count == len(blocks) - 1)
+        def add_group(g):
+            sums, added = pair_sum.get(g, (None, 0))
+            count = len(groups[g])
+            pairs = min(PAIR, count // 2)
+            ends = ((count - pairs) * E_BLOCKS, count * E_BLOCKS)
+            for block in range(count * E_BLOCKS):
+                j, i = divmod(block, E_BLOCKS)
+                if (g, j) not in summed and not any(end - added <= block < end for end in ends):
+                    add_block(prod[g][:, j, i * P : (i + 1) * P], i)
+            for block in range(added):
+                add_block(sums[:, block * P : (block + 1) * P], (block - added) % E_BLOCKS)
 
         def add_product(t, closes=False):
             g, col = place[t]
@@ -327,7 +342,7 @@ def tile_hydraencoderlayer_pa_t_kernel(tc, x, wk, wv, out):
             products = groups[k - 1]
             late = [t for t in groups[k] if t in on_gpsimd]
             squares_here = t0 + QUAD - 1 in on_gpsimd
-            by_vector = k % COPY_EVERY == COPY_AT or len(products) < QUAD
+            by_vector = k % COPY_EVERY == COPY_AT or k == 13
             for j in range(QUAD):
                 pass_a(t0 + j)
                 if j < QUAD - 1:
@@ -344,29 +359,35 @@ def tile_hydraencoderlayer_pa_t_kernel(tc, x, wk, wv, out):
             square_sum(t0 + 1)
             if late:
                 sum_folded(late[0])
-            copy_a(t0 + 2)
-            clamp_norms(k)
             for t in products[2:-1]:
                 product(t)
             if by_vector:
+                copy_a(t0 + 2, on_vector)
+                copy_a(t0 + 3)
+                clamp_norms(k)
                 square_sum(t0 + 2)
                 invert_norms(k)
             else:
+                copy_a(t0 + 2)
+                clamp_norms(k)
                 copy_a(t0 + 3)
                 invert_norms(k)
                 square_sum(t0 + 2)
-            if by_vector:
-                copy_a(t0 + QUAD - 1, on_vector)
+            pairs = [n for n in (2 * k + 5, 2 * k + 6) if n < N_TILES // PAIR]
+            if len(pairs) < PAIR:
+                transpose_pair(pairs[0])
+                regroup_pair(pairs.pop())
             product(products[-1])
-            if squares_here:
-                add_pairs(k - 1, ADD_COLS, len(products) - PAIR)
-            else:
-                add_pairs(k - 1)
+            folds_here = t0 - 1 in on_gpsimd
+            add_pairs(k - 1, ADD_SQUARES if squares_here else ADD_FOLDS if folds_here else PAIR * E_BLOCKS)
             quantise(QUAD * (k + 2) - PAIR, QUAD)
-            fold(k)
+            if batch_tiles(k + 2) > QUAD:
+                quantise(N_TILES - PAIR, PAIR)
+            if folds_here:
+                fold(k)
+                fold(k + 1)
             if squares_here:
                 square_on_gpsimd(t0 + QUAD - 1)
-            pairs = [n for n in (2 * k + 5, 2 * k + 6) if n < N_TILES // PAIR]
             for n in pairs:
                 transpose_pair(n)
             if k == 3:
@@ -383,92 +404,92 @@ def tile_hydraencoderlayer_pa_t_kernel(tc, x, wk, wv, out):
         quantise_weight("wk", slice(DI // 2, DI))
         transpose_tiles([0])
         transpose_tiles([1])
-        transpose_pair(1)
+        transpose_tiles([2])
+        transpose_tiles([3])
         for t in range(PAIR):
             regroup(t, 1, on_scalar)
             quantise(t, 1)
-        regroup_pair(1, on_scalar)
+        regroup(2, 1, on_vector)
+        regroup(3, 1, on_scalar)
         pass_a(0)
         pass_a(1)
         quantise(2, 2)
         transpose_pair(2)
         transpose_pair(3)
+        square_sum(0, a_ps)
         copy_a(0)
         copy_a(1, on_vector)
         pass_a(2)
         pass_a(3)
         regroup_pair(2)
-        square_sum(0)
+        square_sum(1)
         regroup_pair(3)
         copy_a(2)
+        transpose_pair(4)
+        transpose_pair(5)
         quantise(4, 2)
         quantise(6, 2)
         interleave_wv()
-        square_sum(1)
-        copy_a(3, on_vector)
-        transpose_pair(4)
+        copy_a(3)
+        square_sum(2)
         pass_a(4)
         pass_a(5)
-        transpose_pair(5)
-        square_sum(2)
-        regroup_pair(4)
-        copy_a(4)
-        square_sum(3)
-        transpose_pair(6)
         pass_a(6)
         pass_a(7)
+        regroup_pair(4)
+        copy_a(4)
+        clamp_norms(0, slice(0, 3))
         regroup_pair(5)
-        copy_a(5)
+        transpose_pair(6)
         transpose_pair(7)
-        clamp_norms(0)
-        square_sum(4)
-        invert_norms(0)
-        regroup_pair(6)
+        copy_a(5, on_vector)
         copy_a(6)
-        copy_a(7, on_vector)
+        invert_norms(0, slice(0, 3))
+        regroup_pair(6)
+        square_sum(4)
+        regroup_pair(7)
         transpose_pair(8)
+        square_sum(5)
+        copy_a(7)
         quantise(8, 2)
         quantise_weight("wv", slice(0, DI))
         quantise(10, 4)
-        regroup_pair(7)
-        square_sum(5)
+        square_on_gpsimd(3)
+        fold(1)
+        fold(2)
+        clamp_norms(0, slice(3, 5))
+        square_sum(6)
+        invert_norms(0, slice(3, 5))
         pass_a(8)
         pass_a(9)
         pass_v(0)
         pass_v(1)
         regroup_pair(8)
         copy_a(8)
-        clamp_norms(1)
-        square_sum(6)
-        invert_norms(1)
+        square_sum(7)
         product(0)
         pass_a(10)
         pass_v(2)
         copy_a(9)
         product(1)
         pass_a(11)
-        pass_v(3)
-        square_sum(7)
-        square_sum(8)
-        product(2)
         pass_v(4)
+        square_sum(8)
         pass_v(5)
         add_product(0)
-        product(3)
-        add_pairs(0, DI, PAIR)
+        transpose_pair(9)
+        transpose_pair(10)
+        product(2)
+        product(4)
+        product(5)
+        add_pairs(0, ADD_SQUARES)
         quantise(14, 4)
         square_sum(9)
         copy_a(10)
         clamp_norms(2)
         copy_a(11)
         invert_norms(2)
-        add_product(1)
-        transpose_pair(9)
-        transpose_pair(10)
-        product(4)
-        product(5)
         square_on_gpsimd(11)
-        add_pairs(1)
         regroup_pair(9)
         regroup_pair(10)
         square_sum(10)
@@ -492,54 +513,54 @@ def tile_hydraencoderlayer_pa_t_kernel(tc, x, wk, wv, out):
         square_sum(56)
         invert_norms(14)
         product(53)
-        add_group(12)
-        product(43)
-        add_pairs(13)
-        quantise(62, 2)
-        fold(14)
-        square_sum(57)
-        sum_folded(47)
-        copy_a(58, on_vector)
         pass_v(54)
         pass_a(60)
         pass_v(55)
-        pass_a(61)
+        add_group(12)
+        product(43)
+        add_pairs(13)
+        copy_a(58)
+        square_sum(57)
         copy_a(59, on_vector)
+        pass_a(61)
+        pass_v(56)
+        pass_v(57)
+        pass_a(62)
         square_sum(58)
         clamp_norms(15)
         square_sum(59)
         invert_norms(15)
         product(54)
-        pass_v(56)
-        pass_v(57)
+        pass_a(63)
         product(55)
         add_pairs(14)
-        pass_v(47)
-        copy_a(60)
+        copy_a(60, on_vector)
         sum_folded(51)
-        add_group(13)
         copy_a(61)
+        pass_v(51)
+        pass_v(58)
+        pass_v(59)
+        add_group(13)
         clamp_norms(16)
         square_sum(60)
         invert_norms(16)
         product(56)
-        pass_a(62)
-        pass_a(63)
-        pass_v(58)
         product(57)
         add_pairs(15)
-        pass_v(59)
-        product(47)
-        pass_v(51)
+        pass_v(60)
+        pass_v(61)
         add_group(14)
         square_sum(61)
         square_sum(62, a_ps)
         clamp_norms(17)
         square_sum(63, a_ps)
         invert_norms(17)
+        product(51)
         product(58)
-        pass_v(60)
-        pass_v(61)
+        taken.extend(range(PAIR))
+        pass_v(62)
+        pass_v(63)
+        add_product(51)
         add_group(15)
         product(59)
         add_pairs(16)
@@ -547,16 +568,11 @@ def tile_hydraencoderlayer_pa_t_kernel(tc, x, wk, wv, out):
         clamp_norms(18)
         copy_a(63)
         invert_norms(18)
-        product(51)
-        taken.extend(range(PAIR))
-        pass_v(62)
-        pass_v(63)
-        add_product(51)
         product(60)
         add_product(60)
-        add_group(16)
         product(61)
         add_product(61)
+        add_group(16)
         product(62)
         add_product(62)
         product(63)

@@ -377,11 +377,13 @@ def tile_hydraencoderlayer_pa_t_kernel(tc, x, wk, wv, out):
             if len(pairs) < PAIR:
                 transpose_pair(pairs[0])
                 regroup_pair(pairs.pop())
+                quantise(QUAD * (k + 2) - PAIR, QUAD)
             product(products[-1])
             folds_here = t0 - 1 in on_gpsimd
             add_pairs(k - 1, ADD_SQUARES if squares_here else ADD_FOLDS if folds_here else PAIR * E_BLOCKS)
-            quantise(QUAD * (k + 2) - PAIR, QUAD)
-            if batch_tiles(k + 2) > QUAD:
+            if pairs:
+                quantise(QUAD * (k + 2) - PAIR, QUAD)
+            else:
                 quantise(N_TILES - PAIR, PAIR)
             if folds_here:
                 fold(k)

@@ -35,6 +35,7 @@ LATE = 2
 FOLDED = 128
 G_FIRST = 0
 G_LAST = 12
+LAST_ADD = 2
 COPY_EVERY = 3
 COPY_AT = 1
 TAIL = 54
@@ -117,14 +118,20 @@ def tile_hydraencoderlayer_pa_t_kernel(tc, x, wk, wv, out):
 
         taken = []
 
-        def next_bank(shape):
-            taken.append(len(taken) % RING)
-            return psum.tile(shape, F32, name="bank%d" % taken[-1])
+        bank_of = {}
+
+        def next_bank(shape, holder=None, after=None):
+            if after is None:
+                taken.append(len(taken) % RING)
+            bank_of[holder] = taken[-1] if after is None else bank_of[after]
+            return psum.tile(shape, F32, name="bank%d" % bank_of[holder])
 
         xt, grouped, x_codes, x_scales = {}, {}, {}, {}
         a_ps, v_ps, a_sb = {}, {}, {}
         folds = {}
-        norm2, clamped, rnorm = {}, {}, {}
+        norm2 = consts.tile([P, N_TILES], F32, name="norm2")
+        clamped = consts.tile([P, N_TILES], F32, name="clamped")
+        rnorm = consts.tile([P, N_TILES], F32, name="rnorm")
         prod, pair_sum, summed, token_sums = {}, {}, set(), []
 
         on_gpsimd = [q * QUAD + QUAD - 1 for q in range(G_FIRST, G_LAST + 1) if q % G_CYCLE != G_OFF]
@@ -134,7 +141,8 @@ def tile_hydraencoderlayer_pa_t_kernel(tc, x, wk, wv, out):
             groups.append(own + [t for t in on_gpsimd if t == first - LATE * QUAD + 1])
         late = [t for t in on_gpsimd if t > TAIL - 2 * QUAD]
         for first in range(TAIL, N_TILES, PAIR):
-            groups.append([t for t in late if 2 * first == 2 * TAIL + t - (TAIL - 7) + QUAD] + [first, first + 1])
+            groups.append([t for t in late if first == N_TILES - PAIR] + [first, first + 1])
+        order = [t for group in groups for t in group]
         place = {t: (g, col) for g in range(len(groups)) for col, t in enumerate(groups[g])}
 
         def batch_of(t):
@@ -186,8 +194,8 @@ def tile_hydraencoderlayer_pa_t_kernel(tc, x, wk, wv, out):
                 in_=grouped[q][:, j * P * PACK : (j + count) * P * PACK],
             )
 
-        def mx_pass(t, label):
-            bank = next_bank([P, DI])
+        def mx_pass(t, label, after):
+            bank = next_bank([P, DI], (label, t), after)
             q, j = batch_of(t)
             cols = slice(j * P, (j + 1) * P)
             nc.tensor.matmul_mx(
@@ -201,21 +209,18 @@ def tile_hydraencoderlayer_pa_t_kernel(tc, x, wk, wv, out):
             )
             return bank
 
-        def pass_a(t):
-            a_ps[t] = mx_pass(t, "wk")
+        def pass_a(t, after=None):
+            a_ps[t] = mx_pass(t, "wk", after)
 
-        def pass_v(t):
-            v_ps[t] = mx_pass(t, "wv")
+        def pass_v(t, after=None):
+            v_ps[t] = mx_pass(t, "wv", after)
 
         def copy_a(t, copy=on_scalar):
             a_sb[t] = work.tile([P, DI], F32, name="a_sb", bufs=QUAD * (LAG + 3))
             copy(out=a_sb[t][:], in_=a_ps[t][:])
 
         def norm_column(t):
-            g, col = place[t]
-            if g not in norm2:
-                norm2[g] = work.tile([P, len(groups[g])], F32, name="norm2", bufs=4)
-            return norm2[g][:, col : col + 1]
+            return norm2[:, order.index(t) : order.index(t) + 1]
 
         def square_sum(t, source=a_sb):
             unread = work.tile([P, DI], BF16, name="squares")
@@ -253,27 +258,28 @@ def tile_hydraencoderlayer_pa_t_kernel(tc, x, wk, wv, out):
                 accum_out=norm_column(t),
             )
 
-        def clamp_norms(g, cols=slice(None)):
-            if g not in clamped:
-                clamped[g] = work.tile([P, len(groups[g])], F32, name="clamped")
-            nc.scalar.activation(out=clamped[g][:, cols], in_=norm2[g][:, cols], func=ACT.Relu, bias=-EPS * EPS)
+        def columns(tiles):
+            return slice(order.index(tiles[0]), order.index(tiles[-1]) + 1)
 
-        def invert_norms(g, cols=slice(None)):
-            if g not in rnorm:
-                rnorm[g] = work.tile([P, len(groups[g])], F32, name="rnorm")
+        def clamp_norms(tiles):
+            cols = columns(tiles)
+            nc.scalar.activation(out=clamped[:, cols], in_=norm2[:, cols], func=ACT.Relu, bias=-EPS * EPS)
+
+        def invert_norms(tiles):
+            cols = columns(tiles)
             nc.scalar.activation(
-                out=rnorm[g][:, cols], in_=clamped[g][:, cols], func=ACT.Abs_reciprocal_sqrt, bias=EPS * EPS
+                out=rnorm[:, cols], in_=clamped[:, cols], func=ACT.Abs_reciprocal_sqrt, bias=EPS * EPS
             )
 
-        def product(t):
+        def product(t, cols=slice(0, DI)):
             g, col = place[t]
             if g not in prod:
                 prod[g] = work.tile([P, QUAD + 1, DI], F32, name="prod")
             nc.vector.scalar_tensor_tensor(
-                out=prod[g][:, col, :],
-                in0=v_ps[t][:],
-                scalar=rnorm[g][:, col : col + 1],
-                in1=a_sb[t][:],
+                out=prod[g][:, col, cols],
+                in0=v_ps[t][:, cols],
+                scalar=rnorm[:, columns([t])],
+                in1=a_sb[t][:, cols],
                 op0=ALU.mult,
                 op1=ALU.mult,
             )
@@ -364,14 +370,14 @@ def tile_hydraencoderlayer_pa_t_kernel(tc, x, wk, wv, out):
             if by_vector:
                 copy_a(t0 + 2, on_vector)
                 copy_a(t0 + 3)
-                clamp_norms(k)
+                clamp_norms(groups[k])
                 square_sum(t0 + 2)
-                invert_norms(k)
+                invert_norms(groups[k])
             else:
                 copy_a(t0 + 2)
-                clamp_norms(k)
+                clamp_norms(groups[k])
                 copy_a(t0 + 3)
-                invert_norms(k)
+                invert_norms(groups[k])
                 square_sum(t0 + 2)
             pairs = [n for n in (2 * k + 5, 2 * k + 6) if n < N_TILES // PAIR]
             if len(pairs) < PAIR:
@@ -387,7 +393,8 @@ def tile_hydraencoderlayer_pa_t_kernel(tc, x, wk, wv, out):
                 quantise(N_TILES - PAIR, PAIR)
             if folds_here:
                 fold(k)
-                fold(k + 1)
+                if pairs:
+                    fold(k + 1)
             if squares_here:
                 square_on_gpsimd(t0 + QUAD - 1)
             for n in pairs:
@@ -440,13 +447,13 @@ def tile_hydraencoderlayer_pa_t_kernel(tc, x, wk, wv, out):
         pass_a(7)
         regroup_pair(4)
         copy_a(4)
-        clamp_norms(0, slice(0, 3))
+        clamp_norms([0, 2])
         regroup_pair(5)
         transpose_pair(6)
         transpose_pair(7)
         copy_a(5, on_vector)
         copy_a(6)
-        invert_norms(0, slice(0, 3))
+        invert_norms([0, 2])
         regroup_pair(6)
         square_sum(4)
         regroup_pair(7)
@@ -459,9 +466,9 @@ def tile_hydraencoderlayer_pa_t_kernel(tc, x, wk, wv, out):
         square_on_gpsimd(3)
         fold(1)
         fold(2)
-        clamp_norms(0, slice(3, 5))
+        clamp_norms([4, 5])
         square_sum(6)
-        invert_norms(0, slice(3, 5))
+        invert_norms([4, 5])
         pass_a(8)
         pass_a(9)
         pass_v(0)
@@ -488,9 +495,9 @@ def tile_hydraencoderlayer_pa_t_kernel(tc, x, wk, wv, out):
         quantise(14, 4)
         square_sum(9)
         copy_a(10)
-        clamp_norms(2)
+        clamp_norms(groups[2])
         copy_a(11)
-        invert_norms(2)
+        invert_norms(groups[2])
         square_on_gpsimd(11)
         regroup_pair(9)
         regroup_pair(10)
@@ -506,78 +513,81 @@ def tile_hydraencoderlayer_pa_t_kernel(tc, x, wk, wv, out):
         pass_v(53)
         pass_a(59)
         copy_a(56)
-        pass_v(43)
+        pass_v(43, ("wk", 56))
         square_sum(55)
         product(50)
+        pass_v(54, ("wv", 50))
         copy_a(57)
         product(52)
-        clamp_norms(14)
+        pass_a(60, ("wv", 52))
+        pass_v(55, ("wk", 57))
+        clamp_norms([54, 55])
         square_sum(56)
-        invert_norms(14)
+        invert_norms([54, 55])
         product(53)
-        pass_v(54)
-        pass_a(60)
-        pass_v(55)
+        pass_a(61, ("wv", 53))
         add_group(12)
         product(43)
         add_pairs(13)
+        fold(14)
         copy_a(58)
         square_sum(57)
         copy_a(59, on_vector)
-        pass_a(61)
-        pass_v(56)
-        pass_v(57)
-        pass_a(62)
+        pass_v(56, ("wv", 43))
+        pass_v(57, ("wk", 58))
+        pass_a(62, ("wk", 59))
         square_sum(58)
-        clamp_norms(15)
+        clamp_norms([56, 57])
         square_sum(59)
-        invert_norms(15)
+        invert_norms([56, 57])
         product(54)
-        pass_a(63)
+        pass_a(63, ("wv", 54))
+        copy_a(60, on_vector)
+        pass_v(58, ("wk", 60))
+        copy_a(61, on_vector)
+        pass_v(59, ("wk", 61))
+        add_group(13)
         product(55)
         add_pairs(14)
-        copy_a(60, on_vector)
-        sum_folded(51)
-        copy_a(61)
-        pass_v(51)
-        pass_v(58)
-        pass_v(59)
-        add_group(13)
-        clamp_norms(16)
         square_sum(60)
-        invert_norms(16)
+        clamp_norms([58, 59])
+        square_sum(61)
+        invert_norms([58, 59])
+        pass_v(60, ("wv", 55))
         product(56)
+        pass_v(61, ("wv", 56))
         product(57)
         add_pairs(15)
-        pass_v(60)
-        pass_v(61)
+        pass_v(51, ("wv", 57))
         add_group(14)
-        square_sum(61)
         square_sum(62, a_ps)
-        clamp_norms(17)
+        clamp_norms([60, 61])
+        sum_folded(51)
+        invert_norms([60, 61])
         square_sum(63, a_ps)
-        invert_norms(17)
-        product(51)
         product(58)
-        taken.extend(range(PAIR))
-        pass_v(62)
-        pass_v(63)
-        add_product(51)
-        add_group(15)
+        pass_v(62, ("wv", 58))
         product(59)
         add_pairs(16)
+        pass_v(63, ("wv", 59))
+        add_group(15)
+        clamp_norms([51, 62])
         copy_a(62)
-        clamp_norms(18)
+        invert_norms([51, 62])
+        clamp_norms([63])
         copy_a(63)
-        invert_norms(18)
+        invert_norms([63])
         product(60)
         add_product(60)
         product(61)
         add_product(61)
         add_group(16)
+        product(51)
+        add_product(51)
         product(62)
         add_product(62)
-        product(63)
+        for half in (slice(0, DI // 2), slice(DI // 2, DI)):
+            product(63, half)
         add_product(63, closes=True)
 
         nc.vector.tensor_reduce(

@@ -42,6 +42,7 @@ TAIL = 54
 WK_SPLIT = 336
 RUN = 4
 WARM_UP = 6
+KEEP_WARM = 3
 
 FLOPS = 2 * 2 * BATCH * TOKENS * D * DI
 
@@ -111,9 +112,9 @@ def tile_hydraencoderlayer_pa_t_kernel(tc, x, wk, wv, out):
                 in_=w_grouped[label][:, cols, :].rearrange("q c t -> q (c t)"),
             )
 
-        def warm_up():
+        def warm_up(count):
             bank = psum.tile([P, DI], F32, name="token_sums")
-            for _ in range(WARM_UP):
+            for _ in range(count):
                 nc.tensor.matmul(out=bank[:], lhsT=zeros[:, :P], rhs=zeros[:], start=True, stop=True)
 
         taken = []
@@ -356,9 +357,9 @@ def tile_hydraencoderlayer_pa_t_kernel(tc, x, wk, wv, out):
             copy_a(t0)
             for t in products[QUAD - 1 :]:
                 pass_v(t)
+            copy_a(t0 + 1)
             if t0 - 1 not in on_gpsimd:
                 square_sum(t0 - 1)
-            copy_a(t0 + 1)
             product(products[0])
             square_sum(t0)
             product(products[1])
@@ -405,7 +406,7 @@ def tile_hydraencoderlayer_pa_t_kernel(tc, x, wk, wv, out):
             for n in pairs:
                 regroup_pair(n)
 
-        warm_up()
+        warm_up(WARM_UP)
         interleave_weight("wk", slice(0, DI // 2), on_vector)
         interleave_weight("wk", slice(DI // 2, WK_SPLIT), on_vector)
         interleave_weight("wk", slice(WK_SPLIT, DI), on_scalar)
@@ -457,6 +458,7 @@ def tile_hydraencoderlayer_pa_t_kernel(tc, x, wk, wv, out):
         regroup_pair(6)
         square_sum(4)
         regroup_pair(7)
+        warm_up(KEEP_WARM)
         transpose_pair(8)
         square_sum(5)
         copy_a(7)

@@ -39,6 +39,10 @@ LAST_ADD = 2
 COPY_EVERY = 3
 COPY_AT = 1
 TAIL = 54
+BLOCK = 16
+TURNED_FIRST = 30
+TURNED = 32
+TURNED_PARTS = ((0, 8), (8, 20), (20, 32))
 WK_SPLIT = 336
 RUN = 4
 WARM_UP = 6
@@ -52,7 +56,7 @@ def tile_hydraencoderlayer_pa_t_kernel(tc, x, wk, wv, out):
     with ExitStack() as ctx:
         ctx.enter_context(tc.manual_schedule())
         consts = ctx.enter_context(tc.tile_pool(name="consts", bufs=1))
-        x_pool = ctx.enter_context(tc.tile_pool(name="x_pool", bufs=N_QUADS))
+        x_pool = ctx.enter_context(tc.tile_pool(name="x_pool", bufs=1))
         stage = ctx.enter_context(tc.tile_pool(name="stage", bufs=1))
         operands = ctx.enter_context(tc.tile_pool(name="operands", bufs=AHEAD + LAG + 3))
         work = ctx.enter_context(tc.tile_pool(name="work", bufs=3))
@@ -72,8 +76,8 @@ def tile_hydraencoderlayer_pa_t_kernel(tc, x, wk, wv, out):
         load_weight("wk", wk)
         chunks = x.rearrange("b (q c t) k -> c (b q) (t k)", c=N_QUADS, t=QUAD)
         x_chunks = []
-        for c in range(N_QUADS):
-            x_sb = x_pool.tile([P, QUAD * D], BF16)
+        for c in range(N_QUADS // 2):
+            x_sb = x_pool.tile([P, QUAD * D], BF16, name="x_rows%d" % c)
             x_chunks.append(x_sb)
             if c == 0:
                 for part in (slice(0, D), slice(D, PAIR * D), slice(PAIR * D, QUAD * D)):
@@ -82,6 +86,20 @@ def tile_hydraencoderlayer_pa_t_kernel(tc, x, wk, wv, out):
                 nc.sync.dma_start(out=x_sb[:], in_=chunks[c])
             if c == 2:
                 load_weight("wv", wv)
+
+        pieces = x.rearrange("b (d s t) (u g i) -> b s g (t u) d i", s=4, t=BLOCK, u=HALVES, g=P // QUADRANT)
+        x_pieces = {}
+        for first, stop in TURNED_PARTS:
+            x_sb = x_pool.tile([P, stop - first, BATCH, 2, 2 * QUADRANT], BF16, name="x_pieces%d" % first)
+            for d in range(first, stop):
+                x_pieces[d] = (x_sb, d - first)
+            for g in range(P // QUADRANT):
+                for b in range(BATCH):
+                    for h in range(2):
+                        nc.sync.dma_start(
+                            out=x_sb[g * QUADRANT : (g + 1) * QUADRANT, :, b, h, :],
+                            in_=pieces[b, 2 + h, g][:, first:stop, :],
+                        )
 
         ident = consts.tile([P, P], F32)
         make_identity(nc, ident[:])
@@ -161,9 +179,10 @@ def tile_hydraencoderlayer_pa_t_kernel(tc, x, wk, wv, out):
             bank = next_bank([P, PAIR, HALVES, P])
             for j, t in enumerate(tiles):
                 xt[t] = (bank, j)
-                x_words = x_chunks[t // QUAD][:].bitcast(F32)
+                c, slot = divmod(t if t < TURNED_FIRST else t - TURNED, QUAD)
+                x_words = x_chunks[c][:].bitcast(F32)
                 for u in range(HALVES):
-                    w0 = (t % QUAD) * WORDS + u * P
+                    w0 = slot * WORDS + u * P
                     nc.tensor.transpose(bank[:, j, u, :], x_words[:, w0 : w0 + P], ident[:])
 
         def transpose_pair(n):
@@ -178,6 +197,15 @@ def tile_hydraencoderlayer_pa_t_kernel(tc, x, wk, wv, out):
             copy(
                 out=words[:, col : col + count, :, :],
                 in_=bank[:].rearrange("p j u r -> p j r u")[:, j : j + count, :, :],
+            )
+
+        def turn(first):
+            q, _ = batch_of(first)
+            grouped[q] = stage_tile(q, [P, batch_tiles(q) * P * PACK])
+            x_sb, d = x_pieces[first - TURNED_FIRST]
+            nc.vector.transpose(
+                out=grouped[q][:].bitcast(F32)[:, : QUAD * WORDS],
+                in_=x_sb[:, d : d + QUAD].rearrange("p d b h i -> p (d b h i)").bitcast(F32),
             )
 
         def regroup_pair(n, copy=on_vector):
@@ -385,6 +413,7 @@ def tile_hydraencoderlayer_pa_t_kernel(tc, x, wk, wv, out):
                 transpose_pair(pairs[0])
                 regroup_pair(pairs.pop())
                 quantise(QUAD * (k + 2) - PAIR, QUAD)
+            turned = bool(pairs) and TURNED_FIRST <= PAIR * pairs[0] < TURNED_FIRST + TURNED
             product(products[-1])
             folds_here = t0 - 1 in on_gpsimd
             add_pairs(k - 1, ADD_SQUARES if squares_here else ADD_FOLDS if folds_here else PAIR * E_BLOCKS)
@@ -398,12 +427,14 @@ def tile_hydraencoderlayer_pa_t_kernel(tc, x, wk, wv, out):
                     fold(k + 1)
             if squares_here:
                 square_on_gpsimd(t0 + QUAD - 1)
-            for n in pairs:
+            for n in [] if turned else pairs:
                 transpose_pair(n)
             if k == 3:
                 add_group(0)
             add_group(k - 2)
-            for n in pairs:
+            if turned:
+                turn(PAIR * pairs[0])
+            for n in [] if turned else pairs:
                 regroup_pair(n)
 
         warm_up(WARM_UP)

@@ -28,13 +28,16 @@ RING = 7
 AHEAD = 3
 LAG = 2
 ADD_SQUARES = 6
-ADD_FOLDS = 6
-G_CYCLE = 2
-G_OFF = 1
+ADD_ALL = 9
+G_EVERY_FROM = 4
+ADD_BOTH = 2
+COPY_A = 4
+COPY_B = 10
+COPY_C = 13
 LATE = 2
 FOLDED = 128
 G_FIRST = 0
-G_LAST = 12
+G_LAST = 11
 LAST_ADD = 2
 COPY_EVERY = 3
 COPY_AT = 1
@@ -101,12 +104,13 @@ def tile_hydraencoderlayer_pa_t_kernel(tc, x, wk, wv, out):
                             in_=pieces[b, 2 + h, g][:, first:stop, :],
                         )
 
-        ident = consts.tile([P, P], F32)
-        make_identity(nc, ident[:])
         out_cols = consts.tile([P, QUADRANT], F32, align_bytes=64)
         nc.vector.memset(out_cols[:], 0.0)
         zeros = consts.tile([P, DI], BF16)
         nc.vector.memset(zeros[:], 0.0)
+        ident = consts.tile([P, P], F32)
+        nc.vector.memset(ident[:], 0.0)
+        make_identity(nc, ident[:], nomemset=True)
         table_load = consts.tile([P, 1], F32)
         nc.scalar.activation(out=table_load[:], in_=zeros[:, :1], func=ACT.Abs_reciprocal_sqrt, bias=1.0)
 
@@ -153,14 +157,15 @@ def tile_hydraencoderlayer_pa_t_kernel(tc, x, wk, wv, out):
         rnorm = consts.tile([P, N_TILES], F32, name="rnorm")
         prod, pair_sum, summed, token_sums = {}, {}, set(), []
 
-        on_gpsimd = [q * QUAD + QUAD - 1 for q in range(G_FIRST, G_LAST + 1) if q % G_CYCLE != G_OFF]
+        on_gpsimd = [q * QUAD + QUAD - 1 for q in range(G_FIRST, G_LAST + 1) if q % 2 == 0 or q > G_EVERY_FROM]
         groups = [[t for t in range(QUAD + PAIR) if t not in on_gpsimd], []]
         for first in range(QUAD + PAIR, TAIL, QUAD):
             own = [t for t in range(first, first + QUAD) if t not in on_gpsimd]
             groups.append(own + [t for t in on_gpsimd if t == first - LATE * QUAD + 1])
-        late = [t for t in on_gpsimd if t > TAIL - 2 * QUAD]
-        for first in range(TAIL, N_TILES, PAIR):
-            groups.append([t for t in late if first == N_TILES - PAIR] + [first, first + 1])
+        groups[-1] += on_gpsimd[-1:]
+        norm_sets = list(groups)
+        last = groups.pop() + list(range(TAIL, N_TILES))
+        groups += [last[i : i + PAIR] for i in range(0, len(last), PAIR)]
         order = [t for group in groups for t in group]
         place = {t: (g, col) for g in range(len(groups)) for col, t in enumerate(groups[g])}
 
@@ -176,7 +181,7 @@ def tile_hydraencoderlayer_pa_t_kernel(tc, x, wk, wv, out):
             return stage.tile(shape, BF16, name={1: "stage_wv", 3: "stage_g"}.get(s, "stage%d" % (s % 3)), align_bytes=64)
 
         def transpose_tiles(tiles):
-            bank = next_bank([P, PAIR, HALVES, P])
+            bank = next_bank([P, PAIR, HALVES, P], ("x", tiles[0]))
             for j, t in enumerate(tiles):
                 xt[t] = (bank, j)
                 c, slot = divmod(t if t < TURNED_FIRST else t - TURNED, QUAD)
@@ -214,8 +219,8 @@ def tile_hydraencoderlayer_pa_t_kernel(tc, x, wk, wv, out):
         def quantise(first, count):
             q, j = batch_of(first)
             if q not in x_codes:
-                x_codes[q] = operands.tile([P, batch_tiles(q) * P], U32, name="x_codes", align_bytes=256)
-                x_scales[q] = operands.tile([P, batch_tiles(q) * P], U8, name="x_scales", align_bytes=256)
+                x_codes[q] = operands.tile([P, batch_tiles(q) * P], U32, name="x_codes%d" % batch_tiles(q), bufs=(1 if batch_tiles(q) > QUAD else None), align_bytes=256)
+                x_scales[q] = operands.tile([P, batch_tiles(q) * P], U8, name="x_scales%d" % batch_tiles(q), bufs=(1 if batch_tiles(q) > QUAD else None), align_bytes=256)
             cols = slice(j * P, (j + count) * P)
             nc.vector.quantize_mx(
                 out=x_codes[q][:, cols].bitcast(FP8X4),
@@ -245,7 +250,7 @@ def tile_hydraencoderlayer_pa_t_kernel(tc, x, wk, wv, out):
             v_ps[t] = mx_pass(t, "wv", after)
 
         def copy_a(t, copy=on_scalar):
-            a_sb[t] = work.tile([P, DI], F32, name="a_sb", bufs=QUAD * (LAG + 3))
+            a_sb[t] = work.tile([P, DI], F32, name="a_sb", bufs=QUAD * (LAG + 2) + PAIR)
             copy(out=a_sb[t][:], in_=a_ps[t][:])
 
         def norm_column(t):
@@ -303,7 +308,10 @@ def tile_hydraencoderlayer_pa_t_kernel(tc, x, wk, wv, out):
         def product(t, cols=slice(0, DI)):
             g, col = place[t]
             if g not in prod:
-                prod[g] = work.tile([P, QUAD + 1, DI], F32, name="prod")
+                if len(groups[g]) == PAIR:
+                    prod[g] = work.tile([P, PAIR, DI], F32, name="prod_pair", bufs=4)
+                else:
+                    prod[g] = work.tile([P, QUAD + 1, DI], F32, name="prod")
             nc.vector.scalar_tensor_tensor(
                 out=prod[g][:, col, cols],
                 in0=v_ps[t][:, cols],
@@ -375,9 +383,9 @@ def tile_hydraencoderlayer_pa_t_kernel(tc, x, wk, wv, out):
         def period(k):
             t0 = QUAD * k
             products = groups[k - 1]
-            late = [t for t in groups[k] if t in on_gpsimd]
+            late = [t for t in norm_sets[k] if t in on_gpsimd]
             squares_here = t0 + QUAD - 1 in on_gpsimd
-            by_vector = k % COPY_EVERY == COPY_AT or k == 13
+            by_vector = len(products) < QUAD or k in (COPY_A, COPY_B, COPY_C)
             for j in range(QUAD):
                 pass_a(t0 + j)
                 if j < QUAD - 1:
@@ -392,39 +400,39 @@ def tile_hydraencoderlayer_pa_t_kernel(tc, x, wk, wv, out):
             square_sum(t0)
             product(products[1])
             square_sum(t0 + 1)
-            if late:
-                sum_folded(late[0])
+            for t in late:
+                sum_folded(t)
             for t in products[2:-1]:
                 product(t)
             if by_vector:
                 copy_a(t0 + 2, on_vector)
                 copy_a(t0 + 3)
-                clamp_norms(groups[k])
+                clamp_norms(norm_sets[k])
                 square_sum(t0 + 2)
-                invert_norms(groups[k])
+                invert_norms(norm_sets[k])
             else:
                 copy_a(t0 + 2)
-                clamp_norms(groups[k])
+                clamp_norms(norm_sets[k])
                 copy_a(t0 + 3)
-                invert_norms(groups[k])
+                invert_norms(norm_sets[k])
                 square_sum(t0 + 2)
             pairs = [n for n in (2 * k + 5, 2 * k + 6) if n < N_TILES // PAIR]
             if len(pairs) < PAIR:
                 transpose_pair(pairs[0])
                 regroup_pair(pairs.pop())
                 quantise(QUAD * (k + 2) - PAIR, QUAD)
+                quantise(N_TILES - PAIR, PAIR)
             turned = bool(pairs) and TURNED_FIRST <= PAIR * pairs[0] < TURNED_FIRST + TURNED
             product(products[-1])
             folds_here = t0 - 1 in on_gpsimd
-            add_pairs(k - 1, ADD_SQUARES if squares_here else ADD_FOLDS if folds_here else PAIR * E_BLOCKS)
+            twice_here = k > 2 and t0 - QUAD - 1 in on_gpsimd
+            add_pairs(k - 1, ADD_ALL - 4 * squares_here - 2 * folds_here - twice_here if pairs else E_BLOCKS)
             if pairs:
                 quantise(QUAD * (k + 2) - PAIR, QUAD)
-            else:
-                quantise(N_TILES - PAIR, PAIR)
-            if folds_here:
+            if pairs:
                 fold(k)
-                if pairs:
-                    fold(k + 1)
+            if t0 - 1 == on_gpsimd[-1]:
+                fold(k + 1)
             if squares_here:
                 square_on_gpsimd(t0 + QUAD - 1)
             for n in [] if turned else pairs:
@@ -538,85 +546,88 @@ def tile_hydraencoderlayer_pa_t_kernel(tc, x, wk, wv, out):
         for k in range(3, 14):
             period(k)
 
-        pass_a(56)
-        pass_v(50)
-        pass_a(57)
-        pass_v(52)
-        pass_a(58)
-        pass_v(53)
-        pass_a(59)
+        pass_a(56, ("wk", 53))
+        pass_v(50, ("wv", 48))
+        pass_a(57, ("wv", 49))
+        pass_v(51, ("x", 62))
+        add_product(46)
+        add_product(49)
+        pass_a(58, ("wk", 54))
+        pass_v(52, ("wv", 39))
+        pass_a(59, ("wk", 55))
         copy_a(56)
-        pass_v(43, ("wk", 56))
         square_sum(55)
         product(50)
-        pass_v(54, ("wv", 50))
+        pass_v(53, ("wv", 50))
+        pass_v(43, ("wk", 56))
+        product(51)
+        add_pairs(13)
+        pass_a(60, ("wv", 51))
+        add_group(12)
         copy_a(57)
         product(52)
-        pass_a(60, ("wv", 52))
-        pass_v(55, ("wk", 57))
+        pass_v(47, ("wv", 52))
+        pass_a(61, ("wk", 57))
         clamp_norms([54, 55])
         square_sum(56)
         invert_norms([54, 55])
         product(53)
-        pass_a(61, ("wv", 53))
-        add_group(12)
-        product(43)
-        add_pairs(13)
-        fold(14)
+        add_pairs(14)
+        pass_v(54, ("wv", 53))
+        add_group(13)
         copy_a(58)
         square_sum(57)
+        product(43)
         copy_a(59, on_vector)
-        pass_v(56, ("wv", 43))
-        pass_v(57, ("wk", 58))
+        pass_v(55, ("wv", 43))
+        pass_v(56, ("wk", 58))
         pass_a(62, ("wk", 59))
+        add_group(14)
         square_sum(58)
         clamp_norms([56, 57])
         square_sum(59)
         invert_norms([56, 57])
-        product(54)
-        pass_a(63, ("wv", 54))
+        product(47)
+        add_pairs(15)
         copy_a(60, on_vector)
-        pass_v(58, ("wk", 60))
-        copy_a(61, on_vector)
-        pass_v(59, ("wk", 61))
-        add_group(13)
+        pass_v(57, ("wv", 47))
+        pass_a(63, ("wk", 60))
+        product(54)
+        pass_v(58, ("wv", 54))
+        add_group(15)
         product(55)
-        add_pairs(14)
+        add_pairs(16)
+        pass_v(59, ("wv", 55))
+        copy_a(61)
         square_sum(60)
         clamp_norms([58, 59])
         square_sum(61)
         invert_norms([58, 59])
-        pass_v(60, ("wv", 55))
         product(56)
+        pass_v(60, ("wk", 61))
         pass_v(61, ("wv", 56))
+        add_group(16)
         product(57)
-        add_pairs(15)
-        pass_v(51, ("wv", 57))
-        add_group(14)
+        add_pairs(17)
+        pass_v(62, ("wv", 57))
         square_sum(62, a_ps)
         clamp_norms([60, 61])
-        sum_folded(51)
-        invert_norms([60, 61])
         square_sum(63, a_ps)
+        invert_norms([60, 61])
         product(58)
-        pass_v(62, ("wv", 58))
+        pass_v(63, ("wv", 58))
         product(59)
-        add_pairs(16)
-        pass_v(63, ("wv", 59))
-        add_group(15)
-        clamp_norms([51, 62])
+        add_pairs(18)
+        add_group(17)
         copy_a(62)
-        invert_norms([51, 62])
-        clamp_norms([63])
+        clamp_norms([62, 63])
         copy_a(63)
-        invert_norms([63])
+        invert_norms([62, 63])
         product(60)
         add_product(60)
         product(61)
         add_product(61)
-        add_group(16)
-        product(51)
-        add_product(51)
+        add_group(18)
         product(62)
         add_product(62)
         for half in (slice(0, DI // 2), slice(DI // 2, DI)):

@@ -32,7 +32,7 @@ ADD_ALL = 9
 G_EVERY_FROM = 4
 ADD_BOTH = 2
 COPY_A = 4
-COPY_B = 10
+COPY_B = 4
 COPY_C = 13
 LATE = 2
 FOLDED = 128

@@ -29,10 +29,12 @@ AHEAD = 3
 LAG = 2
 ADD_SQUARES = 6
 ADD_ALL = 9
-G_EVERY_FROM = 4
+ADD_FULL = 0
+THIRD = 1
+G_EVERY_FROM = 2
 ADD_BOTH = 2
-COPY_A = 4
-COPY_B = 4
+COPY_A = 13
+COPY_B = 13
 COPY_C = 13
 LATE = 2
 FOLDED = 128
@@ -151,7 +153,7 @@ def tile_hydraencoderlayer_pa_t_kernel(tc, x, wk, wv, out):
 
         xt, grouped, x_codes, x_scales = {}, {}, {}, {}
         a_ps, v_ps, a_sb = {}, {}, {}
-        folds = {}
+        folds, gated, thrice = {}, set(), {}
         norm2 = consts.tile([P, N_TILES], F32, name="norm2")
         clamped = consts.tile([P, N_TILES], F32, name="clamped")
         rnorm = consts.tile([P, N_TILES], F32, name="rnorm")
@@ -263,6 +265,8 @@ def tile_hydraencoderlayer_pa_t_kernel(tc, x, wk, wv, out):
         def fold_tile(q):
             if q == 1 and q not in folds:
                 folds[q] = stage.tile([P, 7, FOLDED], F32, name="stage_g", align_bytes=64)
+            if q in gated and q not in folds:
+                folds[q] = stage.tile([P, 7, FOLDED], F32, name="stage%d" % ((q + 1) % 3), align_bytes=64)
             if q not in folds:
                 folds[q] = work.tile([P, 7, FOLDED], F32, name="folds", bufs=LATE + 1)
             return folds[q]
@@ -283,11 +287,21 @@ def tile_hydraencoderlayer_pa_t_kernel(tc, x, wk, wv, out):
                     op=ALU.add,
                 )
 
+        def fold_again(q):
+            t = QUAD * (q - 1) - 1
+            thrice[t] = work.tile([P, FOLDED // 2], F32, name="thrice")
+            twice = folds[q + 1][:, 0, :]
+            nc.gpsimd.tensor_tensor(out=thrice[t][:], in0=twice[:, : FOLDED // 2], in1=twice[:, FOLDED // 2 :], op=ALU.add)
+
         def sum_folded(t):
-            unread = work.tile([P, FOLDED], BF16, name="folded_unread")
+            if t == on_gpsimd[0]:
+                source = folds[PAIR][:, 1:3, :].rearrange("p i c -> p (i c)")
+            else:
+                source = thrice[t][:] if t in thrice else folds[t // QUAD + 3][:, 0, :]
+            unread = work.tile([P, source.shape[1]], BF16, name="folded_unread")
             nc.scalar.activation(
                 out=unread[:],
-                in_=folds[t // QUAD + 3][:, 0, :],
+                in_=source,
                 func=ACT.Identity,
                 accum_out=norm_column(t),
             )
@@ -309,7 +323,7 @@ def tile_hydraencoderlayer_pa_t_kernel(tc, x, wk, wv, out):
             g, col = place[t]
             if g not in prod:
                 if len(groups[g]) == PAIR:
-                    prod[g] = work.tile([P, PAIR, DI], F32, name="prod_pair", bufs=4)
+                    prod[g] = work.tile([P, PAIR, DI], F32, name="prod_pair", bufs=3)
                 else:
                     prod[g] = work.tile([P, QUAD + 1, DI], F32, name="prod")
             nc.vector.scalar_tensor_tensor(
@@ -426,11 +440,19 @@ def tile_hydraencoderlayer_pa_t_kernel(tc, x, wk, wv, out):
             product(products[-1])
             folds_here = t0 - 1 in on_gpsimd
             twice_here = k > 2 and t0 - QUAD - 1 in on_gpsimd
-            add_pairs(k - 1, ADD_ALL - 4 * squares_here - 2 * folds_here - twice_here if pairs else E_BLOCKS)
+            added = ADD_ALL - 4 * squares_here - 2 * folds_here - twice_here if pairs else E_BLOCKS
+            if squares_here and folds_here and twice_here:
+                added = ADD_FULL
+            if added:
+                add_pairs(k - 1, added)
+            else:
+                gated.add(k + 1)
             if pairs:
                 quantise(QUAD * (k + 2) - PAIR, QUAD)
             if pairs:
                 fold(k)
+            if THIRD and not added:
+                fold_again(k)
             if t0 - 1 == on_gpsimd[-1]:
                 fold(k + 1)
             if squares_here:
@@ -506,7 +528,6 @@ def tile_hydraencoderlayer_pa_t_kernel(tc, x, wk, wv, out):
         quantise(10, 4)
         square_on_gpsimd(3)
         fold(1)
-        fold(2)
         clamp_norms([4, 5])
         square_sum(6)
         invert_norms([4, 5])

@@ -22,32 +22,18 @@ HALVES = WORDS // P
 E_BLOCKS = DI // P
 PAIR = 2
 QUAD = 4
-N_QUADS = BATCH * TOKENS // (QUAD * P)
-N_TILES = N_QUADS * QUAD
+N_TILES = BATCH * TOKENS // P
+N_QUADS = N_TILES // QUAD
 RING = 7
-AHEAD = 3
-LAG = 2
-ADD_SQUARES = 6
-ADD_ALL = 9
-ADD_FULL = 0
-THIRD = 1
-G_EVERY_FROM = 2
-ADD_BOTH = 2
-COPY_A = 13
-COPY_B = 13
-COPY_C = 13
-LATE = 2
+STAGES = 3
+FIRST_PERIOD = 3
+LAST_PERIOD = N_QUADS - 3
+LAST_RUN = QUAD + PAIR
+TURNED, TURNED_FIRST, TURNED_PART = N_TILES // 2, 30, 8
+BLOCK = QUADRANT // HALVES
+SQUARED_QUADS = [q for q in range(LAST_PERIOD - 1) if q != 1]
 FOLDED = 128
-G_FIRST = 0
-G_LAST = 11
-LAST_ADD = 2
-COPY_EVERY = 3
-COPY_AT = 1
-TAIL = 54
-BLOCK = 16
-TURNED_FIRST = 30
-TURNED = 32
-TURNED_PARTS = ((0, 8), (8, 20), (20, 32))
+ADD_BESIDE_SQUARE, ADD_BESIDE_BOTH, ADD_BESIDE_FOLDS = 6, 3, 6
 WK_SPLIT = 336
 RUN = 4
 WARM_UP = 6
@@ -63,7 +49,7 @@ def tile_hydraencoderlayer_pa_t_kernel(tc, x, wk, wv, out):
         consts = ctx.enter_context(tc.tile_pool(name="consts", bufs=1))
         x_pool = ctx.enter_context(tc.tile_pool(name="x_pool", bufs=1))
         stage = ctx.enter_context(tc.tile_pool(name="stage", bufs=1))
-        operands = ctx.enter_context(tc.tile_pool(name="operands", bufs=AHEAD + LAG + 3))
+        operands = ctx.enter_context(tc.tile_pool(name="operands", bufs=8))
         work = ctx.enter_context(tc.tile_pool(name="work", bufs=3))
         psum = ctx.enter_context(tc.psum_pool(name="psum", bufs=1))
         on_vector = nc.vector.tensor_copy
@@ -79,31 +65,29 @@ def tile_hydraencoderlayer_pa_t_kernel(tc, x, wk, wv, out):
             )
 
         load_weight("wk", wk)
-        chunks = x.rearrange("b (q c t) k -> c (b q) (t k)", c=N_QUADS, t=QUAD)
-        x_chunks = []
-        for c in range(N_QUADS // 2):
-            x_sb = x_pool.tile([P, QUAD * D], BF16, name="x_rows%d" % c)
-            x_chunks.append(x_sb)
+        rows = x.rearrange("b (q c t) k -> c (b q) (t k)", c=N_QUADS, t=QUAD)
+        x_rows = []
+        for c in range((N_TILES - TURNED) // QUAD):
+            x_rows.append(x_pool.tile([P, QUAD * D], BF16, name="x_rows%d" % c))
             if c == 0:
                 for part in (slice(0, D), slice(D, PAIR * D), slice(PAIR * D, QUAD * D)):
-                    nc.sync.dma_start(out=x_sb[:, part], in_=chunks[c][:, part])
+                    nc.sync.dma_start(out=x_rows[c][:, part], in_=rows[c][:, part])
             else:
-                nc.sync.dma_start(out=x_sb[:], in_=chunks[c])
+                nc.sync.dma_start(out=x_rows[c][:], in_=rows[c])
             if c == 2:
                 load_weight("wv", wv)
 
         pieces = x.rearrange("b (d s t) (u g i) -> b s g (t u) d i", s=4, t=BLOCK, u=HALVES, g=P // QUADRANT)
-        x_pieces = {}
-        for first, stop in TURNED_PARTS:
-            x_sb = x_pool.tile([P, stop - first, BATCH, 2, 2 * QUADRANT], BF16, name="x_pieces%d" % first)
-            for d in range(first, stop):
-                x_pieces[d] = (x_sb, d - first)
+        x_pieces = []
+        for first in range(0, TURNED, TURNED_PART):
+            part = x_pool.tile([P, TURNED_PART, BATCH, 2, 2 * QUADRANT], BF16, name="x_pieces%d" % first)
+            x_pieces.append(part)
             for g in range(P // QUADRANT):
                 for b in range(BATCH):
                     for h in range(2):
                         nc.sync.dma_start(
-                            out=x_sb[g * QUADRANT : (g + 1) * QUADRANT, :, b, h, :],
-                            in_=pieces[b, 2 + h, g][:, first:stop, :],
+                            out=part[g * QUADRANT : (g + 1) * QUADRANT, :, b, h, :],
+                            in_=pieces[b, 2 + h, g][:, first : first + TURNED_PART, :],
                         )
 
         out_cols = consts.tile([P, QUADRANT], F32, align_bytes=64)
@@ -116,18 +100,68 @@ def tile_hydraencoderlayer_pa_t_kernel(tc, x, wk, wv, out):
         table_load = consts.tile([P, 1], F32)
         nc.scalar.activation(out=table_load[:], in_=zeros[:, :1], func=ACT.Abs_reciprocal_sqrt, bias=1.0)
 
+        def warm_up(count):
+            bank = psum.tile([P, DI], F32, name="token_sums")
+            for _ in range(count):
+                nc.tensor.matmul(out=bank[:], lhsT=zeros[:, :P], rhs=zeros[:], start=True, stop=True)
+
+        squared = [q * QUAD + QUAD - 1 for q in SQUARED_QUADS]
+        norm_sets = [[t for t in range(QUAD + PAIR) if t not in squared], []]
+        for g in range(PAIR, LAST_PERIOD + 1):
+            own = [t for t in range(QUAD * g - PAIR, QUAD * g + PAIR) if t not in squared]
+            norm_sets.append(own + [t for t in squared if t == QUAD * (g - PAIR) - 1])
+        norm_sets[-1].append(squared[-1])
+        rest = norm_sets[-1] + list(range(QUAD * LAST_PERIOD + PAIR, N_TILES))
+        groups = norm_sets[:-1] + [rest[i : i + PAIR] for i in range(0, len(rest), PAIR)]
+        order = [t for group in groups for t in group]
+        place = {t: (g, col) for g in range(len(groups)) for col, t in enumerate(groups[g])}
+
+        def run_of(t):
+            if t >= N_TILES - LAST_RUN:
+                return N_QUADS - 1, t - (N_TILES - LAST_RUN)
+            return divmod(t if t < PAIR * QUAD else t + PAIR, QUAD)
+
+        def run_tiles(r):
+            return LAST_RUN if r == N_QUADS - 1 else QUAD
+
+        def stage_tile(r, shape, dtype):
+            name = {1: "stage_wv", 3: "stage_squares"}.get(r, "stage%d" % (r % STAGES))
+            return stage.tile(shape, dtype, name=name, align_bytes=64)
+
+        taken, held, free = [], {}, list(range(RING))
+
+        def take_bank(holder, shape, in_turn):
+            bank = len(taken) % RING if in_turn else free[0]
+            taken.append(bank)
+            free.remove(bank)
+            held[holder] = bank
+            return psum.tile(shape, F32, name="bank%d" % bank)
+
+        def release_bank(holder):
+            free.append(held.pop(holder))
+
         w_grouped, w_codes, w_scales = {}, {}, {}
         for label in ("wk", "wv"):
             w_codes[label] = consts.tile([P, DI], U32, name="%s_codes" % label, align_bytes=256)
             w_scales[label] = consts.tile([P, DI], U8, name="%s_scales" % label, align_bytes=256)
-
         w_grouped["wk"] = consts.tile([P, DI, PACK], BF16, name="wk_grouped", align_bytes=64)
 
-        def interleave_weight(label, cols, copy):
-            by_column = w_raw[label][:].rearrange("q t (c i) -> q c t i", i=RUN)
-            side_by_side = w_grouped[label][:].rearrange("q (c i) t -> q c t i", i=RUN)
+        def interleave_wk(cols, copy):
+            by_column = w_raw["wk"][:].rearrange("q t (c i) -> q c t i", i=RUN)
+            side_by_side = w_grouped["wk"][:].rearrange("q (c i) t -> q c t i", i=RUN)
             runs = slice(cols.start // RUN, cols.stop // RUN)
             copy(out=side_by_side[:, runs], in_=by_column[:, runs])
+
+        def interleave_wv():
+            w_grouped["wv"] = stage_tile(1, [P, DI, PACK], BF16)
+            nc.gpsimd.tensor_scalar(
+                out=w_grouped["wv"][:],
+                in0=w_raw["wv"][:].rearrange("q t c -> q c t"),
+                scalar1=1.0,
+                scalar2=0.0,
+                op0=ALU.mult,
+                op1=ALU.add,
+            )
 
         def quantise_weight(label, cols):
             nc.vector.quantize_mx(
@@ -136,108 +170,61 @@ def tile_hydraencoderlayer_pa_t_kernel(tc, x, wk, wv, out):
                 in_=w_grouped[label][:, cols, :].rearrange("q c t -> q (c t)"),
             )
 
-        def warm_up(count):
-            bank = psum.tile([P, DI], F32, name="token_sums")
-            for _ in range(count):
-                nc.tensor.matmul(out=bank[:], lhsT=zeros[:, :P], rhs=zeros[:], start=True, stop=True)
+        x_banks, grouped, x_codes, x_scales = {}, {}, {}, {}
 
-        taken = []
+        def staged_words(first, count):
+            r, j = run_of(first)
+            if r not in grouped:
+                grouped[r] = stage_tile(r, [P, run_tiles(r) * P * PACK], BF16)
+            return grouped[r][:].bitcast(F32)[:, j * WORDS : (j + count) * WORDS]
 
-        bank_of = {}
-
-        def next_bank(shape, holder=None, after=None):
-            if after is None:
-                taken.append(len(taken) % RING)
-            bank_of[holder] = taken[-1] if after is None else bank_of[after]
-            return psum.tile(shape, F32, name="bank%d" % bank_of[holder])
-
-        xt, grouped, x_codes, x_scales = {}, {}, {}, {}
-        a_ps, v_ps, a_sb = {}, {}, {}
-        folds, gated, thrice = {}, set(), {}
-        norm2 = consts.tile([P, N_TILES], F32, name="norm2")
-        clamped = consts.tile([P, N_TILES], F32, name="clamped")
-        rnorm = consts.tile([P, N_TILES], F32, name="rnorm")
-        prod, pair_sum, summed, token_sums = {}, {}, set(), []
-
-        on_gpsimd = [q * QUAD + QUAD - 1 for q in range(G_FIRST, G_LAST + 1) if q % 2 == 0 or q > G_EVERY_FROM]
-        groups = [[t for t in range(QUAD + PAIR) if t not in on_gpsimd], []]
-        for first in range(QUAD + PAIR, TAIL, QUAD):
-            own = [t for t in range(first, first + QUAD) if t not in on_gpsimd]
-            groups.append(own + [t for t in on_gpsimd if t == first - LATE * QUAD + 1])
-        groups[-1] += on_gpsimd[-1:]
-        norm_sets = list(groups)
-        last = groups.pop() + list(range(TAIL, N_TILES))
-        groups += [last[i : i + PAIR] for i in range(0, len(last), PAIR)]
-        order = [t for group in groups for t in group]
-        place = {t: (g, col) for g in range(len(groups)) for col, t in enumerate(groups[g])}
-
-        def batch_of(t):
-            if t >= N_TILES - QUAD - PAIR:
-                return (N_QUADS - 1, t - (N_TILES - QUAD - PAIR))
-            return divmod(t if t < 2 * QUAD else t + PAIR, QUAD)
-
-        def batch_tiles(q):
-            return QUAD + PAIR if q == N_QUADS - 1 else QUAD
-
-        def stage_tile(s, shape):
-            return stage.tile(shape, BF16, name={1: "stage_wv", 3: "stage_g"}.get(s, "stage%d" % (s % 3)), align_bytes=64)
-
-        def transpose_tiles(tiles):
-            bank = next_bank([P, PAIR, HALVES, P], ("x", tiles[0]))
-            for j, t in enumerate(tiles):
-                xt[t] = (bank, j)
+        def transpose(first, count=PAIR):
+            x_banks[first] = take_bank(("x", first), [P, PAIR, HALVES, P], True)
+            for j in range(count):
+                t = first + j
                 c, slot = divmod(t if t < TURNED_FIRST else t - TURNED, QUAD)
-                x_words = x_chunks[c][:].bitcast(F32)
+                words = x_rows[c][:].bitcast(F32)
                 for u in range(HALVES):
                     w0 = slot * WORDS + u * P
-                    nc.tensor.transpose(bank[:, j, u, :], x_words[:, w0 : w0 + P], ident[:])
+                    nc.tensor.transpose(x_banks[first][:, j, u, :], words[:, w0 : w0 + P], ident[:])
 
-        def transpose_pair(n):
-            transpose_tiles([PAIR * n, PAIR * n + 1])
-
-        def regroup(first, count, copy):
-            q, col = batch_of(first)
-            if q not in grouped:
-                grouped[q] = stage_tile(q, [P, batch_tiles(q) * P * PACK])
-            words = grouped[q][:].bitcast(F32).rearrange("p (j r u) -> p j r u", r=P, u=HALVES)
-            bank, j = xt[first]
+        def regroup(first, count=PAIR, copy=on_vector):
             copy(
-                out=words[:, col : col + count, :, :],
-                in_=bank[:].rearrange("p j u r -> p j r u")[:, j : j + count, :, :],
+                out=staged_words(first, count).rearrange("p (j r u) -> p j r u", r=P, u=HALVES),
+                in_=x_banks[first][:].rearrange("p j u r -> p j r u")[:, :count, :, :],
             )
+            release_bank(("x", first))
 
         def turn(first):
-            q, _ = batch_of(first)
-            grouped[q] = stage_tile(q, [P, batch_tiles(q) * P * PACK])
-            x_sb, d = x_pieces[first - TURNED_FIRST]
+            part, d = divmod(first - TURNED_FIRST, TURNED_PART)
             nc.vector.transpose(
-                out=grouped[q][:].bitcast(F32)[:, : QUAD * WORDS],
-                in_=x_sb[:, d : d + QUAD].rearrange("p d b h i -> p (d b h i)").bitcast(F32),
+                out=staged_words(first, QUAD),
+                in_=x_pieces[part][:, d : d + QUAD].rearrange("p d b h i -> p (d b h i)").bitcast(F32),
             )
-
-        def regroup_pair(n, copy=on_vector):
-            regroup(PAIR * n, PAIR, copy)
 
         def quantise(first, count):
-            q, j = batch_of(first)
-            if q not in x_codes:
-                x_codes[q] = operands.tile([P, batch_tiles(q) * P], U32, name="x_codes%d" % batch_tiles(q), bufs=(1 if batch_tiles(q) > QUAD else None), align_bytes=256)
-                x_scales[q] = operands.tile([P, batch_tiles(q) * P], U8, name="x_scales%d" % batch_tiles(q), bufs=(1 if batch_tiles(q) > QUAD else None), align_bytes=256)
+            r, j = run_of(first)
+            if r not in x_codes:
+                size, bufs = run_tiles(r), 1 if run_tiles(r) > QUAD else None
+                x_codes[r] = operands.tile([P, size * P], U32, name="x_codes%d" % size, bufs=bufs, align_bytes=256)
+                x_scales[r] = operands.tile([P, size * P], U8, name="x_scales%d" % size, bufs=bufs, align_bytes=256)
             cols = slice(j * P, (j + count) * P)
             nc.vector.quantize_mx(
-                out=x_codes[q][:, cols].bitcast(FP8X4),
-                scales=x_scales[q][:, cols],
-                in_=grouped[q][:, j * P * PACK : (j + count) * P * PACK],
+                out=x_codes[r][:, cols].bitcast(FP8X4),
+                scales=x_scales[r][:, cols],
+                in_=grouped[r][:, j * P * PACK : (j + count) * P * PACK],
             )
 
-        def mx_pass(t, label, after):
-            bank = next_bank([P, DI], (label, t), after)
-            q, j = batch_of(t)
+        a_ps, v_ps, a_sb = {}, {}, {}
+
+        def mx_pass(t, label, in_turn):
+            bank = take_bank((label, t), [P, DI], in_turn)
+            r, j = run_of(t)
             cols = slice(j * P, (j + 1) * P)
             nc.tensor.matmul_mx(
                 out=bank[:],
-                lhsT=x_codes[q][:, cols].bitcast(FP8X4),
-                lhsT_scale=x_scales[q][:, cols],
+                lhsT=x_codes[r][:, cols].bitcast(FP8X4),
+                lhsT_scale=x_scales[r][:, cols],
                 rhs=w_codes[label][:].bitcast(FP8X4),
                 rhs_scale=w_scales[label][:],
                 start=True,
@@ -245,69 +232,62 @@ def tile_hydraencoderlayer_pa_t_kernel(tc, x, wk, wv, out):
             )
             return bank
 
-        def pass_a(t, after=None):
-            a_ps[t] = mx_pass(t, "wk", after)
+        def pass_a(t, in_turn=True):
+            a_ps[t] = mx_pass(t, "wk", in_turn)
 
-        def pass_v(t, after=None):
-            v_ps[t] = mx_pass(t, "wv", after)
+        def pass_v(t, in_turn=True):
+            v_ps[t] = mx_pass(t, "wv", in_turn)
 
         def copy_a(t, copy=on_scalar):
-            a_sb[t] = work.tile([P, DI], F32, name="a_sb", bufs=QUAD * (LAG + 2) + PAIR)
+            a_sb[t] = work.tile([P, DI], F32, name="a_sb", bufs=QUAD * QUAD + PAIR)
             copy(out=a_sb[t][:], in_=a_ps[t][:])
+            release_bank(("wk", t))
 
-        def norm_column(t):
-            return norm2[:, order.index(t) : order.index(t) + 1]
-
-        def square_sum(t, source=a_sb):
-            unread = work.tile([P, DI], BF16, name="squares")
-            nc.scalar.activation(out=unread[:], in_=source[t][:], func=ACT.Square, accum_out=norm_column(t))
-
-        def fold_tile(q):
-            if q == 1 and q not in folds:
-                folds[q] = stage.tile([P, 7, FOLDED], F32, name="stage_g", align_bytes=64)
-            if q in gated and q not in folds:
-                folds[q] = stage.tile([P, 7, FOLDED], F32, name="stage%d" % ((q + 1) % 3), align_bytes=64)
-            if q not in folds:
-                folds[q] = work.tile([P, 7, FOLDED], F32, name="folds", bufs=LATE + 1)
-            return folds[q]
-
-        def square_on_gpsimd(t):
-            blocks = a_sb[t][:].rearrange("p (i c) -> p i c", c=FOLDED)
-            nc.gpsimd.tensor_tensor(out=fold_tile(t // QUAD + 1)[:, 3:, :], in0=blocks, in1=blocks, op=ALU.mult)
-
-        def fold(q):
-            once, twice = QUAD * q - 1 in on_gpsimd, QUAD * (q - 1) - 1 in on_gpsimd
-            pieces = slice(0 if twice else 1, 3 if once else 1)
-            if once or twice:
-                source = fold_tile(q)[:, 1:, :].rearrange("p (i h) c -> p h i c", h=2)
-                nc.gpsimd.tensor_tensor(
-                    out=fold_tile(q + 1)[:, pieces, :],
-                    in0=source[:, 0, pieces, :],
-                    in1=source[:, 1, pieces, :],
-                    op=ALU.add,
-                )
-
-        def fold_again(q):
-            t = QUAD * (q - 1) - 1
-            thrice[t] = work.tile([P, FOLDED // 2], F32, name="thrice")
-            twice = folds[q + 1][:, 0, :]
-            nc.gpsimd.tensor_tensor(out=thrice[t][:], in0=twice[:, : FOLDED // 2], in1=twice[:, FOLDED // 2 :], op=ALU.add)
-
-        def sum_folded(t):
-            if t == on_gpsimd[0]:
-                source = folds[PAIR][:, 1:3, :].rearrange("p i c -> p (i c)")
-            else:
-                source = thrice[t][:] if t in thrice else folds[t // QUAD + 3][:, 0, :]
-            unread = work.tile([P, source.shape[1]], BF16, name="folded_unread")
-            nc.scalar.activation(
-                out=unread[:],
-                in_=source,
-                func=ACT.Identity,
-                accum_out=norm_column(t),
-            )
+        norm2 = consts.tile([P, N_TILES], F32, name="norm2")
+        clamped = consts.tile([P, N_TILES], F32, name="clamped")
+        rnorm = consts.tile([P, N_TILES], F32, name="rnorm")
+        folds, left_to_sum = {}, {}
 
         def columns(tiles):
             return slice(order.index(tiles[0]), order.index(tiles[-1]) + 1)
+
+        def square_sum(t, source=a_sb):
+            unread = work.tile([P, DI], BF16, name="squares")
+            nc.scalar.activation(out=unread[:], in_=source[t][:], func=ACT.Square, accum_out=norm2[:, columns([t])])
+
+        def open_folds(q, run=None):
+            if run is None:
+                folds[q] = work.tile([P, 7, FOLDED], F32, name="folds")
+            else:
+                folds[q] = stage_tile(run, [P, 7, FOLDED], F32)
+
+        def square_on_gpsimd(t):
+            blocks = a_sb[t][:].rearrange("p (i c) -> p i c", c=FOLDED)
+            nc.gpsimd.tensor_tensor(out=folds[t // QUAD + 1][:, 3:, :], in0=blocks, in1=blocks, op=ALU.mult)
+
+        def fold(q, once, twice):
+            blocks = slice(0 if twice else 1, 3 if once else 1)
+            halves = folds[q][:, 1:, :].rearrange("p (i h) c -> p h i c", h=2)
+            nc.gpsimd.tensor_tensor(
+                out=folds[q + 1][:, blocks, :], in0=halves[:, 0, blocks, :], in1=halves[:, 1, blocks, :], op=ALU.add
+            )
+            if twice:
+                left_to_sum[QUAD * (q - 1) - 1] = folds[q + 1][:, 0, :]
+            if once:
+                left_to_sum[QUAD * q - 1] = folds[q + 1][:, 1:3, :].rearrange("p i c -> p (i c)")
+
+        def fold_again(t):
+            twice, thrice = left_to_sum[t], work.tile([P, FOLDED // 2], F32, name="thrice")
+            nc.gpsimd.tensor_tensor(
+                out=thrice[:], in0=twice[:, : FOLDED // 2], in1=twice[:, FOLDED // 2 :], op=ALU.add
+            )
+            left_to_sum[t] = thrice[:]
+
+        def sum_folded(t):
+            unread = work.tile([P, left_to_sum[t].shape[1]], BF16, name="folded_unread")
+            nc.scalar.activation(
+                out=unread[:], in_=left_to_sum[t], func=ACT.Identity, accum_out=norm2[:, columns([t])]
+            )
 
         def clamp_norms(tiles):
             cols = columns(tiles)
@@ -319,13 +299,13 @@ def tile_hydraencoderlayer_pa_t_kernel(tc, x, wk, wv, out):
                 out=rnorm[:, cols], in_=clamped[:, cols], func=ACT.Abs_reciprocal_sqrt, bias=EPS * EPS
             )
 
+        prod, pair_sum, summed, token_sums = {}, {}, set(), []
+
         def product(t, cols=slice(0, DI)):
             g, col = place[t]
             if g not in prod:
-                if len(groups[g]) == PAIR:
-                    prod[g] = work.tile([P, PAIR, DI], F32, name="prod_pair", bufs=3)
-                else:
-                    prod[g] = work.tile([P, QUAD + 1, DI], F32, name="prod")
+                width = PAIR if len(groups[g]) == PAIR else QUAD + 1
+                prod[g] = work.tile([P, width, DI], F32, name="prod%d" % width)
             nc.vector.scalar_tensor_tensor(
                 out=prod[g][:, col, cols],
                 in0=v_ps[t][:, cols],
@@ -334,18 +314,21 @@ def tile_hydraencoderlayer_pa_t_kernel(tc, x, wk, wv, out):
                 op0=ALU.mult,
                 op1=ALU.mult,
             )
+            if cols.stop == DI:
+                release_bank(("wv", t))
 
-        def add_pairs(g, blocks=PAIR * E_BLOCKS):
+        def pair_ends(g):
             count = len(groups[g])
-            pairs = min(PAIR, count // 2)
-            blocks = min(blocks, pairs * E_BLOCKS)
+            return (count - min(PAIR, count // 2)) * E_BLOCKS, count * E_BLOCKS
+
+        def add_pairs(g, blocks=E_BLOCKS):
             flat = prod[g][:].rearrange("p j e -> p (j e)")
-            ends = ((count - pairs) * DI, count * DI)
-            pair_sum[g] = (work.tile([P, PAIR * DI], F32, name="pair_sum", bufs=3), blocks)
+            first_end, second_end = pair_ends(g)
+            pair_sum[g] = (work.tile([P, PAIR * DI], F32, name="pair_sum"), blocks)
             nc.gpsimd.tensor_tensor(
                 out=pair_sum[g][0][:, : blocks * P],
-                in0=flat[:, ends[0] - blocks * P : ends[0]],
-                in1=flat[:, ends[1] - blocks * P : ends[1]],
+                in0=flat[:, (first_end - blocks) * P : first_end * P],
+                in1=flat[:, (second_end - blocks) * P : second_end * P],
                 op=ALU.add,
             )
 
@@ -354,71 +337,48 @@ def tile_hydraencoderlayer_pa_t_kernel(tc, x, wk, wv, out):
             if opens:
                 token_sums.append(psum.tile([P, E_BLOCKS, P], F32, name="token_sums"))
             nc.tensor.matmul(
-                out=token_sums[0][:, i, :],
-                lhsT=source,
-                rhs=ident[:],
-                is_transpose=True,
-                start=opens,
-                stop=closes,
+                out=token_sums[0][:, i, :], lhsT=source, rhs=ident[:], is_transpose=True, start=opens, stop=closes
             )
 
-        def add_tile(source, closes=False):
+        def add_product(t, closes=False):
+            g, col = place[t]
+            summed.add(t)
             for i in range(E_BLOCKS):
-                add_block(source[:, i * P : (i + 1) * P], i, closes and i == E_BLOCKS - 1)
+                add_block(prod[g][:, col, i * P : (i + 1) * P], i, closes and i == E_BLOCKS - 1)
 
         def add_group(g):
             sums, added = pair_sum.get(g, (None, 0))
-            count = len(groups[g])
-            pairs = min(PAIR, count // 2)
-            ends = ((count - pairs) * E_BLOCKS, count * E_BLOCKS)
-            for block in range(count * E_BLOCKS):
+            for block in range(len(groups[g]) * E_BLOCKS):
                 j, i = divmod(block, E_BLOCKS)
-                if (g, j) not in summed and not any(end - added <= block < end for end in ends):
+                if groups[g][j] not in summed and not any(end - added <= block < end for end in pair_ends(g)):
                     add_block(prod[g][:, j, i * P : (i + 1) * P], i)
             for block in range(added):
                 add_block(sums[:, block * P : (block + 1) * P], (block - added) % E_BLOCKS)
 
-        def add_product(t, closes=False):
-            g, col = place[t]
-            summed.add((g, col))
-            add_tile(prod[g][:, col, :], closes)
-
-        def interleave_wv():
-            w_grouped["wv"] = stage_tile(1, [P, DI, PACK])
-            nc.gpsimd.tensor_scalar(
-                out=w_grouped["wv"][:],
-                in0=w_raw["wv"][:].rearrange("q t c -> q c t"),
-                scalar1=1.0,
-                scalar2=0.0,
-                op0=ALU.mult,
-                op1=ALU.add,
-            )
-
         def period(k):
             t0 = QUAD * k
-            products = groups[k - 1]
-            late = [t for t in norm_sets[k] if t in on_gpsimd]
-            squares_here = t0 + QUAD - 1 in on_gpsimd
-            by_vector = len(products) < QUAD or k in (COPY_A, COPY_B, COPY_C)
-            for j in range(QUAD):
+            products, last = groups[k - 1], k == LAST_PERIOD
+            squares, once, twice = (QUAD * q + QUAD - 1 in squared for q in (k, k - 1, k - 2))
+            for j in range(QUAD - 1):
                 pass_a(t0 + j)
-                if j < QUAD - 1:
-                    pass_v(products[j])
+                pass_v(products[j])
+            pass_a(t0 + QUAD - 1)
             copy_a(t0)
             for t in products[QUAD - 1 :]:
                 pass_v(t)
             copy_a(t0 + 1)
-            if t0 - 1 not in on_gpsimd:
+            if not once:
                 square_sum(t0 - 1)
             product(products[0])
             square_sum(t0)
             product(products[1])
             square_sum(t0 + 1)
-            for t in late:
-                sum_folded(t)
-            for t in products[2:-1]:
+            for t in norm_sets[k]:
+                if t in squared:
+                    sum_folded(t)
+            for t in products[PAIR:-1]:
                 product(t)
-            if by_vector:
+            if len(products) < QUAD or last:
                 copy_a(t0 + 2, on_vector)
                 copy_a(t0 + 3)
                 clamp_norms(norm_sets[k])
@@ -430,53 +390,52 @@ def tile_hydraencoderlayer_pa_t_kernel(tc, x, wk, wv, out):
                 copy_a(t0 + 3)
                 invert_norms(norm_sets[k])
                 square_sum(t0 + 2)
-            pairs = [n for n in (2 * k + 5, 2 * k + 6) if n < N_TILES // PAIR]
-            if len(pairs) < PAIR:
-                transpose_pair(pairs[0])
-                regroup_pair(pairs.pop())
-                quantise(QUAD * (k + 2) - PAIR, QUAD)
-                quantise(N_TILES - PAIR, PAIR)
-            turned = bool(pairs) and TURNED_FIRST <= PAIR * pairs[0] < TURNED_FIRST + TURNED
+            ahead = QUAD * (k + 3) - PAIR
+            if last:
+                transpose(ahead)
+                regroup(ahead)
+                quantise(ahead - QUAD, QUAD)
+                quantise(ahead, PAIR)
+                product(products[-1])
+                add_pairs(k - 1)
+                add_group(k - 2)
+                return
             product(products[-1])
-            folds_here = t0 - 1 in on_gpsimd
-            twice_here = k > 2 and t0 - QUAD - 1 in on_gpsimd
-            added = ADD_ALL - 4 * squares_here - 2 * folds_here - twice_here if pairs else E_BLOCKS
-            if squares_here and folds_here and twice_here:
-                added = ADD_FULL
-            if added:
-                add_pairs(k - 1, added)
+            if squares and once and twice:
+                quantise(ahead - QUAD, QUAD)
+                open_folds(k + 1, k + 2)
+                fold(k, once, twice)
+                fold_again(t0 - QUAD - 1)
             else:
-                gated.add(k + 1)
-            if pairs:
-                quantise(QUAD * (k + 2) - PAIR, QUAD)
-            if pairs:
-                fold(k)
-            if THIRD and not added:
-                fold_again(k)
-            if t0 - 1 == on_gpsimd[-1]:
-                fold(k + 1)
-            if squares_here:
+                add_pairs(k - 1, ADD_BESIDE_BOTH if squares else ADD_BESIDE_FOLDS)
+                quantise(ahead - QUAD, QUAD)
+                open_folds(k + 1)
+                fold(k, once, twice)
+            if squares:
                 square_on_gpsimd(t0 + QUAD - 1)
-            for n in [] if turned else pairs:
-                transpose_pair(n)
-            if k == 3:
+            else:
+                open_folds(k + 2)
+                fold(k + 1, False, True)
+            turned = ahead >= TURNED_FIRST
+            firsts = [] if turned else [ahead, ahead + PAIR]
+            for first in firsts:
+                transpose(first)
+            if k == FIRST_PERIOD:
                 add_group(0)
             add_group(k - 2)
             if turned:
-                turn(PAIR * pairs[0])
-            for n in [] if turned else pairs:
-                regroup_pair(n)
+                turn(ahead)
+            for first in firsts:
+                regroup(first)
 
         warm_up(WARM_UP)
-        interleave_weight("wk", slice(0, DI // 2), on_vector)
-        interleave_weight("wk", slice(DI // 2, WK_SPLIT), on_vector)
-        interleave_weight("wk", slice(WK_SPLIT, DI), on_scalar)
+        interleave_wk(slice(0, DI // 2), on_vector)
+        interleave_wk(slice(DI // 2, WK_SPLIT), on_vector)
+        interleave_wk(slice(WK_SPLIT, DI), on_scalar)
         quantise_weight("wk", slice(0, DI // 2))
         quantise_weight("wk", slice(DI // 2, DI))
-        transpose_tiles([0])
-        transpose_tiles([1])
-        transpose_tiles([2])
-        transpose_tiles([3])
+        for t in range(QUAD):
+            transpose(t, 1)
         for t in range(PAIR):
             regroup(t, 1, on_scalar)
             quantise(t, 1)
@@ -484,50 +443,52 @@ def tile_hydraencoderlayer_pa_t_kernel(tc, x, wk, wv, out):
         regroup(3, 1, on_scalar)
         pass_a(0)
         pass_a(1)
-        quantise(2, 2)
-        transpose_pair(2)
-        transpose_pair(3)
+        quantise(2, PAIR)
+        transpose(4)
+        transpose(6)
         square_sum(0, a_ps)
         copy_a(0)
         copy_a(1, on_vector)
         pass_a(2)
         pass_a(3)
-        regroup_pair(2)
+        regroup(4)
         square_sum(1)
-        regroup_pair(3)
+        regroup(6)
         copy_a(2)
-        transpose_pair(4)
-        transpose_pair(5)
-        quantise(4, 2)
-        quantise(6, 2)
+        transpose(8)
+        transpose(10)
+        quantise(4, PAIR)
+        quantise(6, PAIR)
+
         interleave_wv()
         copy_a(3)
         square_sum(2)
-        pass_a(4)
-        pass_a(5)
-        pass_a(6)
-        pass_a(7)
-        regroup_pair(4)
+        for t in range(QUAD, PAIR * QUAD):
+            pass_a(t)
+        regroup(8)
         copy_a(4)
         clamp_norms([0, 2])
-        regroup_pair(5)
-        transpose_pair(6)
-        transpose_pair(7)
+        regroup(10)
+        transpose(12)
+        transpose(14)
         copy_a(5, on_vector)
         copy_a(6)
         invert_norms([0, 2])
-        regroup_pair(6)
+        regroup(12)
         square_sum(4)
-        regroup_pair(7)
+        regroup(14)
         warm_up(KEEP_WARM)
-        transpose_pair(8)
+        transpose(16)
         square_sum(5)
         copy_a(7)
-        quantise(8, 2)
+
+        quantise(8, PAIR)
         quantise_weight("wv", slice(0, DI))
-        quantise(10, 4)
+        quantise(10, QUAD)
+        open_folds(1, 3)
         square_on_gpsimd(3)
-        fold(1)
+        open_folds(2)
+        fold(1, True, False)
         clamp_norms([4, 5])
         square_sum(6)
         invert_norms([4, 5])
@@ -535,7 +496,7 @@ def tile_hydraencoderlayer_pa_t_kernel(tc, x, wk, wv, out):
         pass_a(9)
         pass_v(0)
         pass_v(1)
-        regroup_pair(8)
+        regroup(16)
         copy_a(8)
         square_sum(7)
         product(0)
@@ -548,61 +509,69 @@ def tile_hydraencoderlayer_pa_t_kernel(tc, x, wk, wv, out):
         square_sum(8)
         pass_v(5)
         add_product(0)
-        transpose_pair(9)
-        transpose_pair(10)
         product(2)
-        product(4)
-        product(5)
-        add_pairs(0, ADD_SQUARES)
-        quantise(14, 4)
+        transpose(18)
         square_sum(9)
         copy_a(10)
-        clamp_norms(groups[2])
+        transpose(20)
+        product(4)
+        product(5)
+        add_pairs(0, ADD_BESIDE_SQUARE)
+        quantise(14, QUAD)
+        clamp_norms(norm_sets[2])
         copy_a(11)
-        invert_norms(groups[2])
+        invert_norms(norm_sets[2])
+        open_folds(3)
         square_on_gpsimd(11)
-        regroup_pair(9)
-        regroup_pair(10)
+        regroup(18)
+        regroup(20)
         square_sum(10)
-        for k in range(3, 14):
+
+        for k in range(FIRST_PERIOD, LAST_PERIOD + 1):
             period(k)
 
-        pass_a(56, ("wk", 53))
-        pass_v(50, ("wv", 48))
-        pass_a(57, ("wv", 49))
-        pass_v(51, ("x", 62))
+        def ahead_a(t):
+            pass_a(t, False)
+
+        def ahead_v(t):
+            pass_v(t, False)
+
+        ahead_a(56)
+        ahead_v(50)
+        ahead_a(57)
+        ahead_v(51)
         add_product(46)
         add_product(49)
-        pass_a(58, ("wk", 54))
-        pass_v(52, ("wv", 39))
-        pass_a(59, ("wk", 55))
+        ahead_a(58)
+        ahead_v(52)
+        ahead_a(59)
         copy_a(56)
         square_sum(55)
         product(50)
-        pass_v(53, ("wv", 50))
-        pass_v(43, ("wk", 56))
+        ahead_v(53)
+        ahead_v(43)
         product(51)
         add_pairs(13)
-        pass_a(60, ("wv", 51))
+        ahead_a(60)
         add_group(12)
         copy_a(57)
         product(52)
-        pass_v(47, ("wv", 52))
-        pass_a(61, ("wk", 57))
+        ahead_v(47)
+        ahead_a(61)
         clamp_norms([54, 55])
         square_sum(56)
         invert_norms([54, 55])
         product(53)
         add_pairs(14)
-        pass_v(54, ("wv", 53))
+        ahead_v(54)
         add_group(13)
         copy_a(58)
         square_sum(57)
         product(43)
         copy_a(59, on_vector)
-        pass_v(55, ("wv", 43))
-        pass_v(56, ("wk", 58))
-        pass_a(62, ("wk", 59))
+        ahead_v(55)
+        ahead_v(56)
+        ahead_a(62)
         add_group(14)
         square_sum(58)
         clamp_norms([56, 57])
@@ -611,32 +580,32 @@ def tile_hydraencoderlayer_pa_t_kernel(tc, x, wk, wv, out):
         product(47)
         add_pairs(15)
         copy_a(60, on_vector)
-        pass_v(57, ("wv", 47))
-        pass_a(63, ("wk", 60))
+        ahead_v(57)
+        ahead_a(63)
         product(54)
-        pass_v(58, ("wv", 54))
+        ahead_v(58)
         add_group(15)
         product(55)
         add_pairs(16)
-        pass_v(59, ("wv", 55))
+        ahead_v(59)
         copy_a(61)
         square_sum(60)
         clamp_norms([58, 59])
         square_sum(61)
         invert_norms([58, 59])
         product(56)
-        pass_v(60, ("wk", 61))
-        pass_v(61, ("wv", 56))
+        ahead_v(60)
+        ahead_v(61)
         add_group(16)
         product(57)
         add_pairs(17)
-        pass_v(62, ("wv", 57))
+        ahead_v(62)
         square_sum(62, a_ps)
         clamp_norms([60, 61])
         square_sum(63, a_ps)
         invert_norms([60, 61])
         product(58)
-        pass_v(63, ("wv", 58))
+        ahead_v(63)
         product(59)
         add_pairs(18)
         add_group(17)
@@ -644,10 +613,9 @@ def tile_hydraencoderlayer_pa_t_kernel(tc, x, wk, wv, out):
         clamp_norms([62, 63])
         copy_a(63)
         invert_norms([62, 63])
-        product(60)
-        add_product(60)
-        product(61)
-        add_product(61)
+        for t in (60, 61):
+            product(t)
+            add_product(t)
         add_group(18)
         product(62)
         add_product(62)
@@ -663,8 +631,7 @@ def tile_hydraencoderlayer_pa_t_kernel(tc, x, wk, wv, out):
         )
         out_rows = consts.tile([P, QUADRANT], F32, align_bytes=64)
         nc.vector.transpose(out=out_rows[:], in_=out_cols[:])
-        pieces = out.rearrange("b o (i g q) -> g (b o i) q", i=E_BLOCKS, q=QUADRANT)
+        stores = out.rearrange("b o (i g q) -> g (b o i) q", i=E_BLOCKS, q=QUADRANT)
         for g in range(P // QUADRANT):
             queue = nc.sync if g % 2 == 0 else nc.scalar
-            rows = slice(g * QUADRANT, g * QUADRANT + BATCH * E_BLOCKS)
-            queue.dma_start(out=pieces[g], in_=out_rows[rows, :])
+            queue.dma_start(out=stores[g], in_=out_rows[g * QUADRANT : g * QUADRANT + BATCH * E_BLOCKS, :])

@@ -530,98 +530,64 @@ def tile_hydraencoderlayer_pa_t_kernel(tc, x, wk, wv, out):
         for k in range(FIRST_PERIOD, LAST_PERIOD + 1):
             period(k)
 
-        def ahead_a(t):
-            pass_a(t, False)
+        first_tile, first_pair = QUAD * (LAST_PERIOD + 1), LAST_PERIOD
+        pairs = groups[first_pair:]
+        by_vector = (first_tile + 3, first_tile + 4)
+        from_psum = pairs[-1]
 
-        def ahead_v(t):
-            pass_v(t, False)
+        v_tiles = [t for pair in pairs for t in pair]
+        passes = [(pass_v, t) for t in v_tiles]
+        for i, t in enumerate(range(first_tile, N_TILES)):
+            passes.insert(PAIR * i, (pass_a, t))
 
-        ahead_a(56)
-        ahead_v(50)
-        ahead_a(57)
-        ahead_v(51)
-        add_product(46)
-        add_product(49)
-        ahead_a(58)
-        ahead_v(52)
-        ahead_a(59)
-        copy_a(56)
-        square_sum(55)
-        product(50)
-        ahead_v(53)
-        ahead_v(43)
-        product(51)
-        add_pairs(13)
-        ahead_a(60)
-        add_group(12)
-        copy_a(57)
-        product(52)
-        ahead_v(47)
-        ahead_a(61)
-        clamp_norms([54, 55])
-        square_sum(56)
-        invert_norms([54, 55])
-        product(53)
-        add_pairs(14)
-        ahead_v(54)
-        add_group(13)
-        copy_a(58)
-        square_sum(57)
-        product(43)
-        copy_a(59, on_vector)
-        ahead_v(55)
-        ahead_v(56)
-        ahead_a(62)
-        add_group(14)
-        square_sum(58)
-        clamp_norms([56, 57])
-        square_sum(59)
-        invert_norms([56, 57])
-        product(47)
-        add_pairs(15)
-        copy_a(60, on_vector)
-        ahead_v(57)
-        ahead_a(63)
-        product(54)
-        ahead_v(58)
-        add_group(15)
-        product(55)
-        add_pairs(16)
-        ahead_v(59)
-        copy_a(61)
-        square_sum(60)
-        clamp_norms([58, 59])
-        square_sum(61)
-        invert_norms([58, 59])
-        product(56)
-        ahead_v(60)
-        ahead_v(61)
-        add_group(16)
-        product(57)
-        add_pairs(17)
-        ahead_v(62)
-        square_sum(62, a_ps)
-        clamp_norms([60, 61])
-        square_sum(63, a_ps)
-        invert_norms([60, 61])
-        product(58)
-        ahead_v(63)
-        product(59)
-        add_pairs(18)
-        add_group(17)
-        copy_a(62)
-        clamp_norms([62, 63])
-        copy_a(63)
-        invert_norms([62, 63])
-        for t in (60, 61):
-            product(t)
+        def run_ahead(count):
+            for _ in range(min(count, len(free), len(passes))):
+                mx, t = passes.pop(0)
+                mx(t, False)
+
+        scalar_work = []
+        for t in range(first_tile, N_TILES):
+            if t not in by_vector and t not in from_psum:
+                scalar_work.append((copy_a, t))
+            scalar_work.append((square_sum, t - 1))
+        scalar_work += [(square_sum, N_TILES - 1)] + [(copy_a, t) for t in from_psum]
+        norm_pairs = {scalar_work.index((square_sum, pair[1])): pair for pair in pairs if pair[1] >= first_tile - 1}
+        vector_work = [(product, t) for t in v_tiles]
+        for late, t in zip(squared[-PAIR:], by_vector):
+            vector_work.insert(vector_work.index((product, late)) + 1, (copy_a, t))
+
+        run_ahead(QUAD)
+        for t in groups[first_pair - 1][::PAIR]:
             add_product(t)
-        add_group(18)
-        product(62)
-        add_product(62)
+        run_ahead(RING)
+        for i, (work_v, t) in enumerate(vector_work[:-1]):
+            if i < len(scalar_work):
+                work_s, s = scalar_work[i]
+                if work_s is square_sum and s in from_psum:
+                    square_sum(s, a_ps)
+                else:
+                    work_s(s)
+                if i - 2 in norm_pairs:
+                    invert_norms(norm_pairs[i - 2])
+                if i - 1 in norm_pairs:
+                    clamp_norms(norm_pairs[i - 1])
+                run_ahead(1)
+            if work_v is copy_a:
+                copy_a(t, on_vector)
+            else:
+                product(t)
+            run_ahead(1)
+            g, col = place[t]
+            if work_v is product and g >= len(groups) - PAIR:
+                add_product(t)
+                if t == N_TILES - QUAD + 1:
+                    add_group(g - 1)
+            elif work_v is product and col == PAIR - 1:
+                add_pairs(g)
+                add_group(g - 1)
         for half in (slice(0, DI // 2), slice(DI // 2, DI)):
-            product(63, half)
-        add_product(63, closes=True)
+            product(N_TILES - 1, half)
+        add_product(N_TILES - 1, closes=True)
 
         nc.vector.tensor_reduce(
             out=out_cols[:, : BATCH * E_BLOCKS].rearrange("e (b i) -> e i b", b=BATCH),

@@ -402,8 +402,9 @@ def tile_hydraencoderlayer_pa_t_kernel(tc, x, wk, wv, out):
                 return
             product(products[-1])
             if squares and once and twice:
+                add_pairs(k - 1, 1)
                 quantise(ahead - QUAD, QUAD)
-                open_folds(k + 1, k + 2)
+                open_folds(k + 1)
                 fold(k, once, twice)
                 fold_again(t0 - QUAD - 1)
             else:

@@ -22,22 +22,25 @@ HALVES = WORDS // P
 E_BLOCKS = DI // P
 PAIR = 2
 QUAD = 4
+SIX = 6
 N_TILES = BATCH * TOKENS // P
-N_QUADS = N_TILES // QUAD
-RING = 7
-STAGES = 3
-FIRST_PERIOD = 3
-LAST_PERIOD = N_QUADS - 3
-LAST_RUN = QUAD + PAIR
-TURNED, TURNED_FIRST, TURNED_PART = N_TILES // 2, 30, 8
 BLOCK = QUADRANT // HALVES
-SQUARED_QUADS = [q for q in range(LAST_PERIOD - 1) if q != 1]
-FOLDED = 128
-ADD_BESIDE_SQUARE, ADD_BESIDE_BOTH, ADD_BESIDE_FOLDS = 6, 3, 6
+ROWS = QUADRANT
+ROW_TILES = BLOCK
+N_RUNS = (N_TILES - ROW_TILES) // SIX
+RING = 6
+FIRST = ROW_TILES - PAIR
 WK_SPLIT = 336
 RUN = 4
 WARM_UP = 6
 KEEP_WARM = 3
+WV_BEHIND = 1
+LAST_WINDOW = 6
+TAIL_COPIES = (60,)
+LEAD = 1
+ADDS = 6
+TAIL_PLACES = (7,)
+NO_ADD = 1
 
 FLOPS = 2 * 2 * BATCH * TOKENS * D * DI
 
@@ -49,8 +52,8 @@ def tile_hydraencoderlayer_pa_t_kernel(tc, x, wk, wv, out):
         consts = ctx.enter_context(tc.tile_pool(name="consts", bufs=1))
         x_pool = ctx.enter_context(tc.tile_pool(name="x_pool", bufs=1))
         stage = ctx.enter_context(tc.tile_pool(name="stage", bufs=1))
-        operands = ctx.enter_context(tc.tile_pool(name="operands", bufs=8))
-        work = ctx.enter_context(tc.tile_pool(name="work", bufs=3))
+        operands = ctx.enter_context(tc.tile_pool(name="operands", bufs=3))
+        work = ctx.enter_context(tc.tile_pool(name="work", bufs=2))
         psum = ctx.enter_context(tc.psum_pool(name="psum", bufs=1))
         on_vector = nc.vector.tensor_copy
         on_scalar = nc.scalar.copy
@@ -65,30 +68,32 @@ def tile_hydraencoderlayer_pa_t_kernel(tc, x, wk, wv, out):
             )
 
         load_weight("wk", wk)
-        rows = x.rearrange("b (q c t) k -> c (b q) (t k)", c=N_QUADS, t=QUAD)
+        rows = x.rearrange("b (q c t) k -> c (b q) (t k)", q=ROWS, t=QUAD)
         x_rows = []
-        for c in range((N_TILES - TURNED) // QUAD):
+        for c in range(ROW_TILES // QUAD):
             x_rows.append(x_pool.tile([P, QUAD * D], BF16, name="x_rows%d" % c))
             if c == 0:
                 for part in (slice(0, D), slice(D, PAIR * D), slice(PAIR * D, QUAD * D)):
                     nc.sync.dma_start(out=x_rows[c][:, part], in_=rows[c][:, part])
             else:
                 nc.sync.dma_start(out=x_rows[c][:], in_=rows[c])
-            if c == 2:
+            if c == WV_BEHIND:
                 load_weight("wv", wv)
 
-        pieces = x.rearrange("b (d s t) (u g i) -> b s g (t u) d i", s=4, t=BLOCK, u=HALVES, g=P // QUADRANT)
-        x_pieces = []
-        for first in range(0, TURNED, TURNED_PART):
-            part = x_pool.tile([P, TURNED_PART, BATCH, 2, 2 * QUADRANT], BF16, name="x_pieces%d" % first)
-            x_pieces.append(part)
-            for g in range(P // QUADRANT):
-                for b in range(BATCH):
-                    for h in range(2):
-                        nc.sync.dma_start(
-                            out=part[g * QUADRANT : (g + 1) * QUADRANT, :, b, h, :],
-                            in_=pieces[b, 2 + h, g][:, first : first + TURNED_PART, :],
-                        )
+        pieces = x.rearrange("b (d s t) (u g i) -> b s g (t u) d i", d=ROWS, t=BLOCK, u=HALVES, g=P // QUADRANT)
+        size = SIX * PAIR
+        parts = [(s, d, size) for s in range(1, QUAD) for d in (0, size)]
+        parts += [(s, PAIR * size, ROWS - PAIR * size) for s in range(1, QUAD)]
+        x_pieces = x_pool.tile([P, N_RUNS * size, BATCH, 2 * QUADRANT], BF16, name="x_pieces", align_bytes=64)
+        filled = 0
+        for s, d, count in parts:
+            for b in range(BATCH):
+                for g in (0, 2, 1, 3):
+                    nc.sync.dma_start(
+                        out=x_pieces[g * QUADRANT : (g + 1) * QUADRANT, filled : filled + count, b, :],
+                        in_=pieces[b, s, g][:, d : d + count, :],
+                    )
+            filled += count
 
         out_cols = consts.tile([P, QUADRANT], F32, align_bytes=64)
         nc.vector.memset(out_cols[:], 0.0)
@@ -97,65 +102,57 @@ def tile_hydraencoderlayer_pa_t_kernel(tc, x, wk, wv, out):
         ident = consts.tile([P, P], F32)
         nc.vector.memset(ident[:], 0.0)
         make_identity(nc, ident[:], nomemset=True)
+        by_batch = consts.tile([P, P], F32)
+        nc.gpsimd.tensor_scalar(
+            out=by_batch[:].rearrange("p (b h t) -> p b h t", b=BATCH, h=PAIR),
+            in0=ident[:].rearrange("p (h b t) -> p b h t", b=BATCH, h=PAIR),
+            scalar1=1.0,
+            scalar2=0.0,
+            op0=ALU.mult,
+            op1=ALU.add,
+        )
         table_load = consts.tile([P, 1], F32)
         nc.scalar.activation(out=table_load[:], in_=zeros[:, :1], func=ACT.Abs_reciprocal_sqrt, bias=1.0)
 
         def warm_up(count):
-            bank = psum.tile([P, DI], F32, name="token_sums")
+            bank = psum.tile([P, DI], F32, name="sums0")
             for _ in range(count):
                 nc.tensor.matmul(out=bank[:], lhsT=zeros[:, :P], rhs=zeros[:], start=True, stop=True)
 
-        squared = [q * QUAD + QUAD - 1 for q in SQUARED_QUADS]
-        norm_sets = [[t for t in range(QUAD + PAIR) if t not in squared], []]
-        for g in range(PAIR, LAST_PERIOD + 1):
-            own = [t for t in range(QUAD * g - PAIR, QUAD * g + PAIR) if t not in squared]
-            norm_sets.append(own + [t for t in squared if t == QUAD * (g - PAIR) - 1])
-        norm_sets[-1].append(squared[-1])
-        rest = norm_sets[-1] + list(range(QUAD * LAST_PERIOD + PAIR, N_TILES))
-        groups = norm_sets[:-1] + [rest[i : i + PAIR] for i in range(0, len(rest), PAIR)]
-        order = [t for group in groups for t in group]
-        place = {t: (g, col) for g in range(len(groups)) for col, t in enumerate(groups[g])}
+        held, free = {}, list(range(RING))
 
-        def run_of(t):
-            if t >= N_TILES - LAST_RUN:
-                return N_QUADS - 1, t - (N_TILES - LAST_RUN)
-            return divmod(t if t < PAIR * QUAD else t + PAIR, QUAD)
-
-        def run_tiles(r):
-            return LAST_RUN if r == N_QUADS - 1 else QUAD
-
-        def stage_tile(r, shape, dtype):
-            name = {1: "stage_wv", 3: "stage_squares"}.get(r, "stage%d" % (r % STAGES))
-            return stage.tile(shape, dtype, name=name, align_bytes=64)
-
-        taken, held, free = [], {}, list(range(RING))
-
-        def take_bank(holder, shape, in_turn):
-            bank = len(taken) % RING if in_turn else free[0]
-            taken.append(bank)
-            free.remove(bank)
-            held[holder] = bank
-            return psum.tile(shape, F32, name="bank%d" % bank)
+        def take_bank(holder, shape):
+            held[holder] = free.pop(0)
+            return psum.tile(shape, F32, name="bank%d" % held[holder])
 
         def release_bank(holder):
             free.append(held.pop(holder))
+
+        stages = [stage.tile([P, SIX * D], BF16, name="stage%d" % i, align_bytes=64) for i in range(PAIR)]
+        row_stage = stage.tile([P, ROW_TILES * D], BF16, name="row_stage", align_bytes=64)
+
+        def staged(first, count):
+            if first < ROW_TILES:
+                return row_stage[:, first * D : (first + count) * D]
+            r, j = divmod(first - ROW_TILES, SIX)
+            return stages[r % PAIR][:, j * D : (j + count) * D]
 
         w_grouped, w_codes, w_scales = {}, {}, {}
         for label in ("wk", "wv"):
             w_codes[label] = consts.tile([P, DI], U32, name="%s_codes" % label, align_bytes=256)
             w_scales[label] = consts.tile([P, DI], U8, name="%s_scales" % label, align_bytes=256)
-        w_grouped["wk"] = consts.tile([P, DI, PACK], BF16, name="wk_grouped", align_bytes=64)
+        w_grouped["wk"] = consts.tile([P, DI, PACK], BF16, name="wk_grouped", align_bytes=64)[:]
 
         def interleave_wk(cols, copy):
             by_column = w_raw["wk"][:].rearrange("q t (c i) -> q c t i", i=RUN)
-            side_by_side = w_grouped["wk"][:].rearrange("q (c i) t -> q c t i", i=RUN)
+            side_by_side = w_grouped["wk"].rearrange("q (c i) t -> q c t i", i=RUN)
             runs = slice(cols.start // RUN, cols.stop // RUN)
             copy(out=side_by_side[:, runs], in_=by_column[:, runs])
 
-        def interleave_wv():
-            w_grouped["wv"] = stage_tile(1, [P, DI, PACK], BF16)
+        def interleave_wv(first):
+            w_grouped["wv"] = staged(first, QUAD).rearrange("q (c t) -> q c t", t=PACK)
             nc.gpsimd.tensor_scalar(
-                out=w_grouped["wv"][:],
+                out=w_grouped["wv"],
                 in0=w_raw["wv"][:].rearrange("q t c -> q c t"),
                 scalar1=1.0,
                 scalar2=0.0,
@@ -170,19 +167,17 @@ def tile_hydraencoderlayer_pa_t_kernel(tc, x, wk, wv, out):
                 in_=w_grouped[label][:, cols, :].rearrange("q c t -> q (c t)"),
             )
 
-        x_banks, grouped, x_codes, x_scales = {}, {}, {}, {}
+        x_banks, x_codes, x_scales = {}, {}, {}
 
-        def staged_words(first, count):
-            r, j = run_of(first)
-            if r not in grouped:
-                grouped[r] = stage_tile(r, [P, run_tiles(r) * P * PACK], BF16)
-            return grouped[r][:].bitcast(F32)[:, j * WORDS : (j + count) * WORDS]
+        def run_of(t):
+            if t < ROW_TILES:
+                return (QUAD, t // QUAD), t % QUAD
+            return (SIX, (t - ROW_TILES) // SIX), (t - ROW_TILES) % SIX
 
         def transpose(first, count=PAIR):
-            x_banks[first] = take_bank(("x", first), [P, PAIR, HALVES, P], True)
+            x_banks[first] = take_bank(("x", first), [P, PAIR, HALVES, P])
             for j in range(count):
-                t = first + j
-                c, slot = divmod(t if t < TURNED_FIRST else t - TURNED, QUAD)
+                c, slot = divmod(first + j, QUAD)
                 words = x_rows[c][:].bitcast(F32)
                 for u in range(HALVES):
                     w0 = slot * WORDS + u * P
@@ -190,41 +185,36 @@ def tile_hydraencoderlayer_pa_t_kernel(tc, x, wk, wv, out):
 
         def regroup(first, count=PAIR, copy=on_vector):
             copy(
-                out=staged_words(first, count).rearrange("p (j r u) -> p j r u", r=P, u=HALVES),
+                out=staged(first, count).bitcast(F32).rearrange("p (j r u) -> p j r u", r=P, u=HALVES),
                 in_=x_banks[first][:].rearrange("p j u r -> p j r u")[:, :count, :, :],
             )
             release_bank(("x", first))
 
-        def turn(first):
-            part, d = divmod(first - TURNED_FIRST, TURNED_PART)
+        def turn(r):
             nc.vector.transpose(
-                out=staged_words(first, QUAD),
-                in_=x_pieces[part][:, d : d + QUAD].rearrange("p d b h i -> p (d b h i)").bitcast(F32),
+                out=stages[r % PAIR][:].bitcast(F32),
+                in_=x_pieces[:, r * size : (r + 1) * size].rearrange("p n b i -> p (n b i)").bitcast(F32),
             )
 
         def quantise(first, count):
-            r, j = run_of(first)
-            if r not in x_codes:
-                size, bufs = run_tiles(r), 1 if run_tiles(r) > QUAD else None
-                x_codes[r] = operands.tile([P, size * P], U32, name="x_codes%d" % size, bufs=bufs, align_bytes=256)
-                x_scales[r] = operands.tile([P, size * P], U8, name="x_scales%d" % size, bufs=bufs, align_bytes=256)
+            run, j = run_of(first)
+            if run not in x_codes:
+                width = run[0]
+                x_codes[run] = operands.tile([P, width * P], U32, name="x_codes%d" % width, bufs=4, align_bytes=256)
+                x_scales[run] = operands.tile([P, width * P], U8, name="x_scales%d" % width, bufs=4, align_bytes=256)
             cols = slice(j * P, (j + count) * P)
-            nc.vector.quantize_mx(
-                out=x_codes[r][:, cols].bitcast(FP8X4),
-                scales=x_scales[r][:, cols],
-                in_=grouped[r][:, j * P * PACK : (j + count) * P * PACK],
-            )
+            nc.vector.quantize_mx(out=x_codes[run][:, cols].bitcast(FP8X4), scales=x_scales[run][:, cols], in_=staged(first, count))
 
-        a_ps, v_ps, a_sb = {}, {}, {}
+        a_ps, v_ps, a_sb, a_pairs = {}, {}, {}, {}
 
-        def mx_pass(t, label, in_turn):
-            bank = take_bank((label, t), [P, DI], in_turn)
-            r, j = run_of(t)
+        def mx_pass(t, label):
+            bank = take_bank((label, t), [P, DI])
+            run, j = run_of(t)
             cols = slice(j * P, (j + 1) * P)
             nc.tensor.matmul_mx(
                 out=bank[:],
-                lhsT=x_codes[r][:, cols].bitcast(FP8X4),
-                lhsT_scale=x_scales[r][:, cols],
+                lhsT=x_codes[run][:, cols].bitcast(FP8X4),
+                lhsT_scale=x_scales[run][:, cols],
                 rhs=w_codes[label][:].bitcast(FP8X4),
                 rhs_scale=w_scales[label][:],
                 start=True,
@@ -232,62 +222,85 @@ def tile_hydraencoderlayer_pa_t_kernel(tc, x, wk, wv, out):
             )
             return bank
 
-        def pass_a(t, in_turn=True):
-            a_ps[t] = mx_pass(t, "wk", in_turn)
+        def pass_a(t):
+            a_ps[t] = mx_pass(t, "wk")
 
-        def pass_v(t, in_turn=True):
-            v_ps[t] = mx_pass(t, "wv", in_turn)
+        def pass_v(t):
+            v_ps[t] = mx_pass(t, "wv")
+
+        def pair_of(w):
+            first = FIRST - 1 + SIX * w if w >= 0 else FIRST - PAIR + SIX * w
+            return [first, first + 1]
+
+        def period_tiles(w):
+            return list(range(FIRST + SIX * w, FIRST + SIX * (w + 1)))
+
+        windows = range(-1, LAST_WINDOW + 1)
+        on_gpsimd = {t: w for w in windows for t in pair_of(w)}
+        groups = [[0, 1, 2], [3, 4, 5]]
+        for w in range(-1, N_RUNS - 1):
+            tiles = [t for t in period_tiles(w)[:4] if t not in on_gpsimd]
+            groups.append(([period_tiles(w - 1)[4]] + pair_of(w - 1) if w > -1 else []) + tiles)
+        done = [t for group in groups for t in group]
+        rest = [t for t in range(N_TILES) if t not in done and t not in on_gpsimd]
+        late = [t for t in on_gpsimd if t not in done]
+        groups.append(rest[:1] + late + rest[1:3])
+        groups.append(rest[3:SIX])
+        groups += [rest[i : i + PAIR] for i in range(SIX, len(rest), PAIR)]
+        order = [t for group in groups for t in group]
 
         def copy_a(t, copy=on_scalar):
-            a_sb[t] = work.tile([P, DI], F32, name="a_sb", bufs=QUAD * QUAD + PAIR)
-            copy(out=a_sb[t][:], in_=a_ps[t][:])
+            if t in on_gpsimd:
+                w = on_gpsimd[t]
+                if w not in a_pairs:
+                    a_pairs[w] = work.tile([P, PAIR, DI], F32, name="a_pair", bufs=4)
+                a_sb[t] = a_pairs[w][:, pair_of(w).index(t), :]
+            else:
+                a_sb[t] = work.tile([P, DI], F32, name="a_sb", bufs=10)[:]
+            copy(out=a_sb[t], in_=a_ps[t][:])
             release_bank(("wk", t))
 
         norm2 = consts.tile([P, N_TILES], F32, name="norm2")
         clamped = consts.tile([P, N_TILES], F32, name="clamped")
         rnorm = consts.tile([P, N_TILES], F32, name="rnorm")
-        folds, left_to_sum = {}, {}
+        once, twice, thrice = {}, {}, {}
 
         def columns(tiles):
             return slice(order.index(tiles[0]), order.index(tiles[-1]) + 1)
 
-        def square_sum(t, source=a_sb):
-            unread = work.tile([P, DI], BF16, name="squares")
-            nc.scalar.activation(out=unread[:], in_=source[t][:], func=ACT.Square, accum_out=norm2[:, columns([t])])
+        def square_sum(t, from_psum=False):
+            unread = work.tile([P, DI], BF16, name="squares", bufs=3)
+            source = a_ps[t][:] if from_psum else a_sb[t]
+            nc.scalar.activation(out=unread[:], in_=source, func=ACT.Square, accum_out=norm2[:, columns([t])])
 
-        def open_folds(q, run=None):
-            if run is None:
-                folds[q] = work.tile([P, 7, FOLDED], F32, name="folds")
-            else:
-                folds[q] = stage_tile(run, [P, 7, FOLDED], F32)
+        def fold(target, source):
+            halves = source.rearrange("p j (h c) -> p h j c", h=2)
+            nc.gpsimd.tensor_tensor(out=target, in0=halves[:, 0], in1=halves[:, 1], op=ALU.add)
 
-        def square_on_gpsimd(t):
-            blocks = a_sb[t][:].rearrange("p (i c) -> p i c", c=FOLDED)
-            nc.gpsimd.tensor_tensor(out=folds[t // QUAD + 1][:, 3:, :], in0=blocks, in1=blocks, op=ALU.mult)
+        def window(w, place):
+            squares = None
+            if w - 1 in windows:
+                twice[w - 1] = place.bitcast(F32)[:, : PAIR * DI // 4].rearrange("p (j c) -> p j c", j=PAIR)
+                fold(twice[w - 1], once[w - 1][:])
+            if w in windows:
+                if w - 1 in windows:
+                    squares = work.tile([P, PAIR, DI], F32, name="pair_squares")[:]
+                else:
+                    squares = place.bitcast(F32)[:, : PAIR * DI].rearrange("p (j c) -> p j c", j=PAIR)
+                nc.gpsimd.tensor_tensor(out=squares, in0=a_pairs[w][:], in1=a_pairs[w][:], op=ALU.mult)
+            if w - 1 in windows:
+                thrice[w - 1] = work.tile([P, PAIR, DI // 8], F32, name="thrice")
+                fold(thrice[w - 1][:], twice[w - 1])
+            if w in windows:
+                once[w] = work.tile([P, PAIR, DI // 2], F32, name="once")
+                fold(once[w][:], squares)
 
-        def fold(q, once, twice):
-            blocks = slice(0 if twice else 1, 3 if once else 1)
-            halves = folds[q][:, 1:, :].rearrange("p (i h) c -> p h i c", h=2)
-            nc.gpsimd.tensor_tensor(
-                out=folds[q + 1][:, blocks, :], in0=halves[:, 0, blocks, :], in1=halves[:, 1, blocks, :], op=ALU.add
-            )
-            if twice:
-                left_to_sum[QUAD * (q - 1) - 1] = folds[q + 1][:, 0, :]
-            if once:
-                left_to_sum[QUAD * q - 1] = folds[q + 1][:, 1:3, :].rearrange("p i c -> p (i c)")
-
-        def fold_again(t):
-            twice, thrice = left_to_sum[t], work.tile([P, FOLDED // 2], F32, name="thrice")
-            nc.gpsimd.tensor_tensor(
-                out=thrice[:], in0=twice[:, : FOLDED // 2], in1=twice[:, FOLDED // 2 :], op=ALU.add
-            )
-            left_to_sum[t] = thrice[:]
-
-        def sum_folded(t):
-            unread = work.tile([P, left_to_sum[t].shape[1]], BF16, name="folded_unread")
-            nc.scalar.activation(
-                out=unread[:], in_=left_to_sum[t], func=ACT.Identity, accum_out=norm2[:, columns([t])]
-            )
+        def sum_folded(w):
+            for j, t in enumerate(pair_of(w)):
+                unread = work.tile([P, DI // 8], BF16, name="folded_unread")
+                nc.scalar.activation(
+                    out=unread[:], in_=thrice[w][:, j, :], func=ACT.Identity, accum_out=norm2[:, columns([t])]
+                )
 
         def clamp_norms(tiles):
             cols = columns(tiles)
@@ -299,15 +312,13 @@ def tile_hydraencoderlayer_pa_t_kernel(tc, x, wk, wv, out):
                 out=rnorm[:, cols], in_=clamped[:, cols], func=ACT.Abs_reciprocal_sqrt, bias=EPS * EPS
             )
 
-        prod, pair_sum, summed, token_sums = {}, {}, set(), []
+        prod, sums, to_sum = {}, [], []
 
         def product(t, cols=slice(0, DI)):
-            g, col = place[t]
-            if g not in prod:
-                width = PAIR if len(groups[g]) == PAIR else QUAD + 1
-                prod[g] = work.tile([P, width, DI], F32, name="prod%d" % width)
+            if t not in prod:
+                prod[t] = work.tile([P, DI], F32, name="prod", bufs=10)
             nc.vector.scalar_tensor_tensor(
-                out=prod[g][:, col, cols],
+                out=prod[t][:, cols],
                 in0=v_ps[t][:, cols],
                 scalar=rnorm[:, columns([t])],
                 in1=a_sb[t][:, cols],
@@ -316,118 +327,96 @@ def tile_hydraencoderlayer_pa_t_kernel(tc, x, wk, wv, out):
             )
             if cols.stop == DI:
                 release_bank(("wv", t))
+                to_sum.append(t)
 
-        def pair_ends(g):
-            count = len(groups[g])
-            return (count - min(PAIR, count // 2)) * E_BLOCKS, count * E_BLOCKS
+        def add_pair(t, other):
+            total = work.tile([P, DI], F32, name="pair_sum", bufs=ADDS)
+            nc.gpsimd.tensor_tensor(out=total[:], in0=prod[t][:], in1=prod[other][:], op=ALU.add)
+            prod[t] = total
+            to_sum.remove(other)
 
-        def add_pairs(g, blocks=E_BLOCKS):
-            flat = prod[g][:].rearrange("p j e -> p (j e)")
-            first_end, second_end = pair_ends(g)
-            pair_sum[g] = (work.tile([P, PAIR * DI], F32, name="pair_sum"), blocks)
-            nc.gpsimd.tensor_tensor(
-                out=pair_sum[g][0][:, : blocks * P],
-                in0=flat[:, (first_end - blocks) * P : first_end * P],
-                in1=flat[:, (second_end - blocks) * P : second_end * P],
-                op=ALU.add,
-            )
+        opened = set()
 
-        def add_block(source, i, closes=False):
-            opens = not token_sums
-            if opens:
-                token_sums.append(psum.tile([P, E_BLOCKS, P], F32, name="token_sums"))
+        def add_block(t, i, closes=False):
+            half, block = divmod(i, PAIR)
+            if not sums:
+                sums.extend(psum.tile([P, E_BLOCKS, P], F32, name="sums%d" % h) for h in range(PAIR))
             nc.tensor.matmul(
-                out=token_sums[0][:, i, :], lhsT=source, rhs=ident[:], is_transpose=True, start=opens, stop=closes
+                out=sums[half][:, block, :],
+                lhsT=prod[t][:, i * P : (i + 1) * P],
+                rhs=(ident if t < ROW_TILES else by_batch)[:],
+                is_transpose=True,
+                start=half not in opened,
+                stop=closes,
             )
+            opened.add(half)
 
-        def add_product(t, closes=False):
-            g, col = place[t]
-            summed.add(t)
-            for i in range(E_BLOCKS):
-                add_block(prod[g][:, col, i * P : (i + 1) * P], i, closes and i == E_BLOCKS - 1)
+        def add_products(count):
+            for t in to_sum[:count]:
+                for i in (0, 2, 1, 3):
+                    add_block(t, i)
+            to_sum[:] = to_sum[count:]
 
-        def add_group(g):
-            sums, added = pair_sum.get(g, (None, 0))
-            for block in range(len(groups[g]) * E_BLOCKS):
-                j, i = divmod(block, E_BLOCKS)
-                if groups[g][j] not in summed and not any(end - added <= block < end for end in pair_ends(g)):
-                    add_block(prod[g][:, j, i * P : (i + 1) * P], i)
-            for block in range(added):
-                add_block(sums[:, block * P : (block + 1) * P], (block - added) % E_BLOCKS)
+        queue = list(order)
 
-        def period(k):
-            t0 = QUAD * k
-            products, last = groups[k - 1], k == LAST_PERIOD
-            squares, once, twice = (QUAD * q + QUAD - 1 in squared for q in (k, k - 1, k - 2))
-            for j in range(QUAD - 1):
-                pass_a(t0 + j)
-                pass_v(products[j])
-            pass_a(t0 + QUAD - 1)
-            copy_a(t0)
-            for t in products[QUAD - 1 :]:
-                pass_v(t)
-            copy_a(t0 + 1)
-            if not once:
-                square_sum(t0 - 1)
-            product(products[0])
-            square_sum(t0)
-            product(products[1])
-            square_sum(t0 + 1)
-            for t in norm_sets[k]:
-                if t in squared:
-                    sum_folded(t)
-            for t in products[PAIR:-1]:
-                product(t)
-            if len(products) < QUAD or last:
-                copy_a(t0 + 2, on_vector)
-                copy_a(t0 + 3)
-                clamp_norms(norm_sets[k])
-                square_sum(t0 + 2)
-                invert_norms(norm_sets[k])
+        def period(w, copies_first=False, copies_last=False):
+            tiles, group = period_tiles(w), groups[w + 3]
+            count = SIX - copies_first - copies_last
+            products = queue[:count]
+            queue[:] = queue[count:]
+            vector_work = [(product, t) for t in products]
+            scalar_work = [(copy_a, tiles[0]), (copy_a, tiles[1])]
+            if tiles[0] not in on_gpsimd:
+                scalar_work.append((square_sum, tiles[0]))
+            for j in range(PAIR, SIX - 1):
+                scalar_work += [(copy_a, tiles[j]), (square_sum, tiles[j - 1])]
+            if copies_first:
+                vector_work.insert(0, (copy_on_vector, tiles[0]))
+                scalar_work.pop(0)
+            if copies_last:
+                vector_work.append((copy_on_vector, tiles[-1]))
+            passes = []
+            for j in range(SIX):
+                passes += [(pass_a, tiles[j])] + [(pass_v, t) for t in products[j : j + 1]]
+            if copies_last:
+                pass
+
+            def run_ahead():
+                while free and passes:
+                    mx, t = passes.pop(0)
+                    mx(t)
+
+            if copies_last:
+                scalar_work[1:1] = [(clamp_norms, groups[1])]
+                scalar_work[3:3] = [(invert_norms, groups[1])]
+            if copies_first:
+                scalar_work.insert(1, (invert_norms, groups[w + 2]))
+            run_ahead()
+            for i in range(len(scalar_work)):
+                for step, t in [scalar_work[i]] + vector_work[:-1][i : i + 1]:
+                    step(t)
+                    run_ahead()
+                if i == 0:
+                    window(w, staged(ROW_TILES + SIX * w, QUAD) if w >= 0 else staged(ROW_TILES - QUAD, QUAD))
+            add_products(SIX)
+            turn(w + 1)
+            if w - 1 in windows:
+                sum_folded(w - 1)
+            if copies_last:
+                square_sum(tiles[-PAIR])
+                clamp_norms(group)
             else:
-                copy_a(t0 + 2)
-                clamp_norms(norm_sets[k])
-                copy_a(t0 + 3)
-                invert_norms(norm_sets[k])
-                square_sum(t0 + 2)
-            ahead = QUAD * (k + 3) - PAIR
-            if last:
-                transpose(ahead)
-                regroup(ahead)
-                quantise(ahead - QUAD, QUAD)
-                quantise(ahead, PAIR)
-                product(products[-1])
-                add_pairs(k - 1)
-                add_group(k - 2)
-                return
-            product(products[-1])
-            if squares and once and twice:
-                add_pairs(k - 1, 1)
-                quantise(ahead - QUAD, QUAD)
-                open_folds(k + 1)
-                fold(k, once, twice)
-                fold_again(t0 - QUAD - 1)
-            else:
-                add_pairs(k - 1, ADD_BESIDE_BOTH if squares else ADD_BESIDE_FOLDS)
-                quantise(ahead - QUAD, QUAD)
-                open_folds(k + 1)
-                fold(k, once, twice)
-            if squares:
-                square_on_gpsimd(t0 + QUAD - 1)
-            else:
-                open_folds(k + 2)
-                fold(k + 1, False, True)
-            turned = ahead >= TURNED_FIRST
-            firsts = [] if turned else [ahead, ahead + PAIR]
-            for first in firsts:
-                transpose(first)
-            if k == FIRST_PERIOD:
-                add_group(0)
-            add_group(k - 2)
-            if turned:
-                turn(ahead)
-            for first in firsts:
-                regroup(first)
+                copy_a(tiles[-1])
+                clamp_norms(group)
+                square_sum(tiles[-PAIR])
+                invert_norms(group)
+            step, t = vector_work[-1]
+            step(t)
+            quantise(ROW_TILES + SIX * (w + 1), QUAD)
+            quantise(ROW_TILES + SIX * (w + 1) + QUAD, PAIR)
+
+        def copy_on_vector(t):
+            copy_a(t, on_vector)
 
         warm_up(WARM_UP)
         interleave_wk(slice(0, DI // 2), on_vector)
@@ -442,163 +431,140 @@ def tile_hydraencoderlayer_pa_t_kernel(tc, x, wk, wv, out):
             quantise(t, 1)
         regroup(2, 1, on_vector)
         regroup(3, 1, on_scalar)
+        transpose(4)
         pass_a(0)
         pass_a(1)
-        quantise(2, PAIR)
-        transpose(4)
         transpose(6)
-        square_sum(0, a_ps)
+        regroup(4)
+        quantise(2, PAIR)
+        square_sum(0, True)
         copy_a(0)
         copy_a(1, on_vector)
         pass_a(2)
         pass_a(3)
-        regroup(4)
-        square_sum(1)
         regroup(6)
+        square_sum(1)
         copy_a(2)
-        transpose(8)
-        transpose(10)
         quantise(4, PAIR)
         quantise(6, PAIR)
-
-        interleave_wv()
+        interleave_wv(4)
+        transpose(8)
+        transpose(10)
+        pass_a(4)
+        pass_a(5)
         copy_a(3)
+        pass_a(6)
         square_sum(2)
-        for t in range(QUAD, PAIR * QUAD):
-            pass_a(t)
         regroup(8)
         copy_a(4)
-        clamp_norms([0, 2])
+        clamp_norms(groups[0])
         regroup(10)
         transpose(12)
         transpose(14)
+        pass_a(7)
         copy_a(5, on_vector)
-        copy_a(6)
-        invert_norms([0, 2])
+        square_sum(3)
+        invert_norms(groups[0])
         regroup(12)
-        square_sum(4)
+        copy_a(6)
         regroup(14)
+        copy_a(7, on_vector)
         warm_up(KEEP_WARM)
-        transpose(16)
-        square_sum(5)
-        copy_a(7)
-
         quantise(8, PAIR)
         quantise_weight("wv", slice(0, DI))
-        quantise(10, QUAD)
-        open_folds(1, 3)
-        square_on_gpsimd(3)
-        open_folds(2)
-        fold(1, True, False)
-        clamp_norms([4, 5])
-        square_sum(6)
-        invert_norms([4, 5])
-        pass_a(8)
-        pass_a(9)
-        pass_v(0)
-        pass_v(1)
-        regroup(16)
-        copy_a(8)
-        square_sum(7)
-        product(0)
-        pass_a(10)
-        pass_v(2)
-        copy_a(9)
-        product(1)
-        pass_a(11)
-        pass_v(4)
-        square_sum(8)
-        pass_v(5)
-        add_product(0)
-        product(2)
-        transpose(18)
-        square_sum(9)
-        copy_a(10)
-        transpose(20)
-        product(4)
-        product(5)
-        add_pairs(0, ADD_BESIDE_SQUARE)
-        quantise(14, QUAD)
-        clamp_norms(norm_sets[2])
-        copy_a(11)
-        invert_norms(norm_sets[2])
-        open_folds(3)
-        square_on_gpsimd(11)
-        regroup(18)
-        regroup(20)
-        square_sum(10)
+        quantise(10, PAIR)
+        quantise(12, QUAD)
+        square_sum(4)
+        square_sum(5)
 
-        for k in range(FIRST_PERIOD, LAST_PERIOD + 1):
-            period(k)
+        period(-1, copies_last=True)
+        period(0, copies_first=True)
+        for w in range(1, N_RUNS - 1):
+            period(w)
 
-        first_tile, first_pair = QUAD * (LAST_PERIOD + 1), LAST_PERIOD
-        pairs = groups[first_pair:]
-        by_vector = (first_tile + 3, first_tile + 4)
-        from_psum = pairs[-1]
-
-        v_tiles = [t for pair in pairs for t in pair]
-        passes = [(pass_v, t) for t in v_tiles]
+        first_tile = period_tiles(N_RUNS - 1)[0]
+        by_vector = TAIL_COPIES
+        from_psum = (N_TILES - PAIR, N_TILES - 1)
+        passes = [(pass_v, t) for t in queue]
         for i, t in enumerate(range(first_tile, N_TILES)):
-            passes.insert(PAIR * i, (pass_a, t))
+            passes.insert(max(PAIR * i, 3 * i - LEAD), (pass_a, t))
 
-        def run_ahead(count):
-            for _ in range(min(count, len(free), len(passes))):
+        def run_ahead():
+            while free and passes:
                 mx, t = passes.pop(0)
-                mx(t, False)
+                mx(t)
 
-        scalar_work = []
+        scalar_work = [(square_sum, first_tile - 1)]
         for t in range(first_tile, N_TILES):
             if t not in by_vector and t not in from_psum:
                 scalar_work.append((copy_a, t))
-            scalar_work.append((square_sum, t - 1))
+            if t > first_tile:
+                scalar_work.append((square_sum, t - 1))
+            if t == first_tile + 1:
+                scalar_work.append((sum_folded, LAST_WINDOW))
         scalar_work += [(square_sum, N_TILES - 1)] + [(copy_a, t) for t in from_psum]
-        norm_pairs = {scalar_work.index((square_sum, pair[1])): pair for pair in pairs if pair[1] >= first_tile - 1}
-        vector_work = [(product, t) for t in v_tiles]
-        for late, t in zip(squared[-PAIR:], by_vector):
-            vector_work.insert(vector_work.index((product, late)) + 1, (copy_a, t))
+        ready = {}
+        for group in groups[N_RUNS + 2 :]:
+            steps = [(sum_folded, on_gpsimd[t]) if t in on_gpsimd else (square_sum, t) for t in group]
+            ready[max(scalar_work.index(step) if step in scalar_work else -1 for step in steps)] = group
+        vector_work = [(product, t) for t in queue]
+        for j, t in enumerate(by_vector):
+            vector_work.insert(TAIL_PLACES[j], (copy_on_vector, t))
 
-        run_ahead(QUAD)
-        for t in groups[first_pair - 1][::PAIR]:
-            add_product(t)
-        run_ahead(RING)
-        for i, (work_v, t) in enumerate(vector_work[:-1]):
-            if i < len(scalar_work):
-                work_s, s = scalar_work[i]
+        window(N_RUNS - 1, staged(first_tile + PAIR, QUAD))
+        run_ahead()
+        added, inverted = [], [t for group in groups[: N_RUNS + 2] for t in group]
+        steps = 0
+        early, first_direct = queue[:PAIR], queue[1]
+        while len(vector_work) > 1 or steps < len(scalar_work) + PAIR:
+            if steps < len(scalar_work):
+                work_s, s = scalar_work[steps]
                 if work_s is square_sum and s in from_psum:
-                    square_sum(s, a_ps)
+                    square_sum(s, True)
                 else:
                     work_s(s)
-                if i - 2 in norm_pairs:
-                    invert_norms(norm_pairs[i - 2])
-                if i - 1 in norm_pairs:
-                    clamp_norms(norm_pairs[i - 1])
-                run_ahead(1)
-            if work_v is copy_a:
-                copy_a(t, on_vector)
-            else:
-                product(t)
-            run_ahead(1)
-            g, col = place[t]
-            if work_v is product and g >= len(groups) - PAIR:
-                add_product(t)
-                if t == N_TILES - QUAD + 1:
-                    add_group(g - 1)
-            elif work_v is product and col == PAIR - 1:
-                add_pairs(g)
-                add_group(g - 1)
-        for half in (slice(0, DI // 2), slice(DI // 2, DI)):
-            product(N_TILES - 1, half)
-        add_product(N_TILES - 1, closes=True)
-
-        nc.vector.tensor_reduce(
-            out=out_cols[:, : BATCH * E_BLOCKS].rearrange("e (b i) -> e i b", b=BATCH),
-            in_=token_sums[0][:].rearrange("e i (b q) -> e i b q", b=BATCH),
-            axis=AXIS.X,
-            op=ALU.add,
-        )
+            if steps - 2 in ready:
+                invert_norms(ready[steps - 2])
+                inverted += ready[steps - 2]
+            if steps - 1 in ready:
+                clamp_norms(ready[steps - 1])
+            steps += 1
+            run_ahead()
+            work_v, t = vector_work[0]
+            if len(vector_work) == 1 or (work_v is product and not (t in inverted and t in a_sb)):
+                continue
+            vector_work.pop(0)
+            work_v(t)
+            run_ahead()
+            left = len(vector_work)
+            if t == first_direct:
+                add_products(PAIR)
+                run_ahead()
+            fresh = [s for s in to_sum if s not in added and t not in early]
+            if work_v is product and len(fresh) >= PAIR and len(added) < ADDS:
+                add_pair(fresh[0], fresh[1])
+                added.append(fresh[0])
+                if len(added) % PAIR == 1 and len(added) > 1:
+                    add_products(PAIR)
+            elif work_v is product and len(added) == ADDS and not passes:
+                direct = [s for s in to_sum if s not in added[-1:] or left <= NO_ADD]
+                to_sum[:] = direct + [s for s in to_sum if s not in direct]
+                add_products(len(direct))
+        last = N_TILES - 1
+        for half in range(PAIR):
+            product(last, slice(half * DI // 2, (half + 1) * DI // 2))
+        for i in range(E_BLOCKS):
+            add_block(last, i, closes=i % PAIR == 1)
+        for half in range(PAIR):
+            nc.vector.tensor_reduce(
+                out=out_cols[:, : BATCH * E_BLOCKS].rearrange("e (b i) -> e i b", b=BATCH)[:, PAIR * half : PAIR * (half + 1)],
+                in_=sums[half][:, :PAIR, :].rearrange("e i (b q) -> e i b q", b=BATCH),
+                axis=AXIS.X,
+                op=ALU.add,
+            )
         out_rows = consts.tile([P, QUADRANT], F32, align_bytes=64)
         nc.vector.transpose(out=out_rows[:], in_=out_cols[:])
         stores = out.rearrange("b o (i g q) -> g (b o i) q", i=E_BLOCKS, q=QUADRANT)
         for g in range(P // QUADRANT):
-            queue = nc.sync if g % 2 == 0 else nc.scalar
-            queue.dma_start(out=stores[g], in_=out_rows[g * QUADRANT : g * QUADRANT + BATCH * E_BLOCKS, :])
+            queue_of = nc.sync if g % 2 == 0 else nc.scalar
+            queue_of.dma_start(out=stores[g], in_=out_rows[g * QUADRANT : g * QUADRANT + BATCH * E_BLOCKS, :])

@@ -81,19 +81,20 @@ def tile_hydraencoderlayer_pa_t_kernel(tc, x, wk, wv, out):
                 load_weight("wv", wv)
 
         pieces = x.rearrange("b (d s t) (u g i) -> b s g (t u) d i", d=ROWS, t=BLOCK, u=HALVES, g=P // QUADRANT)
-        size = SIX * PAIR
-        parts = [(s, d, size) for s in range(1, QUAD) for d in (0, size)]
-        parts += [(s, PAIR * size, ROWS - PAIR * size) for s in range(1, QUAD)]
+        size = QUAD * PAIR
         x_pieces = x_pool.tile([P, N_RUNS * size, BATCH, 2 * QUADRANT], BF16, name="x_pieces", align_bytes=64)
-        filled = 0
-        for s, d, count in parts:
+        for r in range(N_RUNS):
+            s, d = divmod(r * size, ROWS)
             for b in range(BATCH):
                 for g in (0, 2, 1, 3):
                     nc.sync.dma_start(
-                        out=x_pieces[g * QUADRANT : (g + 1) * QUADRANT, filled : filled + count, b, :],
-                        in_=pieces[b, s, g][:, d : d + count, :],
+                        out=x_pieces[g * QUADRANT : (g + 1) * QUADRANT, r * size : (r + 1) * size, b, :],
+                        in_=pieces[b, PAIR + s, g][:, d : d + size, :],
                     )
-            filled += count
+            if r % PAIR == 0:
+                c = ROW_TILES // QUAD + r // PAIR
+                x_rows.append(x_pool.tile([P, QUAD * D], BF16, name="x_rows%d" % c))
+                nc.sync.dma_start(out=x_rows[c][:], in_=rows[c])
 
         out_cols = consts.tile([P, QUADRANT], F32, align_bytes=64)
         nc.vector.memset(out_cols[:], 0.0)
@@ -106,6 +107,15 @@ def tile_hydraencoderlayer_pa_t_kernel(tc, x, wk, wv, out):
         nc.gpsimd.tensor_scalar(
             out=by_batch[:].rearrange("p (b h t) -> p b h t", b=BATCH, h=PAIR),
             in0=ident[:].rearrange("p (h b t) -> p b h t", b=BATCH, h=PAIR),
+            scalar1=1.0,
+            scalar2=0.0,
+            op0=ALU.mult,
+            op1=ALU.add,
+        )
+        by_half = consts.tile([P, P], F32)
+        nc.gpsimd.tensor_scalar(
+            out=by_half[:].rearrange("p (h b t) -> p b h t", b=BATCH, h=PAIR),
+            in0=ident[:].rearrange("p (b h t) -> p b h t", b=BATCH, h=PAIR),
             scalar1=1.0,
             scalar2=0.0,
             op0=ALU.mult,
@@ -177,11 +187,15 @@ def tile_hydraencoderlayer_pa_t_kernel(tc, x, wk, wv, out):
         def transpose(first, count=PAIR):
             x_banks[first] = take_bank(("x", first), [P, PAIR, HALVES, P])
             for j in range(count):
-                c, slot = divmod(first + j, QUAD)
+                t = first + j
+                if t >= ROW_TILES:
+                    r, place = divmod(t - ROW_TILES, SIX)
+                    t = ROW_TILES + PAIR * r + place - QUAD
+                c, slot = divmod(t, QUAD)
                 words = x_rows[c][:].bitcast(F32)
                 for u in range(HALVES):
                     w0 = slot * WORDS + u * P
-                    nc.tensor.transpose(x_banks[first][:, j, u, :], words[:, w0 : w0 + P], ident[:])
+                    nc.tensor.transpose(x_banks[first][:, j, u, :], words[:, w0 : w0 + P], (ident if first < ROW_TILES else by_half)[:])
 
         def regroup(first, count=PAIR, copy=on_vector):
             copy(
@@ -192,7 +206,7 @@ def tile_hydraencoderlayer_pa_t_kernel(tc, x, wk, wv, out):
 
         def turn(r):
             nc.vector.transpose(
-                out=stages[r % PAIR][:].bitcast(F32),
+                out=stages[r % PAIR][:, : QUAD * D].bitcast(F32),
                 in_=x_pieces[:, r * size : (r + 1) * size].rearrange("p n b i -> p (n b i)").bitcast(F32),
             )
 
@@ -398,8 +412,10 @@ def tile_hydraencoderlayer_pa_t_kernel(tc, x, wk, wv, out):
                     run_ahead()
                 if i == 0:
                     window(w, staged(ROW_TILES + SIX * w, QUAD) if w >= 0 else staged(ROW_TILES - QUAD, QUAD))
+            transpose(ROW_TILES + SIX * (w + 1) + QUAD)
             add_products(SIX)
             turn(w + 1)
+            regroup(ROW_TILES + SIX * (w + 1) + QUAD)
             if w - 1 in windows:
                 sum_folded(w - 1)
             if copies_last:

@@ -29,6 +29,9 @@ ROWS = QUADRANT
 ROW_TILES = BLOCK
 N_RUNS = (N_TILES - ROW_TILES) // SIX
 RING = 6
+RUN_LENGTH = 7
+PARTS = (8, 12, 12, 8, 12, 12)
+TURNED = (0, 4, 4, 4, 4, 4, 6, 6)
 FIRST = ROW_TILES - PAIR
 WK_SPLIT = 336
 RUN = 4
@@ -81,20 +84,25 @@ def tile_hydraencoderlayer_pa_t_kernel(tc, x, wk, wv, out):
                 load_weight("wv", wv)
 
         pieces = x.rearrange("b (d s t) (u g i) -> b s g (t u) d i", d=ROWS, t=BLOCK, u=HALVES, g=P // QUADRANT)
-        size = QUAD * PAIR
-        x_pieces = x_pool.tile([P, N_RUNS * size, BATCH, 2 * QUADRANT], BF16, name="x_pieces", align_bytes=64)
-        for r in range(N_RUNS):
-            s, d = divmod(r * size, ROWS)
+        x_pieces = x_pool.tile([P, PAIR * ROWS, BATCH, 2 * QUADRANT], BF16, name="x_pieces", align_bytes=64)
+
+        def load_rows(c):
+            x_rows.append(x_pool.tile([P, QUAD * D], BF16, name="x_rows%d" % c))
+            nc.sync.dma_start(out=x_rows[c][:], in_=rows[c])
+
+        load_rows(4)
+        filled = 0
+        for part, count in enumerate(PARTS):
+            if part < 3:
+                load_rows(5 + part)
+            s, d = divmod(filled, ROWS)
             for b in range(BATCH):
                 for g in (0, 2, 1, 3):
                     nc.sync.dma_start(
-                        out=x_pieces[g * QUADRANT : (g + 1) * QUADRANT, r * size : (r + 1) * size, b, :],
-                        in_=pieces[b, PAIR + s, g][:, d : d + size, :],
+                        out=x_pieces[g * QUADRANT : (g + 1) * QUADRANT, filled : filled + count, b, :],
+                        in_=pieces[b, PAIR + s, g][:, d : d + count, :],
                     )
-            if r % PAIR == 0:
-                c = ROW_TILES // QUAD + r // PAIR
-                x_rows.append(x_pool.tile([P, QUAD * D], BF16, name="x_rows%d" % c))
-                nc.sync.dma_start(out=x_rows[c][:], in_=rows[c])
+            filled += count
 
         out_cols = consts.tile([P, QUADRANT], F32, align_bytes=64)
         nc.vector.memset(out_cols[:], 0.0)
@@ -190,7 +198,7 @@ def tile_hydraencoderlayer_pa_t_kernel(tc, x, wk, wv, out):
                 t = first + j
                 if t >= ROW_TILES:
                     r, place = divmod(t - ROW_TILES, SIX)
-                    t = ROW_TILES + PAIR * r + place - QUAD
+                    t = ROW_TILES + sum(SIX - n for n in TURNED[:r]) + place - TURNED[r]
                 c, slot = divmod(t, QUAD)
                 words = x_rows[c][:].bitcast(F32)
                 for u in range(HALVES):
@@ -206,8 +214,8 @@ def tile_hydraencoderlayer_pa_t_kernel(tc, x, wk, wv, out):
 
         def turn(r):
             nc.vector.transpose(
-                out=stages[r % PAIR][:, : QUAD * D].bitcast(F32),
-                in_=x_pieces[:, r * size : (r + 1) * size].rearrange("p n b i -> p (n b i)").bitcast(F32),
+                out=stages[r % PAIR][:, : TURNED[r] * D].bitcast(F32),
+                in_=x_pieces[:, PAIR * sum(TURNED[:r]) : PAIR * sum(TURNED[: r + 1])].rearrange("p n b i -> p (n b i)").bitcast(F32),
             )
 
         def quantise(first, count):
@@ -330,7 +338,7 @@ def tile_hydraencoderlayer_pa_t_kernel(tc, x, wk, wv, out):
 
         def product(t, cols=slice(0, DI)):
             if t not in prod:
-                prod[t] = work.tile([P, DI], F32, name="prod", bufs=10)
+                prod[t] = work.tile([P, DI], F32, name="prod", bufs=12)
             nc.vector.scalar_tensor_tensor(
                 out=prod[t][:, cols],
                 in0=v_ps[t][:, cols],
@@ -412,10 +420,15 @@ def tile_hydraencoderlayer_pa_t_kernel(tc, x, wk, wv, out):
                     run_ahead()
                 if i == 0:
                     window(w, staged(ROW_TILES + SIX * w, QUAD) if w >= 0 else staged(ROW_TILES - QUAD, QUAD))
-            transpose(ROW_TILES + SIX * (w + 1) + QUAD)
-            add_products(SIX)
-            turn(w + 1)
-            regroup(ROW_TILES + SIX * (w + 1) + QUAD)
+            x_first = ROW_TILES + SIX * (w + 1)
+            pairs = range(x_first + TURNED[w + 1], x_first + SIX, PAIR)
+            for first in pairs:
+                transpose(first)
+            add_products(RUN_LENGTH - len(pairs))
+            if TURNED[w + 1]:
+                turn(w + 1)
+            for first in pairs:
+                regroup(first)
             if w - 1 in windows:
                 sum_folded(w - 1)
             if copies_last:

@@ -30,19 +30,20 @@ ROW_TILES = BLOCK
 N_RUNS = (N_TILES - ROW_TILES) // SIX
 RING = 6
 RUN_LENGTH = 7
-PARTS = (8, 12, 12, 8, 12, 12)
-TURNED = (0, 4, 4, 4, 4, 4, 6, 6)
+PARTS = (8, 12, 12, 12, 12, 8)
+HEAD_TILES = ROW_TILES + PAIR * QUAD
+TURNED = (4, 4, 4, 4, 6, 6, 4)
 FIRST = ROW_TILES - PAIR
 WK_SPLIT = 336
 RUN = 4
 WARM_UP = 6
 KEEP_WARM = 3
-WV_BEHIND = 1
+WV_BEHIND = 2
 LAST_WINDOW = 6
-TAIL_COPIES = (60,)
+TAIL_COPIES = ()
 LEAD = 1
 ADDS = 6
-TAIL_PLACES = (7,)
+TAIL_PLACES = (6,)
 NO_ADD = 1
 
 FLOPS = 2 * 2 * BATCH * TOKENS * D * DI
@@ -150,9 +151,10 @@ def tile_hydraencoderlayer_pa_t_kernel(tc, x, wk, wv, out):
         row_stage = stage.tile([P, ROW_TILES * D], BF16, name="row_stage", align_bytes=64)
 
         def staged(first, count):
-            if first < ROW_TILES:
-                return row_stage[:, first * D : (first + count) * D]
-            r, j = divmod(first - ROW_TILES, SIX)
+            if first < HEAD_TILES:
+                place = first if first < ROW_TILES else first - ROW_TILES + (first - ROW_TILES) // QUAD * QUAD
+                return row_stage[:, place * D : (place + count) * D]
+            r, j = divmod(first - HEAD_TILES, SIX)
             return stages[r % PAIR][:, j * D : (j + count) * D]
 
         w_grouped, w_codes, w_scales = {}, {}, {}
@@ -188,17 +190,20 @@ def tile_hydraencoderlayer_pa_t_kernel(tc, x, wk, wv, out):
         x_banks, x_codes, x_scales = {}, {}, {}
 
         def run_of(t):
-            if t < ROW_TILES:
+            if t < HEAD_TILES:
                 return (QUAD, t // QUAD), t % QUAD
-            return (SIX, (t - ROW_TILES) // SIX), (t - ROW_TILES) % SIX
+            return (SIX, (t - HEAD_TILES) // SIX), (t - HEAD_TILES) % SIX
 
-        def transpose(first, count=PAIR):
-            x_banks[first] = take_bank(("x", first), [P, PAIR, HALVES, P])
+        def transpose(first, count=PAIR, bank=None):
+            if bank is None:
+                x_banks[first] = take_bank(("x", first), [P, PAIR, HALVES, P])
+            else:
+                x_banks[first] = psum.tile([P, PAIR, HALVES, P], F32, name=bank)
             for j in range(count):
                 t = first + j
-                if t >= ROW_TILES:
-                    r, place = divmod(t - ROW_TILES, SIX)
-                    t = ROW_TILES + sum(SIX - n for n in TURNED[:r]) + place - TURNED[r]
+                if t >= HEAD_TILES:
+                    r, place = divmod(t - HEAD_TILES, SIX)
+                    t = HEAD_TILES + PAIR * r + place - QUAD
                 c, slot = divmod(t, QUAD)
                 words = x_rows[c][:].bitcast(F32)
                 for u in range(HALVES):
@@ -210,7 +215,8 @@ def tile_hydraencoderlayer_pa_t_kernel(tc, x, wk, wv, out):
                 out=staged(first, count).bitcast(F32).rearrange("p (j r u) -> p j r u", r=P, u=HALVES),
                 in_=x_banks[first][:].rearrange("p j u r -> p j r u")[:, :count, :, :],
             )
-            release_bank(("x", first))
+            if ("x", first) in held:
+                release_bank(("x", first))
 
         def turn(r):
             nc.vector.transpose(
@@ -222,8 +228,8 @@ def tile_hydraencoderlayer_pa_t_kernel(tc, x, wk, wv, out):
             run, j = run_of(first)
             if run not in x_codes:
                 width = run[0]
-                x_codes[run] = operands.tile([P, width * P], U32, name="x_codes%d" % width, bufs=4, align_bytes=256)
-                x_scales[run] = operands.tile([P, width * P], U8, name="x_scales%d" % width, bufs=4, align_bytes=256)
+                x_codes[run] = operands.tile([P, width * P], U32, name="x_codes%d" % width, bufs=PAIR * QUAD + PAIR - width, align_bytes=256)
+                x_scales[run] = operands.tile([P, width * P], U8, name="x_scales%d" % width, bufs=PAIR * QUAD + PAIR - width, align_bytes=256)
             cols = slice(j * P, (j + count) * P)
             nc.vector.quantize_mx(out=x_codes[run][:, cols].bitcast(FP8X4), scales=x_scales[run][:, cols], in_=staged(first, count))
 
@@ -266,9 +272,8 @@ def tile_hydraencoderlayer_pa_t_kernel(tc, x, wk, wv, out):
         done = [t for group in groups for t in group]
         rest = [t for t in range(N_TILES) if t not in done and t not in on_gpsimd]
         late = [t for t in on_gpsimd if t not in done]
-        groups.append(rest[:1] + late + rest[1:3])
-        groups.append(rest[3:SIX])
-        groups += [rest[i : i + PAIR] for i in range(SIX, len(rest), PAIR)]
+        groups += [rest[:PAIR], late + rest[PAIR:QUAD]]
+        groups += [rest[i : i + PAIR] for i in range(QUAD, len(rest), PAIR)]
         order = [t for group in groups for t in group]
 
         def copy_a(t, copy=on_scalar):
@@ -381,68 +386,75 @@ def tile_hydraencoderlayer_pa_t_kernel(tc, x, wk, wv, out):
 
         queue = list(order)
 
-        def period(w, copies_first=False, copies_last=False):
+        def period(w, count=SIX):
             tiles, group = period_tiles(w), groups[w + 3]
-            count = SIX - copies_first - copies_last
             products = queue[:count]
             queue[:] = queue[count:]
-            vector_work = [(product, t) for t in products]
             scalar_work = [(copy_a, tiles[0]), (copy_a, tiles[1])]
-            if tiles[0] not in on_gpsimd:
+            if w < 0:
+                scalar_work[1:] = [(clamp_norms, groups[1]), (copy_a, tiles[1]), (invert_norms, groups[1])]
                 scalar_work.append((square_sum, tiles[0]))
             for j in range(PAIR, SIX - 1):
                 scalar_work += [(copy_a, tiles[j]), (square_sum, tiles[j - 1])]
-            if copies_first:
-                vector_work.insert(0, (copy_on_vector, tiles[0]))
-                scalar_work.pop(0)
-            if copies_last:
-                vector_work.append((copy_on_vector, tiles[-1]))
             passes = []
             for j in range(SIX):
                 passes += [(pass_a, tiles[j])] + [(pass_v, t) for t in products[j : j + 1]]
-            if copies_last:
-                pass
 
             def run_ahead():
                 while free and passes:
                     mx, t = passes.pop(0)
                     mx(t)
 
-            if copies_last:
-                scalar_work[1:1] = [(clamp_norms, groups[1])]
-                scalar_work[3:3] = [(invert_norms, groups[1])]
-            if copies_first:
-                scalar_work.insert(1, (invert_norms, groups[w + 2]))
+            if w == 0:
+                passes = [passes[i] for i in (1, 0, 3, 2, 5, 4, 7, 6, 9, 8, 11, 10)]
+            if w < 0:
+                passes[1:5] = [passes[2], passes[1], passes[3], passes[4]]
+                passes[5:5] = [(transpose, ROW_TILES + QUAD), (transpose, ROW_TILES + SIX)]
+                passes[7], passes[8] = passes[8], passes[7]
+                passes[9], passes[10] = passes[10], passes[9]
+            x_first = HEAD_TILES + SIX * w if w >= 0 else ROW_TILES
+            x_end = min(HEAD_TILES + SIX * (w + 1), N_TILES)
+            pairs = list(range(x_first + (TURNED[w] if w >= 0 else QUAD), x_end, PAIR))
+            vector_work = [(product, t) for t in products[:-1]]
+            if w < 0:
+                vector_work[1:1] = [(regroup, ROW_TILES + PAIR)]
+                vector_work[3:3] = [(regroup, first) for first in pairs]
             run_ahead()
-            for i in range(len(scalar_work)):
-                for step, t in [scalar_work[i]] + vector_work[:-1][i : i + 1]:
+            for step, t in scalar_work:
+                step(t)
+                run_ahead()
+                if t == tiles[0] and step is copy_a:
+                    window(w, staged(HEAD_TILES + SIX * (w - 1) if w > 0 else ROW_TILES + QUAD * w, QUAD))
+                if vector_work and step in (copy_a, square_sum):
+                    step, t = vector_work.pop(0)
                     step(t)
                     run_ahead()
-                if i == 0:
-                    window(w, staged(ROW_TILES + SIX * w, QUAD) if w >= 0 else staged(ROW_TILES - QUAD, QUAD))
-            x_first = ROW_TILES + SIX * (w + 1)
-            pairs = range(x_first + TURNED[w + 1], x_first + SIX, PAIR)
             for first in pairs:
-                transpose(first)
-            add_products(RUN_LENGTH - len(pairs))
-            if TURNED[w + 1]:
-                turn(w + 1)
+                if first not in x_banks:
+                    transpose(first)
+            add_products(RUN_LENGTH - len(pairs) if w >= 0 else PAIR)
+            if w >= 0:
+                turn(w)
             for first in pairs:
-                regroup(first)
+                if w >= 0:
+                    regroup(first)
             if w - 1 in windows:
                 sum_folded(w - 1)
-            if copies_last:
-                square_sum(tiles[-PAIR])
-                clamp_norms(group)
-            else:
+            if x_end < N_TILES:
                 copy_a(tiles[-1])
                 clamp_norms(group)
                 square_sum(tiles[-PAIR])
                 invert_norms(group)
-            step, t = vector_work[-1]
-            step(t)
-            quantise(ROW_TILES + SIX * (w + 1), QUAD)
-            quantise(ROW_TILES + SIX * (w + 1) + QUAD, PAIR)
+            else:
+                square_sum(tiles[-PAIR])
+                clamp_norms(group)
+                copy_a(tiles[-1], on_vector)
+                square_sum(tiles[-1])
+                invert_norms(group)
+            product(products[-1])
+            quantise(x_first, QUAD)
+            if x_first + QUAD < x_end:
+                quantise(x_first + QUAD, x_end - x_first - QUAD)
 
         def copy_on_vector(t):
             copy_a(t, on_vector)
@@ -460,55 +472,57 @@ def tile_hydraencoderlayer_pa_t_kernel(tc, x, wk, wv, out):
             quantise(t, 1)
         regroup(2, 1, on_vector)
         regroup(3, 1, on_scalar)
-        transpose(4)
         pass_a(0)
         pass_a(1)
-        transpose(6)
-        regroup(4)
         quantise(2, PAIR)
+        transpose(4)
+        transpose(6)
         square_sum(0, True)
         copy_a(0)
         copy_a(1, on_vector)
         pass_a(2)
         pass_a(3)
-        regroup(6)
+        regroup(4)
         square_sum(1)
+        regroup(6)
         copy_a(2)
+        transpose(8)
+        transpose(10)
         quantise(4, PAIR)
         quantise(6, PAIR)
         interleave_wv(4)
-        transpose(8)
-        transpose(10)
         pass_a(4)
         pass_a(5)
         copy_a(3)
         pass_a(6)
         square_sum(2)
         regroup(8)
+        pass_a(7)
         copy_a(4)
         clamp_norms(groups[0])
         regroup(10)
         transpose(12)
         transpose(14)
-        pass_a(7)
         copy_a(5, on_vector)
         square_sum(3)
         invert_norms(groups[0])
+        copy_a(7, on_vector)
         regroup(12)
         copy_a(6)
-        regroup(14)
-        copy_a(7, on_vector)
+        regroup(14, copy=on_scalar)
         warm_up(KEEP_WARM)
+        transpose(16, bank="sums1")
+        transpose(18, bank="sums0")
         quantise(8, PAIR)
         quantise_weight("wv", slice(0, DI))
         quantise(10, PAIR)
         quantise(12, QUAD)
+        regroup(16)
         square_sum(4)
         square_sum(5)
 
-        period(-1, copies_last=True)
-        period(0, copies_first=True)
-        for w in range(1, N_RUNS - 1):
+        period(-1, QUAD)
+        for w in range(N_RUNS - 1):
             period(w)
 
         first_tile = period_tiles(N_RUNS - 1)[0]
@@ -523,13 +537,13 @@ def tile_hydraencoderlayer_pa_t_kernel(tc, x, wk, wv, out):
                 mx, t = passes.pop(0)
                 mx(t)
 
-        scalar_work = [(square_sum, first_tile - 1)]
+        scalar_work = []
         for t in range(first_tile, N_TILES):
             if t not in by_vector and t not in from_psum:
                 scalar_work.append((copy_a, t))
             if t > first_tile:
                 scalar_work.append((square_sum, t - 1))
-            if t == first_tile + 1:
+            if t == first_tile + PAIR:
                 scalar_work.append((sum_folded, LAST_WINDOW))
         scalar_work += [(square_sum, N_TILES - 1)] + [(copy_a, t) for t in from_psum]
         ready = {}
@@ -540,11 +554,10 @@ def tile_hydraencoderlayer_pa_t_kernel(tc, x, wk, wv, out):
         for j, t in enumerate(by_vector):
             vector_work.insert(TAIL_PLACES[j], (copy_on_vector, t))
 
-        window(N_RUNS - 1, staged(first_tile + PAIR, QUAD))
+        window(N_RUNS - 1, staged(N_TILES - QUAD, QUAD))
         run_ahead()
         added, inverted = [], [t for group in groups[: N_RUNS + 2] for t in group]
         steps = 0
-        early, first_direct = queue[:PAIR], queue[1]
         while len(vector_work) > 1 or steps < len(scalar_work) + PAIR:
             if steps < len(scalar_work):
                 work_s, s = scalar_work[steps]
@@ -564,21 +577,20 @@ def tile_hydraencoderlayer_pa_t_kernel(tc, x, wk, wv, out):
                 continue
             vector_work.pop(0)
             work_v(t)
-            run_ahead()
             left = len(vector_work)
-            if t == first_direct:
+            if t == queue[0]:
                 add_products(PAIR)
-                run_ahead()
-            fresh = [s for s in to_sum if s not in added and t not in early]
+            fresh = [s for s in to_sum if s not in added]
             if work_v is product and len(fresh) >= PAIR and len(added) < ADDS:
                 add_pair(fresh[0], fresh[1])
                 added.append(fresh[0])
                 if len(added) % PAIR == 1 and len(added) > 1:
                     add_products(PAIR)
             elif work_v is product and len(added) == ADDS and not passes:
-                direct = [s for s in to_sum if s not in added[-1:] or left <= NO_ADD]
+                direct = [s for s in to_sum if s not in added[len(added) - left // PAIR :] or left <= NO_ADD]
                 to_sum[:] = direct + [s for s in to_sum if s not in direct]
                 add_products(len(direct))
+            run_ahead()
         last = N_TILES - 1
         for half in range(PAIR):
             product(last, slice(half * DI // 2, (half + 1) * DI // 2))

@@ -105,12 +105,12 @@ def tile_hydraencoderlayer_pa_t_kernel(tc, x, wk, wv, out):
                     )
             filled += count
 
-        out_cols = consts.tile([P, QUADRANT], F32, align_bytes=64)
-        nc.vector.memset(out_cols[:], 0.0)
         zeros = consts.tile([P, DI], BF16)
         nc.vector.memset(zeros[:], 0.0)
         ident = consts.tile([P, P], F32)
         nc.vector.memset(ident[:], 0.0)
+        out_cols = consts.tile([P, QUADRANT], F32, align_bytes=64)
+        nc.vector.memset(out_cols[:], 0.0)
         make_identity(nc, ident[:], nomemset=True)
         by_batch = consts.tile([P, P], F32)
         nc.gpsimd.tensor_scalar(
@@ -459,7 +459,7 @@ def tile_hydraencoderlayer_pa_t_kernel(tc, x, wk, wv, out):
         def copy_on_vector(t):
             copy_a(t, on_vector)
 
-        warm_up(WARM_UP)
+        warm_up(QUAD)
         interleave_wk(slice(0, DI // 2), on_vector)
         interleave_wk(slice(DI // 2, WK_SPLIT), on_vector)
         interleave_wk(slice(WK_SPLIT, DI), on_scalar)
@@ -467,6 +467,8 @@ def tile_hydraencoderlayer_pa_t_kernel(tc, x, wk, wv, out):
         quantise_weight("wk", slice(DI // 2, DI))
         for t in range(QUAD):
             transpose(t, 1)
+            if t == 1:
+                warm_up(WARM_UP - QUAD)
         for t in range(PAIR):
             regroup(t, 1, on_scalar)
             quantise(t, 1)

@@ -26,25 +26,18 @@ SIX = 6
 N_TILES = BATCH * TOKENS // P
 BLOCK = QUADRANT // HALVES
 ROWS = QUADRANT
-ROW_TILES = BLOCK
-N_RUNS = (N_TILES - ROW_TILES) // SIX
+PLAIN_TILES = BLOCK
+HEAD_TILES = PLAIN_TILES + PAIR * QUAD
+TURNED = (4, 4, 4, 4, 6, 6, 4)
+PARTS = (8, 12, 12, 12, 12, 8)
+N_PERIODS = len(TURNED)
+FIRST = PLAIN_TILES - PAIR
 RING = 6
 RUN_LENGTH = 7
-PARTS = (8, 12, 12, 12, 12, 8)
-HEAD_TILES = ROW_TILES + PAIR * QUAD
-TURNED = (4, 4, 4, 4, 6, 6, 4)
-FIRST = ROW_TILES - PAIR
 WK_SPLIT = 336
 RUN = 4
-WARM_UP = 6
-KEEP_WARM = 3
-WV_BEHIND = 2
-LAST_WINDOW = 6
-TAIL_COPIES = ()
-LEAD = 1
 ADDS = 6
-TAIL_PLACES = (6,)
-NO_ADD = 1
+WARM_UP = 4
 
 FLOPS = 2 * 2 * BATCH * TOKENS * D * DI
 
@@ -56,7 +49,7 @@ def tile_hydraencoderlayer_pa_t_kernel(tc, x, wk, wv, out):
         consts = ctx.enter_context(tc.tile_pool(name="consts", bufs=1))
         x_pool = ctx.enter_context(tc.tile_pool(name="x_pool", bufs=1))
         stage = ctx.enter_context(tc.tile_pool(name="stage", bufs=1))
-        operands = ctx.enter_context(tc.tile_pool(name="operands", bufs=3))
+        operands = ctx.enter_context(tc.tile_pool(name="operands", bufs=1))
         work = ctx.enter_context(tc.tile_pool(name="work", bufs=2))
         psum = ctx.enter_context(tc.psum_pool(name="psum", bufs=1))
         on_vector = nc.vector.tensor_copy
@@ -71,31 +64,29 @@ def tile_hydraencoderlayer_pa_t_kernel(tc, x, wk, wv, out):
                 in_=w.rearrange("(u q e) c -> q u (e c)", u=HALVES, e=2),
             )
 
-        load_weight("wk", wk)
         rows = x.rearrange("b (q c t) k -> c (b q) (t k)", q=ROWS, t=QUAD)
         x_rows = []
-        for c in range(ROW_TILES // QUAD):
+
+        def load_rows(parts=(slice(0, QUAD * D),)):
+            c = len(x_rows)
             x_rows.append(x_pool.tile([P, QUAD * D], BF16, name="x_rows%d" % c))
-            if c == 0:
-                for part in (slice(0, D), slice(D, PAIR * D), slice(PAIR * D, QUAD * D)):
-                    nc.sync.dma_start(out=x_rows[c][:, part], in_=rows[c][:, part])
-            else:
-                nc.sync.dma_start(out=x_rows[c][:], in_=rows[c])
-            if c == WV_BEHIND:
-                load_weight("wv", wv)
+            for part in parts:
+                nc.sync.dma_start(out=x_rows[c][:, part], in_=rows[c][:, part])
+
+        load_weight("wk", wk)
+        load_rows((slice(0, D), slice(D, PAIR * D), slice(PAIR * D, QUAD * D)))
+        load_rows()
+        load_rows()
+        load_weight("wv", wv)
+        load_rows()
+        load_rows()
 
         pieces = x.rearrange("b (d s t) (u g i) -> b s g (t u) d i", d=ROWS, t=BLOCK, u=HALVES, g=P // QUADRANT)
         x_pieces = x_pool.tile([P, PAIR * ROWS, BATCH, 2 * QUADRANT], BF16, name="x_pieces", align_bytes=64)
-
-        def load_rows(c):
-            x_rows.append(x_pool.tile([P, QUAD * D], BF16, name="x_rows%d" % c))
-            nc.sync.dma_start(out=x_rows[c][:], in_=rows[c])
-
-        load_rows(4)
         filled = 0
-        for part, count in enumerate(PARTS):
-            if part < 3:
-                load_rows(5 + part)
+        for count in PARTS:
+            if len(x_rows) < PAIR * QUAD:
+                load_rows()
             s, d = divmod(filled, ROWS)
             for b in range(BATCH):
                 for g in (0, 2, 1, 3):
@@ -112,24 +103,21 @@ def tile_hydraencoderlayer_pa_t_kernel(tc, x, wk, wv, out):
         out_cols = consts.tile([P, QUADRANT], F32, align_bytes=64)
         nc.vector.memset(out_cols[:], 0.0)
         make_identity(nc, ident[:], nomemset=True)
-        by_batch = consts.tile([P, P], F32)
-        nc.gpsimd.tensor_scalar(
-            out=by_batch[:].rearrange("p (b h t) -> p b h t", b=BATCH, h=PAIR),
-            in0=ident[:].rearrange("p (h b t) -> p b h t", b=BATCH, h=PAIR),
-            scalar1=1.0,
-            scalar2=0.0,
-            op0=ALU.mult,
-            op1=ALU.add,
-        )
-        by_half = consts.tile([P, P], F32)
-        nc.gpsimd.tensor_scalar(
-            out=by_half[:].rearrange("p (h b t) -> p b h t", b=BATCH, h=PAIR),
-            in0=ident[:].rearrange("p (b h t) -> p b h t", b=BATCH, h=PAIR),
-            scalar1=1.0,
-            scalar2=0.0,
-            op0=ALU.mult,
-            op1=ALU.add,
-        )
+
+        def permuted(target, source):
+            matrix = consts.tile([P, P], F32, name="by_" + target[0])
+            nc.gpsimd.tensor_scalar(
+                out=matrix[:].rearrange("p (%s) -> p b h t" % target, b=BATCH, h=PAIR),
+                in0=ident[:].rearrange("p (%s) -> p b h t" % source, b=BATCH, h=PAIR),
+                scalar1=1.0,
+                scalar2=0.0,
+                op0=ALU.mult,
+                op1=ALU.add,
+            )
+            return matrix
+
+        by_batch = permuted("b h t", "h b t")
+        by_half = permuted("h b t", "b h t")
         table_load = consts.tile([P, 1], F32)
         nc.scalar.activation(out=table_load[:], in_=zeros[:, :1], func=ACT.Abs_reciprocal_sqrt, bias=1.0)
 
@@ -148,11 +136,11 @@ def tile_hydraencoderlayer_pa_t_kernel(tc, x, wk, wv, out):
             free.append(held.pop(holder))
 
         stages = [stage.tile([P, SIX * D], BF16, name="stage%d" % i, align_bytes=64) for i in range(PAIR)]
-        row_stage = stage.tile([P, ROW_TILES * D], BF16, name="row_stage", align_bytes=64)
+        row_stage = stage.tile([P, PLAIN_TILES * D], BF16, name="row_stage", align_bytes=64)
 
         def staged(first, count):
             if first < HEAD_TILES:
-                place = first if first < ROW_TILES else first - ROW_TILES + (first - ROW_TILES) // QUAD * QUAD
+                place = first if first < PLAIN_TILES else first - PLAIN_TILES + (first - PLAIN_TILES) // QUAD * QUAD
                 return row_stage[:, place * D : (place + count) * D]
             r, j = divmod(first - HEAD_TILES, SIX)
             return stages[r % PAIR][:, j * D : (j + count) * D]
@@ -199,6 +187,7 @@ def tile_hydraencoderlayer_pa_t_kernel(tc, x, wk, wv, out):
                 x_banks[first] = take_bank(("x", first), [P, PAIR, HALVES, P])
             else:
                 x_banks[first] = psum.tile([P, PAIR, HALVES, P], F32, name=bank)
+            order_of_tokens = ident if first < PLAIN_TILES else by_half
             for j in range(count):
                 t = first + j
                 if t >= HEAD_TILES:
@@ -208,7 +197,7 @@ def tile_hydraencoderlayer_pa_t_kernel(tc, x, wk, wv, out):
                 words = x_rows[c][:].bitcast(F32)
                 for u in range(HALVES):
                     w0 = slot * WORDS + u * P
-                    nc.tensor.transpose(x_banks[first][:, j, u, :], words[:, w0 : w0 + P], (ident if first < ROW_TILES else by_half)[:])
+                    nc.tensor.transpose(x_banks[first][:, j, u, :], words[:, w0 : w0 + P], order_of_tokens[:])
 
         def regroup(first, count=PAIR, copy=on_vector):
             copy(
@@ -219,19 +208,23 @@ def tile_hydraencoderlayer_pa_t_kernel(tc, x, wk, wv, out):
                 release_bank(("x", first))
 
         def turn(r):
+            blocks = slice(PAIR * sum(TURNED[:r]), PAIR * sum(TURNED[: r + 1]))
             nc.vector.transpose(
                 out=stages[r % PAIR][:, : TURNED[r] * D].bitcast(F32),
-                in_=x_pieces[:, PAIR * sum(TURNED[:r]) : PAIR * sum(TURNED[: r + 1])].rearrange("p n b i -> p (n b i)").bitcast(F32),
+                in_=x_pieces[:, blocks].rearrange("p n b i -> p (n b i)").bitcast(F32),
             )
 
         def quantise(first, count):
             run, j = run_of(first)
             if run not in x_codes:
                 width = run[0]
-                x_codes[run] = operands.tile([P, width * P], U32, name="x_codes%d" % width, bufs=PAIR * QUAD + PAIR - width, align_bytes=256)
-                x_scales[run] = operands.tile([P, width * P], U8, name="x_scales%d" % width, bufs=PAIR * QUAD + PAIR - width, align_bytes=256)
+                bufs = HEAD_TILES // QUAD if width == QUAD else QUAD
+                x_codes[run] = operands.tile([P, width * P], U32, name="codes%d" % width, bufs=bufs, align_bytes=256)
+                x_scales[run] = operands.tile([P, width * P], U8, name="scales%d" % width, bufs=bufs, align_bytes=256)
             cols = slice(j * P, (j + count) * P)
-            nc.vector.quantize_mx(out=x_codes[run][:, cols].bitcast(FP8X4), scales=x_scales[run][:, cols], in_=staged(first, count))
+            nc.vector.quantize_mx(
+                out=x_codes[run][:, cols].bitcast(FP8X4), scales=x_scales[run][:, cols], in_=staged(first, count)
+            )
 
         a_ps, v_ps, a_sb, a_pairs = {}, {}, {}, {}
 
@@ -263,12 +256,12 @@ def tile_hydraencoderlayer_pa_t_kernel(tc, x, wk, wv, out):
         def period_tiles(w):
             return list(range(FIRST + SIX * w, FIRST + SIX * (w + 1)))
 
-        windows = range(-1, LAST_WINDOW + 1)
+        windows = range(-1, N_PERIODS)
         on_gpsimd = {t: w for w in windows for t in pair_of(w)}
         groups = [[0, 1, 2], [3, 4, 5]]
-        for w in range(-1, N_RUNS - 1):
-            tiles = [t for t in period_tiles(w)[:4] if t not in on_gpsimd]
-            groups.append(([period_tiles(w - 1)[4]] + pair_of(w - 1) if w > -1 else []) + tiles)
+        for w in windows:
+            tiles = [t for t in period_tiles(w)[:QUAD] if t not in on_gpsimd]
+            groups.append(([period_tiles(w - 1)[QUAD]] + pair_of(w - 1) if w > -1 else []) + tiles)
         done = [t for group in groups for t in group]
         rest = [t for t in range(N_TILES) if t not in done and t not in on_gpsimd]
         late = [t for t in on_gpsimd if t not in done]
@@ -295,9 +288,9 @@ def tile_hydraencoderlayer_pa_t_kernel(tc, x, wk, wv, out):
         def columns(tiles):
             return slice(order.index(tiles[0]), order.index(tiles[-1]) + 1)
 
-        def square_sum(t, from_psum=False):
+        def square_sum(t):
             unread = work.tile([P, DI], BF16, name="squares", bufs=3)
-            source = a_ps[t][:] if from_psum else a_sb[t]
+            source = a_sb[t] if t in a_sb else a_ps[t][:]
             nc.scalar.activation(out=unread[:], in_=source, func=ACT.Square, accum_out=norm2[:, columns([t])])
 
         def fold(target, source):
@@ -305,7 +298,6 @@ def tile_hydraencoderlayer_pa_t_kernel(tc, x, wk, wv, out):
             nc.gpsimd.tensor_tensor(out=target, in0=halves[:, 0], in1=halves[:, 1], op=ALU.add)
 
         def window(w, place):
-            squares = None
             if w - 1 in windows:
                 twice[w - 1] = place.bitcast(F32)[:, : PAIR * DI // 4].rearrange("p (j c) -> p j c", j=PAIR)
                 fold(twice[w - 1], once[w - 1][:])
@@ -371,7 +363,7 @@ def tile_hydraencoderlayer_pa_t_kernel(tc, x, wk, wv, out):
             nc.tensor.matmul(
                 out=sums[half][:, block, :],
                 lhsT=prod[t][:, i * P : (i + 1) * P],
-                rhs=(ident if t < ROW_TILES else by_batch)[:],
+                rhs=(ident if t < PLAIN_TILES else by_batch)[:],
                 is_transpose=True,
                 start=half not in opened,
                 stop=closes,
@@ -384,82 +376,59 @@ def tile_hydraencoderlayer_pa_t_kernel(tc, x, wk, wv, out):
                     add_block(t, i)
             to_sum[:] = to_sum[count:]
 
-        queue = list(order)
+        queue, passes = list(order[QUAD:]), []
 
-        def period(w, count=SIX):
-            tiles, group = period_tiles(w), groups[w + 3]
-            products = queue[:count]
-            queue[:] = queue[count:]
+        def run_ahead():
+            while free and passes:
+                mx, t = passes.pop(0)
+                mx(t)
+
+        def period(w):
+            tiles, group, products = period_tiles(w), groups[w + 3], queue[:SIX]
+            queue[:] = queue[SIX:]
+            x_first = HEAD_TILES + SIX * w
+            x_end = min(x_first + SIX, N_TILES)
+            pairs = range(x_first + TURNED[w], x_end, PAIR)
             scalar_work = [(copy_a, tiles[0]), (copy_a, tiles[1])]
-            if w < 0:
-                scalar_work[1:] = [(clamp_norms, groups[1]), (copy_a, tiles[1]), (invert_norms, groups[1])]
-                scalar_work.append((square_sum, tiles[0]))
             for j in range(PAIR, SIX - 1):
                 scalar_work += [(copy_a, tiles[j]), (square_sum, tiles[j - 1])]
-            passes = []
-            for j in range(SIX):
-                passes += [(pass_a, tiles[j])] + [(pass_v, t) for t in products[j : j + 1]]
-
-            def run_ahead():
-                while free and passes:
-                    mx, t = passes.pop(0)
-                    mx(t)
-
-            if w == 0:
-                passes = [passes[i] for i in (1, 0, 3, 2, 5, 4, 7, 6, 9, 8, 11, 10)]
-            if w < 0:
-                passes[1:5] = [passes[2], passes[1], passes[3], passes[4]]
-                passes[5:5] = [(transpose, ROW_TILES + QUAD), (transpose, ROW_TILES + SIX)]
-                passes[7], passes[8] = passes[8], passes[7]
-                passes[9], passes[10] = passes[10], passes[9]
-            x_first = HEAD_TILES + SIX * w if w >= 0 else ROW_TILES
-            x_end = min(HEAD_TILES + SIX * (w + 1), N_TILES)
-            pairs = list(range(x_first + (TURNED[w] if w >= 0 else QUAD), x_end, PAIR))
             vector_work = [(product, t) for t in products[:-1]]
-            if w < 0:
-                vector_work[1:1] = [(regroup, ROW_TILES + PAIR)]
-                vector_work[3:3] = [(regroup, first) for first in pairs]
+            for j in range(SIX):
+                both = [(pass_a, tiles[j]), (pass_v, products[j])]
+                passes.extend(both if w > 0 else both[::-1])
             run_ahead()
             for step, t in scalar_work:
                 step(t)
                 run_ahead()
-                if t == tiles[0] and step is copy_a:
-                    window(w, staged(HEAD_TILES + SIX * (w - 1) if w > 0 else ROW_TILES + QUAD * w, QUAD))
-                if vector_work and step in (copy_a, square_sum):
+                if t == tiles[0]:
+                    window(w, staged(x_first - SIX if w > 0 else PLAIN_TILES, QUAD))
+                if vector_work:
                     step, t = vector_work.pop(0)
                     step(t)
                     run_ahead()
             for first in pairs:
-                if first not in x_banks:
-                    transpose(first)
-            add_products(RUN_LENGTH - len(pairs) if w >= 0 else PAIR)
-            if w >= 0:
-                turn(w)
+                transpose(first)
+            add_products(RUN_LENGTH - len(pairs))
+            turn(w)
             for first in pairs:
-                if w >= 0:
-                    regroup(first)
-            if w - 1 in windows:
-                sum_folded(w - 1)
+                regroup(first)
+            sum_folded(w - 1)
             if x_end < N_TILES:
                 copy_a(tiles[-1])
                 clamp_norms(group)
                 square_sum(tiles[-PAIR])
-                invert_norms(group)
             else:
                 square_sum(tiles[-PAIR])
                 clamp_norms(group)
                 copy_a(tiles[-1], on_vector)
                 square_sum(tiles[-1])
-                invert_norms(group)
+            invert_norms(group)
             product(products[-1])
             quantise(x_first, QUAD)
             if x_first + QUAD < x_end:
-                quantise(x_first + QUAD, x_end - x_first - QUAD)
+                quantise(x_first + QUAD, PAIR)
 
-        def copy_on_vector(t):
-            copy_a(t, on_vector)
-
-        warm_up(QUAD)
+        warm_up(WARM_UP)
         interleave_wk(slice(0, DI // 2), on_vector)
         interleave_wk(slice(DI // 2, WK_SPLIT), on_vector)
         interleave_wk(slice(WK_SPLIT, DI), on_scalar)
@@ -468,7 +437,7 @@ def tile_hydraencoderlayer_pa_t_kernel(tc, x, wk, wv, out):
         for t in range(QUAD):
             transpose(t, 1)
             if t == 1:
-                warm_up(WARM_UP - QUAD)
+                warm_up(PAIR)
         for t in range(PAIR):
             regroup(t, 1, on_scalar)
             quantise(t, 1)
@@ -479,7 +448,7 @@ def tile_hydraencoderlayer_pa_t_kernel(tc, x, wk, wv, out):
         quantise(2, PAIR)
         transpose(4)
         transpose(6)
-        square_sum(0, True)
+        square_sum(0)
         copy_a(0)
         copy_a(1, on_vector)
         pass_a(2)
@@ -492,6 +461,7 @@ def tile_hydraencoderlayer_pa_t_kernel(tc, x, wk, wv, out):
         transpose(10)
         quantise(4, PAIR)
         quantise(6, PAIR)
+
         interleave_wv(4)
         pass_a(4)
         pass_a(5)
@@ -512,9 +482,9 @@ def tile_hydraencoderlayer_pa_t_kernel(tc, x, wk, wv, out):
         regroup(12)
         copy_a(6)
         regroup(14, copy=on_scalar)
-        warm_up(KEEP_WARM)
         transpose(16, bank="sums1")
         transpose(18, bank="sums0")
+
         quantise(8, PAIR)
         quantise_weight("wv", slice(0, DI))
         quantise(10, PAIR)
@@ -522,85 +492,109 @@ def tile_hydraencoderlayer_pa_t_kernel(tc, x, wk, wv, out):
         regroup(16)
         square_sum(4)
         square_sum(5)
+        pass_a(8)
+        pass_a(9)
+        pass_v(0)
+        pass_v(1)
+        pass_a(10)
+        copy_a(8)
+        clamp_norms(groups[1])
+        window(-1, staged(12, QUAD))
+        product(0)
+        transpose(20)
+        transpose(22)
+        copy_a(9)
+        invert_norms(groups[1])
+        regroup(18)
+        pass_a(11)
+        pass_v(2)
+        square_sum(8)
+        product(1)
+        pass_a(12)
+        copy_a(10)
+        regroup(20)
+        pass_v(3)
+        pass_a(13)
+        square_sum(9)
+        regroup(22)
+        copy_a(11)
+        product(2)
+        add_products(PAIR)
+        square_sum(10)
+        copy_a(12)
+        square_sum(11)
+        copy_a(13)
+        clamp_norms(groups[2])
+        square_sum(12)
+        invert_norms(groups[2])
+        product(3)
+        quantise(16, QUAD)
+        quantise(20, QUAD)
 
-        period(-1, QUAD)
-        for w in range(N_RUNS - 1):
+        for w in range(N_PERIODS):
             period(w)
 
-        first_tile = period_tiles(N_RUNS - 1)[0]
-        by_vector = TAIL_COPIES
+        first_tile = period_tiles(N_PERIODS)[0]
         from_psum = (N_TILES - PAIR, N_TILES - 1)
-        passes = [(pass_v, t) for t in queue]
+        passes.extend((pass_v, t) for t in queue)
         for i, t in enumerate(range(first_tile, N_TILES)):
-            passes.insert(max(PAIR * i, 3 * i - LEAD), (pass_a, t))
-
-        def run_ahead():
-            while free and passes:
-                mx, t = passes.pop(0)
-                mx(t)
-
+            passes.insert(max(3 * i - 1, 0), (pass_a, t))
         scalar_work = []
         for t in range(first_tile, N_TILES):
-            if t not in by_vector and t not in from_psum:
+            if t not in from_psum:
                 scalar_work.append((copy_a, t))
             if t > first_tile:
                 scalar_work.append((square_sum, t - 1))
             if t == first_tile + PAIR:
-                scalar_work.append((sum_folded, LAST_WINDOW))
+                scalar_work.append((sum_folded, windows[-1]))
         scalar_work += [(square_sum, N_TILES - 1)] + [(copy_a, t) for t in from_psum]
-        ready = {}
-        for group in groups[N_RUNS + 2 :]:
+        complete = {}
+        for group in groups[N_PERIODS + 3 :]:
             steps = [(sum_folded, on_gpsimd[t]) if t in on_gpsimd else (square_sum, t) for t in group]
-            ready[max(scalar_work.index(step) if step in scalar_work else -1 for step in steps)] = group
+            complete[max(scalar_work.index(step) if step in scalar_work else -1 for step in steps)] = group
         vector_work = [(product, t) for t in queue]
-        for j, t in enumerate(by_vector):
-            vector_work.insert(TAIL_PLACES[j], (copy_on_vector, t))
 
-        window(N_RUNS - 1, staged(N_TILES - QUAD, QUAD))
+        window(N_PERIODS, staged(N_TILES - QUAD, QUAD))
         run_ahead()
-        added, inverted = [], [t for group in groups[: N_RUNS + 2] for t in group]
-        steps = 0
-        while len(vector_work) > 1 or steps < len(scalar_work) + PAIR:
-            if steps < len(scalar_work):
-                work_s, s = scalar_work[steps]
-                if work_s is square_sum and s in from_psum:
-                    square_sum(s, True)
-                else:
-                    work_s(s)
-            if steps - 2 in ready:
-                invert_norms(ready[steps - 2])
-                inverted += ready[steps - 2]
-            if steps - 1 in ready:
-                clamp_norms(ready[steps - 1])
-            steps += 1
+        added, inverted = [], [t for group in groups[: N_PERIODS + 3] for t in group]
+        for i in range(len(vector_work) + 1):
+            if i < len(scalar_work):
+                step, t = scalar_work[i]
+                step(t)
+            if i - 2 in complete:
+                invert_norms(complete[i - 2])
+                inverted += complete[i - 2]
+            if i - 1 in complete:
+                clamp_norms(complete[i - 1])
             run_ahead()
-            work_v, t = vector_work[0]
-            if len(vector_work) == 1 or (work_v is product and not (t in inverted and t in a_sb)):
+            step, t = vector_work[0]
+            if len(vector_work) == 1 or (step is product and not (t in inverted and t in a_sb)):
                 continue
             vector_work.pop(0)
-            work_v(t)
-            left = len(vector_work)
+            step(t)
+            fresh = [s for s in to_sum if s not in added]
             if t == queue[0]:
                 add_products(PAIR)
-            fresh = [s for s in to_sum if s not in added]
-            if work_v is product and len(fresh) >= PAIR and len(added) < ADDS:
+            elif step is product and len(fresh) >= PAIR and len(added) < ADDS:
                 add_pair(fresh[0], fresh[1])
                 added.append(fresh[0])
                 if len(added) % PAIR == 1 and len(added) > 1:
                     add_products(PAIR)
-            elif work_v is product and len(added) == ADDS and not passes:
-                direct = [s for s in to_sum if s not in added[len(added) - left // PAIR :] or left <= NO_ADD]
-                to_sum[:] = direct + [s for s in to_sum if s not in direct]
-                add_products(len(direct))
+            elif step is product and len(added) == ADDS and not passes:
+                unfinished = added[len(added) - len(vector_work) // PAIR :]
+                to_sum.sort(key=lambda s: s in unfinished)
+                add_products(len([s for s in to_sum if s not in unfinished]))
             run_ahead()
+
         last = N_TILES - 1
         for half in range(PAIR):
             product(last, slice(half * DI // 2, (half + 1) * DI // 2))
         for i in range(E_BLOCKS):
             add_block(last, i, closes=i % PAIR == 1)
+        by_block = out_cols[:, : BATCH * E_BLOCKS].rearrange("e (b i) -> e i b", b=BATCH)
         for half in range(PAIR):
             nc.vector.tensor_reduce(
-                out=out_cols[:, : BATCH * E_BLOCKS].rearrange("e (b i) -> e i b", b=BATCH)[:, PAIR * half : PAIR * (half + 1)],
+                out=by_block[:, PAIR * half : PAIR * (half + 1)],
                 in_=sums[half][:, :PAIR, :].rearrange("e i (b q) -> e i b q", b=BATCH),
                 axis=AXIS.X,
                 op=ALU.add,
@@ -609,5 +603,5 @@ def tile_hydraencoderlayer_pa_t_kernel(tc, x, wk, wv, out):
         nc.vector.transpose(out=out_rows[:], in_=out_cols[:])
         stores = out.rearrange("b o (i g q) -> g (b o i) q", i=E_BLOCKS, q=QUADRANT)
         for g in range(P // QUADRANT):
-            queue_of = nc.sync if g % 2 == 0 else nc.scalar
-            queue_of.dma_start(out=stores[g], in_=out_rows[g * QUADRANT : g * QUADRANT + BATCH * E_BLOCKS, :])
+            engine = nc.sync if g % 2 == 0 else nc.scalar
+            engine.dma_start(out=stores[g], in_=out_rows[g * QUADRANT : g * QUADRANT + BATCH * E_BLOCKS, :])

from contextlib import ExitStack

import concourse.mybir as mybir
from concourse.masks import make_identity

F32 = mybir.dt.float32
BF16 = mybir.dt.bfloat16
U32 = mybir.dt.uint32
U8 = mybir.dt.uint8
FP8X4 = mybir.dt.float8_e4m3fn_x4
ACT = mybir.ActivationFunctionType
ALU = mybir.AluOpType
AXIS = mybir.AxisListType

P = 128
QUADRANT = 32
PACK = 4
BATCH, TOKENS, D, DI = 4, 2048, 512, 512
EPS = 1e-12
WORDS = D // 2
HALVES = WORDS // P
E_BLOCKS = DI // P
PAIR = 2
QUAD = 4
SIX = 6
N_TILES = BATCH * TOKENS // P
BLOCK = QUADRANT // HALVES
ROWS = QUADRANT
PLAIN_TILES = BLOCK
HEAD_TILES = PLAIN_TILES + PAIR * QUAD
TURNED = (4, 4, 4, 4, 6, 6, 4)
PARTS = (8, 12, 12, 12, 12, 8)
N_PERIODS = len(TURNED)
FIRST = PLAIN_TILES - PAIR
RING = 6
RUN_LENGTH = 7
WK_SPLIT = 336
RUN = 4
ADDS = 6
WARM_UP = 4

FLOPS = 2 * 2 * BATCH * TOKENS * D * DI


def tile_hydraencoderlayer_pa_t_kernel(tc, x, wk, wv, out):
    nc = tc.nc
    with ExitStack() as ctx:
        ctx.enter_context(tc.manual_schedule())
        consts = ctx.enter_context(tc.tile_pool(name="consts", bufs=1))
        x_pool = ctx.enter_context(tc.tile_pool(name="x_pool", bufs=1))
        stage = ctx.enter_context(tc.tile_pool(name="stage", bufs=1))
        operands = ctx.enter_context(tc.tile_pool(name="operands", bufs=1))
        work = ctx.enter_context(tc.tile_pool(name="work", bufs=2))
        psum = ctx.enter_context(tc.psum_pool(name="psum", bufs=1))
        on_vector = nc.vector.tensor_copy
        on_scalar = nc.scalar.copy

        w_raw = {}

        def load_weight(label, w):
            w_raw[label] = consts.tile([P, PACK, DI], BF16, name="%s_raw" % label)
            nc.sync.dma_start(
                out=w_raw[label][:].rearrange("q (u e) c -> q u (e c)", u=HALVES),
                in_=w.rearrange("(u q e) c -> q u (e c)", u=HALVES, e=2),
            )

        rows = x.rearrange("b (q c t) k -> c (b q) (t k)", q=ROWS, t=QUAD)
        x_rows = []

        def load_rows(parts=(slice(0, QUAD * D),)):
            c = len(x_rows)
            x_rows.append(x_pool.tile([P, QUAD * D], BF16, name="x_rows%d" % c))
            for part in parts:
                nc.sync.dma_start(out=x_rows[c][:, part], in_=rows[c][:, part])

        load_weight("wk", wk)
        load_rows((slice(0, D), slice(D, PAIR * D), slice(PAIR * D, QUAD * D)))
        load_rows()
        load_rows()
        load_weight("wv", wv)
        load_rows()
        load_rows()

        pieces = x.rearrange("b (d s t) (u g i) -> b s g (t u) d i", d=ROWS, t=BLOCK, u=HALVES, g=P // QUADRANT)
        x_pieces = x_pool.tile([P, PAIR * ROWS, BATCH, 2 * QUADRANT], BF16, name="x_pieces", align_bytes=64)
        filled = 0
        for count in PARTS:
            if len(x_rows) < PAIR * QUAD:
                load_rows()
            s, d = divmod(filled, ROWS)
            for b in range(BATCH):
                for g in (0, 2, 1, 3):
                    nc.sync.dma_start(
                        out=x_pieces[g * QUADRANT : (g + 1) * QUADRANT, filled : filled + count, b, :],
                        in_=pieces[b, PAIR + s, g][:, d : d + count, :],
                    )
            filled += count

        zeros = consts.tile([P, DI], BF16)
        nc.vector.memset(zeros[:], 0.0)
        ident = consts.tile([P, P], F32)
        nc.vector.memset(ident[:], 0.0)
        out_cols = consts.tile([P, QUADRANT], F32, align_bytes=64)
        nc.vector.memset(out_cols[:], 0.0)
        make_identity(nc, ident[:], nomemset=True)

        def permuted(target, source):
            matrix = consts.tile([P, P], F32, name="by_" + target[0])
            nc.gpsimd.tensor_scalar(
                out=matrix[:].rearrange("p (%s) -> p b h t" % target, b=BATCH, h=PAIR),
                in0=ident[:].rearrange("p (%s) -> p b h t" % source, b=BATCH, h=PAIR),
                scalar1=1.0,
                scalar2=0.0,
                op0=ALU.mult,
                op1=ALU.add,
            )
            return matrix

        by_batch = permuted("b h t", "h b t")
        by_half = permuted("h b t", "b h t")
        table_load = consts.tile([P, 1], F32)
        nc.scalar.activation(out=table_load[:], in_=zeros[:, :1], func=ACT.Abs_reciprocal_sqrt, bias=1.0)

        def warm_up(count):
            bank = psum.tile([P, DI], F32, name="sums0")
            for _ in range(count):
                nc.tensor.matmul(out=bank[:], lhsT=zeros[:, :P], rhs=zeros[:], start=True, stop=True)

        held, free = {}, list(range(RING))

        def take_bank(holder, shape):
            held[holder] = free.pop(0)
            return psum.tile(shape, F32, name="bank%d" % held[holder])

        def release_bank(holder):
            free.append(held.pop(holder))

        stages = [stage.tile([P, SIX * D], BF16, name="stage%d" % i, align_bytes=64) for i in range(PAIR)]
        row_stage = stage.tile([P, PLAIN_TILES * D], BF16, name="row_stage", align_bytes=64)

        def staged(first, count):
            if first < HEAD_TILES:
                place = first if first < PLAIN_TILES else first - PLAIN_TILES + (first - PLAIN_TILES) // QUAD * QUAD
                return row_stage[:, place * D : (place + count) * D]
            r, j = divmod(first - HEAD_TILES, SIX)
            return stages[r % PAIR][:, j * D : (j + count) * D]

        w_grouped, w_codes, w_scales = {}, {}, {}
        for label in ("wk", "wv"):
            w_codes[label] = consts.tile([P, DI], U32, name="%s_codes" % label, align_bytes=256)
            w_scales[label] = consts.tile([P, DI], U8, name="%s_scales" % label, align_bytes=256)
        w_grouped["wk"] = consts.tile([P, DI, PACK], BF16, name="wk_grouped", align_bytes=64)[:]

        def interleave_wk(cols, copy):
            by_column = w_raw["wk"][:].rearrange("q t (c i) -> q c t i", i=RUN)
            side_by_side = w_grouped["wk"].rearrange("q (c i) t -> q c t i", i=RUN)
            runs = slice(cols.start // RUN, cols.stop // RUN)
            copy(out=side_by_side[:, runs], in_=by_column[:, runs])

        def interleave_wv(first):
            w_grouped["wv"] = staged(first, QUAD).rearrange("q (c t) -> q c t", t=PACK)
            nc.gpsimd.tensor_scalar(
                out=w_grouped["wv"],
                in0=w_raw["wv"][:].rearrange("q t c -> q c t"),
                scalar1=1.0,
                scalar2=0.0,
                op0=ALU.mult,
                op1=ALU.add,
            )

        def quantise_weight(label, cols):
            nc.vector.quantize_mx(
                out=w_codes[label][:, cols].bitcast(FP8X4),
                scales=w_scales[label][:, cols],
                in_=w_grouped[label][:, cols, :].rearrange("q c t -> q (c t)"),
            )

        x_banks, x_codes, x_scales = {}, {}, {}

        def run_of(t):
            if t < HEAD_TILES:
                return (QUAD, t // QUAD), t % QUAD
            return (SIX, (t - HEAD_TILES) // SIX), (t - HEAD_TILES) % SIX

        def transpose(first, count=PAIR, bank=None):
            if bank is None:
                x_banks[first] = take_bank(("x", first), [P, PAIR, HALVES, P])
            else:
                x_banks[first] = psum.tile([P, PAIR, HALVES, P], F32, name=bank)
            order_of_tokens = ident if first < PLAIN_TILES else by_half
            for j in range(count):
                t = first + j
                if t >= HEAD_TILES:
                    r, place = divmod(t - HEAD_TILES, SIX)
                    t = HEAD_TILES + PAIR * r + place - QUAD
                c, slot = divmod(t, QUAD)
                words = x_rows[c][:].bitcast(F32)
                for u in range(HALVES):
                    w0 = slot * WORDS + u * P
                    nc.tensor.transpose(x_banks[first][:, j, u, :], words[:, w0 : w0 + P], order_of_tokens[:])

        def regroup(first, count=PAIR, copy=on_vector):
            copy(
                out=staged(first, count).bitcast(F32).rearrange("p (j r u) -> p j r u", r=P, u=HALVES),
                in_=x_banks[first][:].rearrange("p j u r -> p j r u")[:, :count, :, :],
            )
            if ("x", first) in held:
                release_bank(("x", first))

        def turn(r):
            blocks = slice(PAIR * sum(TURNED[:r]), PAIR * sum(TURNED[: r + 1]))
            nc.vector.transpose(
                out=stages[r % PAIR][:, : TURNED[r] * D].bitcast(F32),
                in_=x_pieces[:, blocks].rearrange("p n b i -> p (n b i)").bitcast(F32),
            )

        def quantise(first, count):
            run, j = run_of(first)
            if run not in x_codes:
                width = run[0]
                bufs = HEAD_TILES // QUAD if width == QUAD else QUAD
                x_codes[run] = operands.tile([P, width * P], U32, name="codes%d" % width, bufs=bufs, align_bytes=256)
                x_scales[run] = operands.tile([P, width * P], U8, name="scales%d" % width, bufs=bufs, align_bytes=256)
            cols = slice(j * P, (j + count) * P)
            nc.vector.quantize_mx(
                out=x_codes[run][:, cols].bitcast(FP8X4), scales=x_scales[run][:, cols], in_=staged(first, count)
            )

        a_ps, v_ps, a_sb, a_pairs = {}, {}, {}, {}

        def mx_pass(t, label):
            bank = take_bank((label, t), [P, DI])
            run, j = run_of(t)
            cols = slice(j * P, (j + 1) * P)
            nc.tensor.matmul_mx(
                out=bank[:],
                lhsT=x_codes[run][:, cols].bitcast(FP8X4),
                lhsT_scale=x_scales[run][:, cols],
                rhs=w_codes[label][:].bitcast(FP8X4),
                rhs_scale=w_scales[label][:],
                start=True,
                stop=True,
            )
            return bank

        def pass_a(t):
            a_ps[t] = mx_pass(t, "wk")

        def pass_v(t):
            v_ps[t] = mx_pass(t, "wv")

        def pair_of(w):
            first = FIRST - 1 + SIX * w if w >= 0 else FIRST - PAIR + SIX * w
            return [first, first + 1]

        def period_tiles(w):
            return list(range(FIRST + SIX * w, FIRST + SIX * (w + 1)))

        windows = range(-1, N_PERIODS)
        on_gpsimd = {t: w for w in windows for t in pair_of(w)}
        groups = [[0, 1, 2], [3, 4, 5]]
        for w in windows:
            tiles = [t for t in period_tiles(w)[:QUAD] if t not in on_gpsimd]
            groups.append(([period_tiles(w - 1)[QUAD]] + pair_of(w - 1) if w > -1 else []) + tiles)
        done = [t for group in groups for t in group]
        rest = [t for t in range(N_TILES) if t not in done and t not in on_gpsimd]
        late = [t for t in on_gpsimd if t not in done]
        groups += [rest[:PAIR], late + rest[PAIR:QUAD]]
        groups += [rest[i : i + PAIR] for i in range(QUAD, len(rest), PAIR)]
        order = [t for group in groups for t in group]

        def copy_a(t, copy=on_scalar):
            if t in on_gpsimd:
                w = on_gpsimd[t]
                if w not in a_pairs:
                    a_pairs[w] = work.tile([P, PAIR, DI], F32, name="a_pair", bufs=4)
                a_sb[t] = a_pairs[w][:, pair_of(w).index(t), :]
            else:
                a_sb[t] = work.tile([P, DI], F32, name="a_sb", bufs=10)[:]
            copy(out=a_sb[t], in_=a_ps[t][:])
            release_bank(("wk", t))

        norm2 = consts.tile([P, N_TILES], F32, name="norm2")
        clamped = consts.tile([P, N_TILES], F32, name="clamped")
        rnorm = consts.tile([P, N_TILES], F32, name="rnorm")
        once, twice, thrice = {}, {}, {}

        def columns(tiles):
            return slice(order.index(tiles[0]), order.index(tiles[-1]) + 1)

        def square_sum(t):
            unread = work.tile([P, DI], BF16, name="squares", bufs=3)
            source = a_sb[t] if t in a_sb else a_ps[t][:]
            nc.scalar.activation(out=unread[:], in_=source, func=ACT.Square, accum_out=norm2[:, columns([t])])

        def fold(target, source):
            halves = source.rearrange("p j (h c) -> p h j c", h=2)
            nc.gpsimd.tensor_tensor(out=target, in0=halves[:, 0], in1=halves[:, 1], op=ALU.add)

        def window(w, place):
            if w - 1 in windows:
                twice[w - 1] = place.bitcast(F32)[:, : PAIR * DI // 4].rearrange("p (j c) -> p j c", j=PAIR)
                fold(twice[w - 1], once[w - 1][:])
            if w in windows:
                if w - 1 in windows:
                    squares = work.tile([P, PAIR, DI], F32, name="pair_squares")[:]
                else:
                    squares = place.bitcast(F32)[:, : PAIR * DI].rearrange("p (j c) -> p j c", j=PAIR)
                nc.gpsimd.tensor_tensor(out=squares, in0=a_pairs[w][:], in1=a_pairs[w][:], op=ALU.mult)
            if w - 1 in windows:
                thrice[w - 1] = work.tile([P, PAIR, DI // 8], F32, name="thrice")
                fold(thrice[w - 1][:], twice[w - 1])
            if w in windows:
                once[w] = work.tile([P, PAIR, DI // 2], F32, name="once")
                fold(once[w][:], squares)

        def sum_folded(w):
            for j, t in enumerate(pair_of(w)):
                unread = work.tile([P, DI // 8], BF16, name="folded_unread")
                nc.scalar.activation(
                    out=unread[:], in_=thrice[w][:, j, :], func=ACT.Identity, accum_out=norm2[:, columns([t])]
                )

        def clamp_norms(tiles):
            cols = columns(tiles)
            nc.scalar.activation(out=clamped[:, cols], in_=norm2[:, cols], func=ACT.Relu, bias=-EPS * EPS)

        def invert_norms(tiles):
            cols = columns(tiles)
            nc.scalar.activation(
                out=rnorm[:, cols], in_=clamped[:, cols], func=ACT.Abs_reciprocal_sqrt, bias=EPS * EPS
            )

        prod, sums, to_sum = {}, [], []

        def product(t, cols=slice(0, DI)):
            if t not in prod:
                prod[t] = work.tile([P, DI], F32, name="prod", bufs=12)
            nc.vector.scalar_tensor_tensor(
                out=prod[t][:, cols],
                in0=v_ps[t][:, cols],
                scalar=rnorm[:, columns([t])],
                in1=a_sb[t][:, cols],
                op0=ALU.mult,
                op1=ALU.mult,
            )
            if cols.stop == DI:
                release_bank(("wv", t))
                to_sum.append(t)

        def add_pair(t, other):
            total = work.tile([P, DI], F32, name="pair_sum", bufs=ADDS)
            nc.gpsimd.tensor_tensor(out=total[:], in0=prod[t][:], in1=prod[other][:], op=ALU.add)
            prod[t] = total
            to_sum.remove(other)

        opened = set()

        def add_block(t, i, closes=False):
            half, block = divmod(i, PAIR)
            if not sums:
                sums.extend(psum.tile([P, E_BLOCKS, P], F32, name="sums%d" % h) for h in range(PAIR))
            nc.tensor.matmul(
                out=sums[half][:, block, :],
                lhsT=prod[t][:, i * P : (i + 1) * P],
                rhs=(ident if t < PLAIN_TILES else by_batch)[:],
                is_transpose=True,
                start=half not in opened,
                stop=closes,
            )
            opened.add(half)

        def add_products(count):
            for t in to_sum[:count]:
                for i in (0, 2, 1, 3):
                    add_block(t, i)
            to_sum[:] = to_sum[count:]

        queue, passes = list(order[QUAD:]), []

        def run_ahead():
            while free and passes:
                mx, t = passes.pop(0)
                mx(t)

        def period(w):
            tiles, group, products = period_tiles(w), groups[w + 3], queue[:SIX]
            queue[:] = queue[SIX:]
            x_first = HEAD_TILES + SIX * w
            x_end = min(x_first + SIX, N_TILES)
            pairs = range(x_first + TURNED[w], x_end, PAIR)
            scalar_work = [(copy_a, tiles[0]), (copy_a, tiles[1])]
            for j in range(PAIR, SIX - 1):
                scalar_work += [(copy_a, tiles[j]), (square_sum, tiles[j - 1])]
            vector_work = [(product, t) for t in products[:-1]]
            for j in range(SIX):
                both = [(pass_a, tiles[j]), (pass_v, products[j])]
                passes.extend(both if w > 0 else both[::-1])
            run_ahead()
            for step, t in scalar_work:
                step(t)
                run_ahead()
                if t == tiles[0]:
                    window(w, staged(x_first - SIX if w > 0 else PLAIN_TILES, QUAD))
                if vector_work:
                    step, t = vector_work.pop(0)
                    step(t)
                    run_ahead()
            for first in pairs:
                transpose(first)
            add_products(RUN_LENGTH - len(pairs))
            turn(w)
            for first in pairs:
                regroup(first)
            sum_folded(w - 1)
            if x_end < N_TILES:
                copy_a(tiles[-1])
                clamp_norms(group)
                square_sum(tiles[-PAIR])
            else:
                square_sum(tiles[-PAIR])
                clamp_norms(group)
                copy_a(tiles[-1], on_vector)
                square_sum(tiles[-1])
            invert_norms(group)
            product(products[-1])
            quantise(x_first, QUAD)
            if x_first + QUAD < x_end:
                quantise(x_first + QUAD, PAIR)

        warm_up(WARM_UP)
        interleave_wk(slice(0, DI // 2), on_vector)
        interleave_wk(slice(DI // 2, WK_SPLIT), on_vector)
        interleave_wk(slice(WK_SPLIT, DI), on_scalar)
        quantise_weight("wk", slice(0, DI // 2))
        quantise_weight("wk", slice(DI // 2, DI))
        for t in range(QUAD):
            transpose(t, 1)
            if t == 1:
                warm_up(PAIR)
        for t in range(PAIR):
            regroup(t, 1, on_scalar)
            quantise(t, 1)
        regroup(2, 1, on_vector)
        regroup(3, 1, on_scalar)
        pass_a(0)
        pass_a(1)
        quantise(2, PAIR)
        transpose(4)
        transpose(6)
        square_sum(0)
        copy_a(0)
        copy_a(1, on_vector)
        pass_a(2)
        pass_a(3)
        regroup(4)
        square_sum(1)
        regroup(6)
        copy_a(2)
        transpose(8)
        transpose(10)
        quantise(4, PAIR)
        quantise(6, PAIR)

        interleave_wv(4)
        pass_a(4)
        pass_a(5)
        copy_a(3)
        pass_a(6)
        square_sum(2)
        regroup(8)
        pass_a(7)
        copy_a(4)
        clamp_norms(groups[0])
        regroup(10)
        transpose(12)
        transpose(14)
        copy_a(5, on_vector)
        square_sum(3)
        invert_norms(groups[0])
        copy_a(7, on_vector)
        regroup(12)
        copy_a(6)
        regroup(14, copy=on_scalar)
        transpose(16, bank="sums1")
        transpose(18, bank="sums0")

        quantise(8, PAIR)
        quantise_weight("wv", slice(0, DI))
        quantise(10, PAIR)
        quantise(12, QUAD)
        regroup(16)
        square_sum(4)
        square_sum(5)
        pass_a(8)
        pass_a(9)
        pass_v(0)
        pass_v(1)
        pass_a(10)
        copy_a(8)
        clamp_norms(groups[1])
        window(-1, staged(12, QUAD))
        product(0)
        transpose(20)
        transpose(22)
        copy_a(9)
        invert_norms(groups[1])
        regroup(18)
        pass_a(11)
        pass_v(2)
        square_sum(8)
        product(1)
        pass_a(12)
        copy_a(10)
        regroup(20)
        pass_v(3)
        pass_a(13)
        square_sum(9)
        regroup(22)
        copy_a(11)
        product(2)
        add_products(PAIR)
        square_sum(10)
        copy_a(12)
        square_sum(11)
        copy_a(13)
        clamp_norms(groups[2])
        square_sum(12)
        invert_norms(groups[2])
        product(3)
        quantise(16, QUAD)
        quantise(20, QUAD)

        for w in range(N_PERIODS):
            period(w)

        first_tile = period_tiles(N_PERIODS)[0]
        from_psum = (N_TILES - PAIR, N_TILES - 1)
        passes.extend((pass_v, t) for t in queue)
        for i, t in enumerate(range(first_tile, N_TILES)):
            passes.insert(max(3 * i - 1, 0), (pass_a, t))
        scalar_work = []
        for t in range(first_tile, N_TILES):
            if t not in from_psum:
                scalar_work.append((copy_a, t))
            if t > first_tile:
                scalar_work.append((square_sum, t - 1))
            if t == first_tile + PAIR:
                scalar_work.append((sum_folded, windows[-1]))
        scalar_work += [(square_sum, N_TILES - 1)] + [(copy_a, t) for t in from_psum]
        complete = {}
        for group in groups[N_PERIODS + 3 :]:
            steps = [(sum_folded, on_gpsimd[t]) if t in on_gpsimd else (square_sum, t) for t in group]
            complete[max(scalar_work.index(step) if step in scalar_work else -1 for step in steps)] = group
        vector_work = [(product, t) for t in queue]

        window(N_PERIODS, staged(N_TILES - QUAD, QUAD))
        run_ahead()
        added, inverted = [], [t for group in groups[: N_PERIODS + 3] for t in group]
        for i in range(len(vector_work) + 1):
            if i < len(scalar_work):
                step, t = scalar_work[i]
                step(t)
            if i - 2 in complete:
                invert_norms(complete[i - 2])
                inverted += complete[i - 2]
            if i - 1 in complete:
                clamp_norms(complete[i - 1])
            run_ahead()
            step, t = vector_work[0]
            if len(vector_work) == 1 or (step is product and not (t in inverted and t in a_sb)):
                continue
            vector_work.pop(0)
            step(t)
            fresh = [s for s in to_sum if s not in added]
            if t == queue[0]:
                add_products(PAIR)
            elif step is product and len(fresh) >= PAIR and len(added) < ADDS:
                add_pair(fresh[0], fresh[1])
                added.append(fresh[0])
                if len(added) % PAIR == 1 and len(added) > 1:
                    add_products(PAIR)
            elif step is product and len(added) == ADDS and not passes:
                unfinished = added[len(added) - len(vector_work) // PAIR :]
                to_sum.sort(key=lambda s: s in unfinished)
                add_products(len([s for s in to_sum if s not in unfinished]))
            run_ahead()

        last = N_TILES - 1
        for half in range(PAIR):
            product(last, slice(half * DI // 2, (half + 1) * DI // 2))
        for i in range(E_BLOCKS):
            add_block(last, i, closes=i % PAIR == 1)
        by_block = out_cols[:, : BATCH * E_BLOCKS].rearrange("e (b i) -> e i b", b=BATCH)
        for half in range(PAIR):
            nc.vector.tensor_reduce(
                out=by_block[:, PAIR * half : PAIR * (half + 1)],
                in_=sums[half][:, :PAIR, :].rearrange("e i (b q) -> e i b q", b=BATCH),
                axis=AXIS.X,
                op=ALU.add,
            )
        out_rows = consts.tile([P, QUADRANT], F32, align_bytes=64)
        nc.vector.transpose(out=out_rows[:], in_=out_cols[:])
        stores = out.rearrange("b o (i g q) -> g (b o i) q", i=E_BLOCKS, q=QUADRANT)
        for g in range(P // QUADRANT):
            engine = nc.sync if g % 2 == 0 else nc.scalar
            engine.dma_start(out=stores[g], in_=out_rows[g * QUADRANT : g * QUADRANT + BATCH * E_BLOCKS, :])
